import numpy as np
import ml_dtypes


def mxq(x, axis, fmt="e4m3"):
    dtype, down = {"e4m3": (ml_dtypes.float8_e4m3fn, 7), "e5m2": (ml_dtypes.float8_e5m2, 14)}[fmt]
    v = np.moveaxis(np.asarray(x, np.float32).astype(ml_dtypes.bfloat16).astype(np.float64), axis, -1)
    blocks = v.reshape(v.shape[:-1] + (-1, 32))
    amax = np.abs(blocks).max(-1, keepdims=True)
    byte = np.maximum(np.where(amax > 0, np.frexp(amax)[1] - 1 + 127, 0) - down, 1)
    scale = np.exp2(byte - 127.0)
    codes = (blocks / scale).astype(np.float32).astype(dtype).astype(np.float64)
    return np.moveaxis((codes * scale).reshape(v.shape), -1, axis)


WIDE = False


def mx_kscale(k):
    if not WIDE:
        return np.ones(k)
    levels = np.array([10, -10, 5, -5, 0])
    a = np.random.permutation(np.resize(levels, k // 512 * 4)).reshape(k // 512, 4)
    idx = np.arange(k)
    return np.exp2(a[idx // 512, idx % 128 // 32])


BF16 = ml_dtypes.bfloat16


def bf(x):
    return np.asarray(x, np.float32).astype(BF16)


def f64(x):
    return np.asarray(x).astype(np.float64)


N2, D, C, K = 8192, 512, 512, 128
EPSILON = 0.02
TEMPERATURE = 0.1
SINKHORN_ITERS = 3
RHO = 0.8
GAIN = 1.5


def log_softmax(v):
    v = v - v.max(axis=1, keepdims=True)
    return v - np.log(np.exp(v).sum(axis=1, keepdims=True))


def sinkhorn_knopp(z):
    Q = np.exp(z / EPSILON).T
    nk, nb = Q.shape
    Q = Q / Q.sum()
    for _ in range(SINKHORN_ITERS):
        Q = Q / (Q.sum(axis=1, keepdims=True) * nk)
        Q = Q / (Q.sum(axis=0, keepdims=True) * nb)
    Q = Q * nb
    return Q.T


def setup_inputs():
    s = mx_kscale(D)
    base = np.repeat(np.random.standard_normal((N2 // 2, D)), 2, axis=0)
    x = np.sqrt(RHO) * base + np.sqrt(1.0 - RHO) * np.random.standard_normal((N2, D))
    return {"x": bf(x * s),
            "head_w": bf(np.random.standard_normal((C, D)) / np.sqrt(D) / s),
            "head_b": bf(np.random.standard_normal(C) * 0.5),
            "cb_v": bf(np.random.standard_normal((K, C)) / np.sqrt(C)),
            "cb_g": bf(GAIN * (1.0 + 0.1 * np.random.standard_normal(K)))}


def reference(x, head_w, head_b, cb_v, cb_g):
    h = (mxq(f64(x), 1, "e4m3") @ mxq(f64(head_w), 1, "e4m3").T) + f64(head_b)
    h = h / np.maximum(np.sqrt((h * h).sum(axis=1, keepdims=True)), 1e-12)
    v = f64(cb_v)
    w = f64(cb_g)[:, None] * v / np.sqrt((v * v).sum(axis=1, keepdims=True))
    z = mxq(h, 1, "e4m3") @ mxq(w, 1, "e4m3").T
    z1, z2 = z[::2], z[1::2]
    log_p1 = log_softmax(z1 / TEMPERATURE)
    log_p2 = log_softmax(z2 / TEMPERATURE)
    q1 = sinkhorn_knopp(z1)
    q2 = sinkhorn_knopp(z2)
    return -0.5 * ((q1 * log_p2).sum(axis=1) + (q2 * log_p1).sum(axis=1))

@@ -1,0 +1,305 @@
+from contextlib import ExitStack
+
+import concourse.bass as bass
+import concourse.mybir as mybir
+import concourse.tile as tile
+from concourse.masks import make_identity
+
+F32 = mybir.dt.float32
+BF16 = mybir.dt.bfloat16
+U32 = mybir.dt.uint32
+U8 = mybir.dt.uint8
+FP8X4 = mybir.dt.float8_e4m3fn_x4
+ALU = mybir.AluOpType
+ACT = mybir.ActivationFunctionType
+AX = mybir.AxisListType
+
+P = 128
+N2, D, C, K = 8192, 512, 512, 128
+VIEWS = 2
+CHUNKS = 32
+GROUP = 4
+GROUPS = CHUNKS // GROUP
+INV_EPS = 50.0
+INV_T = 10.0
+
+FLOPS = 2 * N2 * D * C + 2 * N2 * C * K
+
+
+def tile_spin_pa_t_kernel(tc, x, head_w, head_b, cb_v, cb_g, out):
+    nc = tc.nc
+    with ExitStack() as ctx:
+        const = ctx.enter_context(tc.tile_pool(name="const", bufs=1))
+        big = ctx.enter_context(tc.tile_pool(name="big", bufs=1))
+        xin = ctx.enter_context(tc.tile_pool(name="xin", bufs=4))
+        stage = ctx.enter_context(tc.tile_pool(name="stage", bufs=2))
+        hbp = ctx.enter_context(tc.tile_pool(name="hbp", bufs=6))
+        small = ctx.enter_context(tc.tile_pool(name="small", bufs=4))
+        pp = ctx.enter_context(tc.tile_pool(name="pp", bufs=3))
+        ps_x = ctx.enter_context(tc.psum_pool(name="ps_x", bufs=1))
+        ps_h = ctx.enter_context(tc.psum_pool(name="ps_h", bufs=2))
+        ps_t = ctx.enter_context(tc.psum_pool(name="ps_t", bufs=2))
+        ps_z = ctx.enter_context(tc.psum_pool(name="ps_z", bufs=1))
+        ps_s = ctx.enter_context(tc.psum_pool(name="ps_s", bufs=2))
+
+        ident_f = const.tile([P, P], F32, name="ident_f")
+        make_identity(nc, ident_f[:])
+        ident_b = const.tile([P, P], BF16, name="ident_b")
+        make_identity(nc, ident_b[:])
+        ones_col = const.tile([P, 1], F32, name="ones_col")
+        nc.vector.memset(ones_col[:], 1.0)
+        neg_half = const.tile([P, GROUP], F32, name="neg_half")
+        nc.vector.memset(neg_half[:], -0.5)
+
+        w_sb = const.tile([P, GROUP * D], BF16, name="w_sb")
+        nc.sync.dma_start(
+            out=w_sb[:].rearrange("p (c k) -> p c k", c=GROUP),
+            in_=head_w.rearrange("(c p) k -> p c k", p=P),
+        )
+        b_bc = const.tile([P, C], BF16, name="b_bc")
+        nc.scalar.dma_start(out=b_bc[:], in_=head_b.partition_broadcast(P))
+        v_sb = const.tile([P, C], BF16, name="v_sb")
+        nc.scalar.dma_start(out=v_sb[:], in_=cb_v)
+        g_sb = const.tile([P, 1], BF16, name="g_sb")
+        with nc.allow_non_contiguous_dma(reason="one gain for each code's partition"):
+            nc.scalar.dma_start(out=g_sb[:], in_=cb_g.rearrange("(p o) -> p o", o=1))
+
+        x_views = x.rearrange("(p m v) d -> v p m d", m=CHUNKS, v=VIEWS)
+
+        def quantise_k_last(src, words, scales):
+            src32 = src[:].bitcast(F32)
+            grouped = stage.tile([P, GROUP * D], BF16, name="grouped", tag="xg", align_bytes=64)
+            g32 = grouped[:].bitcast(F32).rearrange("p (c s u) -> p c s u", c=GROUP, u=2)
+            for half in range(2):
+                xt = ps_x.tile([P, 2, 2, P], F32, name="xt", tag="xt")
+                for cc in range(2):
+                    c = 2 * half + cc
+                    for u in range(2):
+                        lo = 256 * c + 128 * u
+                        nc.tensor.transpose(xt[:, cc, u, :], src32[:, lo:lo + 128], ident_f[:])
+                dst = g32[:, 2 * half:2 * half + 2, :, :]
+                srcv = xt[:].rearrange("p c u s -> p c s u")
+                if half == 0:
+                    nc.vector.tensor_copy(out=dst, in_=srcv)
+                else:
+                    nc.scalar.copy(out=dst, in_=srcv)
+            nc.vector.quantize_mx(out=words.bitcast(FP8X4), scales=scales, in_=grouped[:])
+
+        wq = const.tile([P, C], U32, name="wq", align_bytes=64)
+        ws = const.tile([P, C], U8, name="ws", align_bytes=64)
+        quantise_k_last(w_sb, wq[:], ws[:])
+
+        junk0 = stage.tile([P, C], BF16, name="junk0", tag="junk")
+        vss = const.tile([P, 1], F32, name="vss")
+        nc.scalar.activation(out=junk0[:], in_=v_sb[:], func=ACT.Square, accum_out=vss[:, 0:1])
+        vrn = const.tile([P, 1], F32, name="vrn")
+        nc.gpsimd.tensor_tensor(out=vrn[:], in0=vss[:], in1=neg_half[:, 0:1], op=ALU.pow)
+        wsc = const.tile([P, 1], F32, name="wsc")
+        nc.vector.tensor_tensor(out=wsc[:], in0=vrn[:], in1=g_sb[:], op=ALU.mult)
+        w_bf = const.tile([P, C], BF16, name="w_bf")
+        nc.vector.tensor_scalar(out=w_bf[:], in0=v_sb[:], scalar1=wsc[:, 0:1], scalar2=None, op0=ALU.mult)
+        wt = ps_t.tile([P, 4, P], BF16, name="wt", tag="ht")
+        for t in range(4):
+            nc.tensor.transpose(wt[:, t, :], w_bf[:, 128 * t:128 * t + 128], ident_b[:])
+        wg = const.tile([P, C], BF16, name="wg", align_bytes=64)
+        nc.vector.tensor_copy(
+            out=wg[:].rearrange("p (s t) -> p s t", t=4), in_=wt[:].rearrange("p t s -> p s t")
+        )
+        cq = const.tile([P, K], U32, name="cq", align_bytes=64)
+        cs8 = const.tile([P, K], U8, name="cs8", align_bytes=64)
+        nc.vector.quantize_mx(out=cq[:].bitcast(FP8X4), scales=cs8[:], in_=wg[:])
+
+        zc = [big.tile([P, CHUNKS * P], F32, name="zc%d" % v) for v in range(VIEWS)]
+        ec = [big.tile([P, CHUNKS * P], F32, name="ec%d" % v) for v in range(VIEWS)]
+        es = [big.tile([P, CHUNKS, P], F32, name="es%d" % v) for v in range(VIEWS)]
+        zmax = [const.tile([P, GROUPS], F32, name="zmax%d" % v) for v in range(VIEWS)]
+        csum = [const.tile([P, GROUPS], F32, name="csum%d" % v) for v in range(VIEWS)]
+        gmax = [const.tile([P, 1], F32, name="gmax%d" % v) for v in range(VIEWS)]
+        sump = [const.tile([P, CHUNKS], F32, name="sump%d" % v) for v in range(VIEWS)]
+        code_w = [None, None]
+
+        def stage_one(v, j):
+            x_sb = xin.tile([P, GROUP * D], BF16, name="x_sb", tag="x_sb")
+            nc.sync.dma_start(
+                out=x_sb[:].rearrange("p (m d) -> p m d", m=GROUP),
+                in_=x_views[v][:, GROUP * j:GROUP * j + GROUP, :],
+            )
+            xq = stage.tile([P, GROUP * P], U32, name="xq", tag="xq", align_bytes=64)
+            xs = stage.tile([P, GROUP * P], U8, name="xs", tag="xs", align_bytes=64)
+            quantise_k_last(x_sb, xq[:], xs[:])
+            ss = small.tile([P, GROUP], F32, name="ss", tag="ss")
+            hbs = []
+            for c in range(GROUP):
+                h_ps = ps_h.tile([P, C], F32, name="h_ps", tag="h_ps")
+                nc.tensor.matmul_mx(
+                    out=h_ps[:],
+                    lhsT=xq[:, P * c:P * c + P].bitcast(FP8X4),
+                    lhsT_scale=xs[:, P * c:P * c + P],
+                    rhs=wq[:].bitcast(FP8X4),
+                    rhs_scale=ws[:],
+                    start=True,
+                    stop=True,
+                )
+                hb = hbp.tile([P, C], F32, name="hb", tag="hb")
+                nc.vector.tensor_tensor(out=hb[:], in0=h_ps[:], in1=b_bc[:], op=ALU.add)
+                junk = stage.tile([P, C], BF16, name="junk", tag="junk")
+                nc.scalar.activation(out=junk[:], in_=hb[:], func=ACT.Square, accum_out=ss[:, c:c + 1])
+                hbs.append(hb)
+            ssm = small.tile([P, GROUP], F32, name="ssm", tag="ssm")
+            nc.gpsimd.tensor_scalar_max(out=ssm[:], in0=ss[:], scalar1=1e-24)
+            rn = small.tile([P, GROUP], F32, name="rn", tag="rn")
+            nc.gpsimd.tensor_tensor(out=rn[:], in0=ssm[:], in1=neg_half[:], op=ALU.pow)
+            hn = stage.tile([P, GROUP * C], BF16, name="hn", tag="hn")
+            for c in range(GROUP):
+                nc.gpsimd.tensor_scalar(
+                    out=hn[:, C * c:C * c + C], in0=hbs[c][:], scalar1=rn[:, c:c + 1], scalar2=0.0,
+                    op0=ALU.mult, op1=ALU.add,
+                )
+            hg = stage.tile([P, GROUP * C], BF16, name="hg", tag="hg", align_bytes=64)
+            hgv = hg[:].rearrange("p (c s t) -> p c s t", c=GROUP, t=4)
+            for half in range(2):
+                ht = ps_t.tile([P, 2, 4, P], BF16, name="ht", tag="ht")
+                for cc in range(2):
+                    c = 2 * half + cc
+                    for t in range(4):
+                        lo = C * c + 128 * t
+                        nc.tensor.transpose(ht[:, cc, t, :], hn[:, lo:lo + 128], ident_b[:])
+                nc.scalar.copy(
+                    out=hgv[:, 2 * half:2 * half + 2, :, :], in_=ht[:].rearrange("p c t s -> p c s t")
+                )
+            hq = stage.tile([P, GROUP * P], U32, name="hq", tag="hq", align_bytes=64)
+            hs = stage.tile([P, GROUP * P], U8, name="hs", tag="hs", align_bytes=64)
+            nc.vector.quantize_mx(out=hq[:].bitcast(FP8X4), scales=hs[:], in_=hg[:])
+            z_ps = ps_z.tile([P, GROUP * P], F32, name="z_ps", tag="z_ps")
+            nc.tensor.matmul_mx(
+                out=z_ps[:],
+                lhsT=cq[:].bitcast(FP8X4),
+                lhsT_scale=cs8[:],
+                rhs=hq[:].bitcast(FP8X4),
+                rhs_scale=hs[:],
+                start=True,
+                stop=True,
+            )
+            w0 = GROUP * P * j
+            nc.vector.tensor_scalar(
+                out=zc[v][:, w0:w0 + GROUP * P], in0=z_ps[:], scalar1=1.0, scalar2=None,
+                op0=ALU.mult, op1=ALU.max, accum_out=zmax[v][:, j:j + 1],
+            )
+
+        def over_codes(mat, vec, name):
+            ps = ps_s.tile([P, CHUNKS], F32, name=name, tag="s2")
+            for m in range(CHUNKS):
+                nc.tensor.matmul(
+                    out=ps[:, m:m + 1], lhsT=mat[:, P * m:P * m + P], rhs=vec[:, 0:1], start=True, stop=True
+                )
+            return ps
+
+        def over_samples(v, u, name):
+            ps = ps_s.tile([P, 1], F32, name=name, tag="s2")
+            for m in range(CHUNKS):
+                nc.tensor.matmul(
+                    out=ps[:, 0:1], lhsT=es[v][:, m, :], rhs=u[:, m:m + 1],
+                    start=(m == 0), stop=(m == CHUNKS - 1),
+                )
+            return ps
+
+        def stage_two(v):
+            cmax = small.tile([P, 1], F32, name="cmax", tag="cmax")
+            nc.vector.tensor_reduce(out=cmax[:], in_=zmax[v][:], axis=AX.X, op=ALU.max)
+            nb_e = small.tile([P, 1], F32, name="nb_e", tag="nb_e")
+            nc.vector.tensor_scalar(out=nb_e[:], in0=cmax[:], scalar1=-INV_EPS, scalar2=None, op0=ALU.mult)
+            for j in range(GROUPS):
+                w0 = GROUP * P * j
+                nc.scalar.activation(
+                    out=ec[v][:, w0:w0 + GROUP * P], in_=zc[v][:, w0:w0 + GROUP * P], func=ACT.Exp,
+                    bias=nb_e[:, 0:1], scale=INV_EPS, accum_out=csum[v][:, j:j + 1],
+                )
+            mrep = small.tile([P, P], F32, name="mrep", tag="mrep")
+            nc.vector.tensor_copy(out=mrep[:], in_=cmax[:, 0:1].to_broadcast([P, P]))
+            mt = ps_s.tile([P, P], F32, name="mt", tag="s2")
+            nc.tensor.transpose(mt[:], mrep[:], ident_f[:])
+            nc.vector.tensor_reduce(out=gmax[v][:], in_=mt[:], axis=AX.X, op=ALU.max)
+            nb_t = small.tile([P, 1], F32, name="nb_t", tag="nb_t")
+            nc.vector.tensor_scalar(out=nb_t[:], in0=gmax[v][:], scalar1=-INV_T, scalar2=None, op0=ALU.mult)
+            for j in range(GROUPS):
+                et = ps_s.tile([P, GROUP, P], F32, name="et", tag="s2")
+                for q in range(GROUP):
+                    m = GROUP * j + q
+                    nc.tensor.transpose(et[:, q, :], ec[v][:, P * m:P * m + P], ident_f[:])
+                if j % 2 == 0:
+                    nc.vector.tensor_copy(out=es[v][:, GROUP * j:GROUP * j + GROUP, :], in_=et[:])
+                else:
+                    nc.scalar.copy(out=es[v][:, GROUP * j:GROUP * j + GROUP, :], in_=et[:])
+            ctot = small.tile([P, 1], F32, name="ctot", tag="ctot")
+            nc.vector.tensor_reduce(out=ctot[:], in_=csum[v][:], axis=AX.X, op=ALU.add)
+            cvec = small.tile([P, 1], F32, name="cvec", tag="cvec")
+            nc.vector.reciprocal(out=cvec[:], in_=ctot[:])
+            for it in range(2):
+                r_ps = over_codes(ec[v], cvec, "r_ps")
+                u = small.tile([P, CHUNKS], F32, name="u", tag="u")
+                nc.vector.reciprocal(out=u[:], in_=r_ps[:])
+                c_ps = over_samples(v, u, "c_ps")
+                cvec = small.tile([P, 1], F32, name="cvec", tag="cvec")
+                nc.vector.reciprocal(out=cvec[:], in_=c_ps[:])
+            code_w[v] = const.tile([P, 1], F32, name="code_w%d" % v)
+            nc.vector.tensor_copy(out=code_w[v][:], in_=cvec[:])
+            sp_ps = ps_s.tile([P, CHUNKS], F32, name="sp_ps", tag="s2")
+            for j in range(GROUPS):
+                w0 = GROUP * P * j
+                pt = pp.tile([P, GROUP * P], F32, name="pt", tag="pt")
+                nc.scalar.activation(
+                    out=pt[:], in_=zc[v][:, w0:w0 + GROUP * P], func=ACT.Exp, bias=nb_t[:, 0:1], scale=INV_T
+                )
+                for q in range(GROUP):
+                    m = GROUP * j + q
+                    nc.tensor.matmul(
+                        out=sp_ps[:, m:m + 1], lhsT=pt[:, P * q:P * q + P], rhs=ones_col[:, 0:1],
+                        start=True, stop=True,
+                    )
+            nc.vector.tensor_copy(out=sump[v][:], in_=sp_ps[:])
+
+        for v in range(VIEWS):
+            for j in range(GROUPS):
+                stage_one(v, j)
+            stage_two(v)
+
+        tq = []
+        lnp = []
+        for v in range(VIEWS):
+            o = 1 - v
+            for j in range(GROUPS):
+                w0 = GROUP * P * j
+                eng = nc.vector if v == 0 else nc.gpsimd
+                eng.tensor_tensor(
+                    out=zc[o][:, w0:w0 + GROUP * P], in0=ec[v][:, w0:w0 + GROUP * P],
+                    in1=zc[o][:, w0:w0 + GROUP * P], op=ALU.mult,
+                )
+        for v in range(VIEWS):
+            o = 1 - v
+            r_ps = over_codes(ec[v], code_w[v], "r3_ps")
+            rec = small.tile([P, CHUNKS], F32, name="rec", tag="rec")
+            nc.vector.reciprocal(out=rec[:], in_=r_ps[:])
+            f_ps = over_codes(zc[o], code_w[v], "f_ps")
+            t = const.tile([P, CHUNKS], F32, name="tq%d" % v)
+            nc.vector.tensor_tensor(out=t[:], in0=f_ps[:], in1=rec[:], op=ALU.mult)
+            tq.append(t)
+            ln = const.tile([P, CHUNKS], F32, name="lnp%d" % v)
+            nc.scalar.activation(out=ln[:], in_=sump[v][:], func=ACT.Ln)
+            lnp.append(ln)
+        tsum = const.tile([P, CHUNKS], F32, name="tsum")
+        nc.vector.tensor_tensor(out=tsum[:], in0=tq[0][:], in1=tq[1][:], op=ALU.add)
+        lsum = const.tile([P, CHUNKS], F32, name="lsum")
+        nc.vector.tensor_tensor(out=lsum[:], in0=lnp[0][:], in1=lnp[1][:], op=ALU.add)
+        msum = const.tile([P, 1], F32, name="msum")
+        nc.vector.tensor_tensor(out=msum[:], in0=gmax[0][:], in1=gmax[1][:], op=ALU.add)
+        msc = const.tile([P, 1], F32, name="msc")
+        nc.vector.tensor_scalar(out=msc[:], in0=msum[:], scalar1=0.5 * INV_T, scalar2=None, op0=ALU.mult)
+        part = const.tile([P, CHUNKS], F32, name="part")
+        nc.vector.tensor_scalar(
+            out=part[:], in0=tsum[:], scalar1=-0.5 * INV_T, scalar2=msc[:, 0:1], op0=ALU.mult, op1=ALU.add
+        )
+        res = const.tile([P, CHUNKS], F32, name="res")
+        nc.vector.scalar_tensor_tensor(
+            out=res[:], in0=lsum[:], scalar=0.5, in1=part[:], op0=ALU.mult, op1=ALU.add
+        )
+        nc.sync.dma_start(out=out.rearrange("(p m) -> p m", m=CHUNKS), in_=res[:])

@@ -1,8 +1,6 @@
 from contextlib import ExitStack
 
-import concourse.bass as bass
 import concourse.mybir as mybir
-import concourse.tile as tile
 from concourse.masks import make_identity
 
 F32 = mybir.dt.float32
@@ -20,6 +18,9 @@ VIEWS = 2
 CHUNKS = 32
 GROUP = 4
 GROUPS = CHUNKS // GROUP
+NG = VIEWS * GROUPS
+W = GROUP * P
+NX = 4
 INV_EPS = 50.0
 INV_T = 10.0
 
@@ -29,263 +30,434 @@ FLOPS = 2 * N2 * D * C + 2 * N2 * C * K
 def tile_spin_pa_t_kernel(tc, x, head_w, head_b, cb_v, cb_g, out):
     nc = tc.nc
     with ExitStack() as ctx:
+        ctx.enter_context(tc.manual_schedule())
         const = ctx.enter_context(tc.tile_pool(name="const", bufs=1))
         big = ctx.enter_context(tc.tile_pool(name="big", bufs=1))
-        xin = ctx.enter_context(tc.tile_pool(name="xin", bufs=4))
-        stage = ctx.enter_context(tc.tile_pool(name="stage", bufs=2))
-        hbp = ctx.enter_context(tc.tile_pool(name="hbp", bufs=6))
         small = ctx.enter_context(tc.tile_pool(name="small", bufs=4))
-        pp = ctx.enter_context(tc.tile_pool(name="pp", bufs=3))
-        ps_x = ctx.enter_context(tc.psum_pool(name="ps_x", bufs=1))
-        ps_h = ctx.enter_context(tc.psum_pool(name="ps_h", bufs=2))
-        ps_t = ctx.enter_context(tc.psum_pool(name="ps_t", bufs=2))
-        ps_z = ctx.enter_context(tc.psum_pool(name="ps_z", bufs=1))
         ps_s = ctx.enter_context(tc.psum_pool(name="ps_s", bufs=2))
-
-        ident_f = const.tile([P, P], F32, name="ident_f")
-        make_identity(nc, ident_f[:])
-        ident_b = const.tile([P, P], BF16, name="ident_b")
-        make_identity(nc, ident_b[:])
-        ones_col = const.tile([P, 1], F32, name="ones_col")
-        nc.vector.memset(ones_col[:], 1.0)
-        neg_half = const.tile([P, GROUP], F32, name="neg_half")
-        nc.vector.memset(neg_half[:], -0.5)
-
-        w_sb = const.tile([P, GROUP * D], BF16, name="w_sb")
-        nc.sync.dma_start(
-            out=w_sb[:].rearrange("p (c k) -> p c k", c=GROUP),
-            in_=head_w.rearrange("(c p) k -> p c k", p=P),
-        )
-        b_bc = const.tile([P, C], BF16, name="b_bc")
-        nc.scalar.dma_start(out=b_bc[:], in_=head_b.partition_broadcast(P))
-        v_sb = const.tile([P, C], BF16, name="v_sb")
-        nc.scalar.dma_start(out=v_sb[:], in_=cb_v)
-        g_sb = const.tile([P, 1], BF16, name="g_sb")
-        with nc.allow_non_contiguous_dma(reason="one gain for each code's partition"):
-            nc.scalar.dma_start(out=g_sb[:], in_=cb_g.rearrange("(p o) -> p o", o=1))
-
-        x_views = x.rearrange("(p m v) d -> v p m d", m=CHUNKS, v=VIEWS)
-
-        def quantise_k_last(src, words, scales):
-            src32 = src[:].bitcast(F32)
-            grouped = stage.tile([P, GROUP * D], BF16, name="grouped", tag="xg", align_bytes=64)
-            g32 = grouped[:].bitcast(F32).rearrange("p (c s u) -> p c s u", c=GROUP, u=2)
-            for half in range(2):
-                xt = ps_x.tile([P, 2, 2, P], F32, name="xt", tag="xt")
-                for cc in range(2):
-                    c = 2 * half + cc
-                    for u in range(2):
-                        lo = 256 * c + 128 * u
-                        nc.tensor.transpose(xt[:, cc, u, :], src32[:, lo:lo + 128], ident_f[:])
-                dst = g32[:, 2 * half:2 * half + 2, :, :]
-                srcv = xt[:].rearrange("p c u s -> p c s u")
-                if half == 0:
-                    nc.vector.tensor_copy(out=dst, in_=srcv)
-                else:
-                    nc.scalar.copy(out=dst, in_=srcv)
-            nc.vector.quantize_mx(out=words.bitcast(FP8X4), scales=scales, in_=grouped[:])
-
-        wq = const.tile([P, C], U32, name="wq", align_bytes=64)
-        ws = const.tile([P, C], U8, name="ws", align_bytes=64)
-        quantise_k_last(w_sb, wq[:], ws[:])
-
-        junk0 = stage.tile([P, C], BF16, name="junk0", tag="junk")
-        vss = const.tile([P, 1], F32, name="vss")
-        nc.scalar.activation(out=junk0[:], in_=v_sb[:], func=ACT.Square, accum_out=vss[:, 0:1])
-        vrn = const.tile([P, 1], F32, name="vrn")
-        nc.gpsimd.tensor_tensor(out=vrn[:], in0=vss[:], in1=neg_half[:, 0:1], op=ALU.pow)
-        wsc = const.tile([P, 1], F32, name="wsc")
-        nc.vector.tensor_tensor(out=wsc[:], in0=vrn[:], in1=g_sb[:], op=ALU.mult)
-        w_bf = const.tile([P, C], BF16, name="w_bf")
-        nc.vector.tensor_scalar(out=w_bf[:], in0=v_sb[:], scalar1=wsc[:, 0:1], scalar2=None, op0=ALU.mult)
-        wt = ps_t.tile([P, 4, P], BF16, name="wt", tag="ht")
-        for t in range(4):
-            nc.tensor.transpose(wt[:, t, :], w_bf[:, 128 * t:128 * t + 128], ident_b[:])
-        wg = const.tile([P, C], BF16, name="wg", align_bytes=64)
-        nc.vector.tensor_copy(
-            out=wg[:].rearrange("p (s t) -> p s t", t=4), in_=wt[:].rearrange("p t s -> p s t")
-        )
-        cq = const.tile([P, K], U32, name="cq", align_bytes=64)
-        cs8 = const.tile([P, K], U8, name="cs8", align_bytes=64)
-        nc.vector.quantize_mx(out=cq[:].bitcast(FP8X4), scales=cs8[:], in_=wg[:])
 
         zc = [big.tile([P, CHUNKS * P], F32, name="zc%d" % v) for v in range(VIEWS)]
         ec = [big.tile([P, CHUNKS * P], F32, name="ec%d" % v) for v in range(VIEWS)]
-        es = [big.tile([P, CHUNKS, P], F32, name="es%d" % v) for v in range(VIEWS)]
+        ech = [big.tile([P, CHUNKS * P], BF16, name="ech%d" % v) for v in range(VIEWS)]
+        ecl = [big.tile([P, CHUNKS * P], BF16, name="ecl%d" % v) for v in range(VIEWS)]
+        es = [big.tile([P, CHUNKS, 2, P], BF16, name="es%d" % v) for v in range(VIEWS)]
         zmax = [const.tile([P, GROUPS], F32, name="zmax%d" % v) for v in range(VIEWS)]
         csum = [const.tile([P, GROUPS], F32, name="csum%d" % v) for v in range(VIEWS)]
+        cmax = [const.tile([P, 1], F32, name="cmax%d" % v) for v in range(VIEWS)]
+        nb_e = [const.tile([P, 1], F32, name="nb_e%d" % v) for v in range(VIEWS)]
+        nb_t = [const.tile([P, 1], F32, name="nb_t%d" % v) for v in range(VIEWS)]
         gmax = [const.tile([P, 1], F32, name="gmax%d" % v) for v in range(VIEWS)]
+        mrep = [const.tile([P, P], F32, name="mrep%d" % v) for v in range(VIEWS)]
         sump = [const.tile([P, CHUNKS], F32, name="sump%d" % v) for v in range(VIEWS)]
-        code_w = [None, None]
+        lnp = [const.tile([P, CHUNKS], F32, name="lnp%d" % v) for v in range(VIEWS)]
+        tq = [const.tile([P, CHUNKS], F32, name="tq%d" % v) for v in range(VIEWS)]
+        live = {}
 
-        def stage_one(v, j):
-            x_sb = xin.tile([P, GROUP * D], BF16, name="x_sb", tag="x_sb")
-            nc.sync.dma_start(
-                out=x_sb[:].rearrange("p (m d) -> p m d", m=GROUP),
-                in_=x_views[v][:, GROUP * j:GROUP * j + GROUP, :],
-            )
-            xq = stage.tile([P, GROUP * P], U32, name="xq", tag="xq", align_bytes=64)
-            xs = stage.tile([P, GROUP * P], U8, name="xs", tag="xs", align_bytes=64)
-            quantise_k_last(x_sb, xq[:], xs[:])
-            ss = small.tile([P, GROUP], F32, name="ss", tag="ss")
-            hbs = []
-            for c in range(GROUP):
-                h_ps = ps_h.tile([P, C], F32, name="h_ps", tag="h_ps")
-                nc.tensor.matmul_mx(
-                    out=h_ps[:],
-                    lhsT=xq[:, P * c:P * c + P].bitcast(FP8X4),
-                    lhsT_scale=xs[:, P * c:P * c + P],
-                    rhs=wq[:].bitcast(FP8X4),
-                    rhs_scale=ws[:],
-                    start=True,
-                    stop=True,
-                )
-                hb = hbp.tile([P, C], F32, name="hb", tag="hb")
-                nc.vector.tensor_tensor(out=hb[:], in0=h_ps[:], in1=b_bc[:], op=ALU.add)
-                junk = stage.tile([P, C], BF16, name="junk", tag="junk")
-                nc.scalar.activation(out=junk[:], in_=hb[:], func=ACT.Square, accum_out=ss[:, c:c + 1])
-                hbs.append(hb)
-            ssm = small.tile([P, GROUP], F32, name="ssm", tag="ssm")
-            nc.gpsimd.tensor_scalar_max(out=ssm[:], in0=ss[:], scalar1=1e-24)
-            rn = small.tile([P, GROUP], F32, name="rn", tag="rn")
-            nc.gpsimd.tensor_tensor(out=rn[:], in0=ssm[:], in1=neg_half[:], op=ALU.pow)
-            hn = stage.tile([P, GROUP * C], BF16, name="hn", tag="hn")
-            for c in range(GROUP):
-                nc.gpsimd.tensor_scalar(
-                    out=hn[:, C * c:C * c + C], in0=hbs[c][:], scalar1=rn[:, c:c + 1], scalar2=0.0,
-                    op0=ALU.mult, op1=ALU.add,
-                )
-            hg = stage.tile([P, GROUP * C], BF16, name="hg", tag="hg", align_bytes=64)
-            hgv = hg[:].rearrange("p (c s t) -> p c s t", c=GROUP, t=4)
-            for half in range(2):
-                ht = ps_t.tile([P, 2, 4, P], BF16, name="ht", tag="ht")
-                for cc in range(2):
-                    c = 2 * half + cc
-                    for t in range(4):
-                        lo = C * c + 128 * t
-                        nc.tensor.transpose(ht[:, cc, t, :], hn[:, lo:lo + 128], ident_b[:])
-                nc.scalar.copy(
-                    out=hgv[:, 2 * half:2 * half + 2, :, :], in_=ht[:].rearrange("p c t s -> p c s t")
-                )
-            hq = stage.tile([P, GROUP * P], U32, name="hq", tag="hq", align_bytes=64)
-            hs = stage.tile([P, GROUP * P], U8, name="hs", tag="hs", align_bytes=64)
-            nc.vector.quantize_mx(out=hq[:].bitcast(FP8X4), scales=hs[:], in_=hg[:])
-            z_ps = ps_z.tile([P, GROUP * P], F32, name="z_ps", tag="z_ps")
-            nc.tensor.matmul_mx(
-                out=z_ps[:],
-                lhsT=cq[:].bitcast(FP8X4),
-                lhsT_scale=cs8[:],
-                rhs=hq[:].bitcast(FP8X4),
-                rhs_scale=hs[:],
-                start=True,
-                stop=True,
-            )
-            w0 = GROUP * P * j
-            nc.vector.tensor_scalar(
-                out=zc[v][:, w0:w0 + GROUP * P], in0=z_ps[:], scalar1=1.0, scalar2=None,
-                op0=ALU.mult, op1=ALU.max, accum_out=zmax[v][:, j:j + 1],
-            )
+        def bank(j):
+            return slice(W * j, W * j + W)
 
-        def over_codes(mat, vec, name):
-            ps = ps_s.tile([P, CHUNKS], F32, name=name, tag="s2")
-            for m in range(CHUNKS):
-                nc.tensor.matmul(
-                    out=ps[:, m:m + 1], lhsT=mat[:, P * m:P * m + P], rhs=vec[:, 0:1], start=True, stop=True
-                )
-            return ps
+        def shift(v):
+            nc.vector.tensor_reduce(out=cmax[v][:], in_=zmax[v][:], axis=AX.X, op=ALU.max)
+            nc.vector.tensor_scalar(out=nb_e[v][:], in0=cmax[v][:], scalar1=-INV_EPS, scalar2=None, op0=ALU.mult)
 
-        def over_samples(v, u, name):
-            ps = ps_s.tile([P, 1], F32, name=name, tag="s2")
-            for m in range(CHUNKS):
-                nc.tensor.matmul(
-                    out=ps[:, 0:1], lhsT=es[v][:, m, :], rhs=u[:, m:m + 1],
-                    start=(m == 0), stop=(m == CHUNKS - 1),
-                )
-            return ps
+        def e_exp(v, j):
+            nc.scalar.activation(out=ec[v][:, bank(j)], in_=zc[v][:, bank(j)], func=ACT.Exp,
+                                 bias=nb_e[v][:, 0:1], scale=INV_EPS, accum_out=csum[v][:, j:j + 1])
 
-        def stage_two(v):
-            cmax = small.tile([P, 1], F32, name="cmax", tag="cmax")
-            nc.vector.tensor_reduce(out=cmax[:], in_=zmax[v][:], axis=AX.X, op=ALU.max)
-            nb_e = small.tile([P, 1], F32, name="nb_e", tag="nb_e")
-            nc.vector.tensor_scalar(out=nb_e[:], in0=cmax[:], scalar1=-INV_EPS, scalar2=None, op0=ALU.mult)
-            for j in range(GROUPS):
-                w0 = GROUP * P * j
-                nc.scalar.activation(
-                    out=ec[v][:, w0:w0 + GROUP * P], in_=zc[v][:, w0:w0 + GROUP * P], func=ACT.Exp,
-                    bias=nb_e[:, 0:1], scale=INV_EPS, accum_out=csum[v][:, j:j + 1],
-                )
-            mrep = small.tile([P, P], F32, name="mrep", tag="mrep")
-            nc.vector.tensor_copy(out=mrep[:], in_=cmax[:, 0:1].to_broadcast([P, P]))
-            mt = ps_s.tile([P, P], F32, name="mt", tag="s2")
-            nc.tensor.transpose(mt[:], mrep[:], ident_f[:])
-            nc.vector.tensor_reduce(out=gmax[v][:], in_=mt[:], axis=AX.X, op=ALU.max)
-            nb_t = small.tile([P, 1], F32, name="nb_t", tag="nb_t")
-            nc.vector.tensor_scalar(out=nb_t[:], in0=gmax[v][:], scalar1=-INV_T, scalar2=None, op0=ALU.mult)
-            for j in range(GROUPS):
-                et = ps_s.tile([P, GROUP, P], F32, name="et", tag="s2")
-                for q in range(GROUP):
-                    m = GROUP * j + q
-                    nc.tensor.transpose(et[:, q, :], ec[v][:, P * m:P * m + P], ident_f[:])
-                if j % 2 == 0:
-                    nc.vector.tensor_copy(out=es[v][:, GROUP * j:GROUP * j + GROUP, :], in_=et[:])
-                else:
-                    nc.scalar.copy(out=es[v][:, GROUP * j:GROUP * j + GROUP, :], in_=et[:])
-            ctot = small.tile([P, 1], F32, name="ctot", tag="ctot")
+        def e_hi(v, j):
+            nc.vector.tensor_copy(out=ech[v][:, bank(j)], in_=ec[v][:, bank(j)])
+
+        def e_lo(v, j, eng):
+            eng.tensor_tensor(out=ecl[v][:, bank(j)], in0=ec[v][:, bank(j)], in1=ech[v][:, bank(j)],
+                              op=ALU.subtract)
+
+        def e_tp(v, j, pool, tag):
+            et = pool.tile([P, GROUP, 2, P], BF16, name="et", tag=tag)
+            for q in range(GROUP):
+                m = GROUP * j + q
+                nc.tensor.transpose(et[:, q, 0, :], ech[v][:, P * m:P * m + P], ident_b[:])
+                nc.tensor.transpose(et[:, q, 1, :], ecl[v][:, P * m:P * m + P], ident_b[:])
+            live[("et", v, j)] = et
+
+        def e_cp(v, j, on_scalar):
+            dst = es[v][:, GROUP * j:GROUP * j + GROUP, :, :]
+            if on_scalar:
+                nc.scalar.copy(out=dst, in_=live[("et", v, j)][:])
+            else:
+                nc.vector.tensor_copy(out=dst, in_=live[("et", v, j)][:])
+
+        def e_pipe(v, pool, tag, lo_on_gpsimd, cp_on_scalar):
+            n = GROUPS
+            for k in range(n + 3):
+                if k < n:
+                    e_exp(v, k)
+                if 0 <= k - 1 < n:
+                    e_hi(v, k - 1)
+                    e_lo(v, k - 1, nc.gpsimd if lo_on_gpsimd(k - 1) else nc.vector)
+                if 0 <= k - 2 < n:
+                    e_tp(v, k - 2, pool, tag)
+                if 0 <= k - 3 < n:
+                    e_cp(v, k - 3, cp_on_scalar(k - 3))
+
+        def split_vec(src, cols, name):
+            two = small.tile([P, cols, 2], BF16, name=name, tag=name)
+            nc.vector.tensor_copy(out=two[:, :, 0], in_=src)
+            nc.vector.tensor_tensor(out=two[:, :, 1], in0=src, in1=two[:, :, 0], op=ALU.subtract)
+            return two
+
+        def c_first(v):
+            ctot = small.tile([P, 1], F32, name="ctot", tag="cr")
             nc.vector.tensor_reduce(out=ctot[:], in_=csum[v][:], axis=AX.X, op=ALU.add)
             cvec = small.tile([P, 1], F32, name="cvec", tag="cvec")
             nc.vector.reciprocal(out=cvec[:], in_=ctot[:])
-            for it in range(2):
-                r_ps = over_codes(ec[v], cvec, "r_ps")
-                u = small.tile([P, CHUNKS], F32, name="u", tag="u")
-                nc.vector.reciprocal(out=u[:], in_=r_ps[:])
-                c_ps = over_samples(v, u, "c_ps")
-                cvec = small.tile([P, 1], F32, name="cvec", tag="cvec")
-                nc.vector.reciprocal(out=cvec[:], in_=c_ps[:])
-            code_w[v] = const.tile([P, 1], F32, name="code_w%d" % v)
-            nc.vector.tensor_copy(out=code_w[v][:], in_=cvec[:])
-            sp_ps = ps_s.tile([P, CHUNKS], F32, name="sp_ps", tag="s2")
-            for j in range(GROUPS):
-                w0 = GROUP * P * j
-                pt = pp.tile([P, GROUP * P], F32, name="pt", tag="pt")
-                nc.scalar.activation(
-                    out=pt[:], in_=zc[v][:, w0:w0 + GROUP * P], func=ACT.Exp, bias=nb_t[:, 0:1], scale=INV_T
-                )
-                for q in range(GROUP):
-                    m = GROUP * j + q
-                    nc.tensor.matmul(
-                        out=sp_ps[:, m:m + 1], lhsT=pt[:, P * q:P * q + P], rhs=ones_col[:, 0:1],
-                        start=True, stop=True,
-                    )
-            nc.vector.tensor_copy(out=sump[v][:], in_=sp_ps[:])
+            live[("c2", v)] = split_vec(cvec[:], 1, "c2_%d" % v)
+
+        def pair_matmuls(ps, hi, lo, vec2):
+            for m in range(CHUNKS):
+                nc.tensor.matmul(out=ps[:, m, :], lhsT=hi(m), rhs=vec2[:, 0, :], start=True, stop=False)
+                nc.tensor.matmul(out=ps[:, m, :], lhsT=lo(m), rhs=vec2[:, 0, :], start=False, stop=True)
+
+        def u_pe(v, pool, tag):
+            ps = pool.tile([P, CHUNKS, 2], F32, name="u_ps", tag=tag)
+            pair_matmuls(ps, lambda m: ech[v][:, P * m:P * m + P], lambda m: ecl[v][:, P * m:P * m + P],
+                         live[("c2", v)])
+            live[("u_ps", v)] = ps
+
+        def u_ve(v, split):
+            r = small.tile([P, CHUNKS], F32, name="r", tag="r")
+            nc.vector.tensor_reduce(out=r[:], in_=live[("u_ps", v)][:], axis=AX.X, op=ALU.add)
+            u = small.tile([P, CHUNKS], F32, name="u", tag="u%d" % v)
+            nc.vector.reciprocal(out=u[:], in_=r[:])
+            live[("u", v)] = u
+            if split:
+                live[("u2", v)] = split_vec(u[:], CHUNKS, "u2_%d" % v)
+
+        def c_pe(v, pool, tag):
+            ps = pool.tile([P, 2], F32, name="c_ps", tag=tag)
+            u2 = live[("u2", v)]
+            for m in range(CHUNKS):
+                for h in range(2):
+                    nc.tensor.matmul(out=ps[:, 0:2], lhsT=es[v][:, m, h, :], rhs=u2[:, m, :],
+                                     start=(m == 0 and h == 0), stop=(m == CHUNKS - 1 and h == 1))
+            live[("c_ps", v)] = ps
+
+        def c_ve(v):
+            r = small.tile([P, 1], F32, name="cr", tag="cr")
+            nc.vector.tensor_reduce(out=r[:], in_=live[("c_ps", v)][:], axis=AX.X, op=ALU.add)
+            cvec = small.tile([P, 1], F32, name="cvec", tag="cvec")
+            nc.vector.reciprocal(out=cvec[:], in_=r[:])
+            live[("c2", v)] = split_vec(cvec[:], 1, "c2_%d" % v)
+
+        with ExitStack() as early:
+            xin = early.enter_context(tc.tile_pool(name="xin", bufs=NX))
+            stage = early.enter_context(tc.tile_pool(name="stage", bufs=2))
+            hbp = early.enter_context(tc.tile_pool(name="hbp", bufs=2 * GROUP))
+            ps_x = early.enter_context(tc.psum_pool(name="ps_x", bufs=1))
+            ps_h = early.enter_context(tc.psum_pool(name="ps_h", bufs=2))
+            ps_t = early.enter_context(tc.psum_pool(name="ps_t", bufs=2))
+            ps_z = early.enter_context(tc.psum_pool(name="ps_z", bufs=1))
+
+            x_views = x.rearrange("(p m v) d -> v p m d", m=CHUNKS, v=VIEWS)
+
+            def ok(g):
+                return 0 <= g < NG
+
+            def load(g):
+                if not ok(g):
+                    return
+                x_sb = xin.tile([P, GROUP * D], BF16, name="x_sb", tag="x_sb")
+                j = g % GROUPS
+                nc.sync.dma_start(out=x_sb[:].rearrange("p (m d) -> p m d", m=GROUP),
+                                  in_=x_views[g // GROUPS][:, GROUP * j:GROUP * j + GROUP, :])
+                live[("x", g)] = x_sb
+
+            def k_to_partitions(src, grouped, half, on_scalar):
+                src32 = src[:].bitcast(F32)
+                g32 = grouped[:].bitcast(F32).rearrange("p (c s u) -> p c s u", c=GROUP, u=2)
+                xt = ps_x.tile([P, 2, 2, P], F32, name="xt", tag="xt")
+                for cc in range(2):
+                    for u in range(2):
+                        lo = 256 * (2 * half + cc) + 128 * u
+                        nc.tensor.transpose(xt[:, cc, u, :], src32[:, lo:lo + 128], ident_f[:])
+                dst = g32[:, 2 * half:2 * half + 2, :, :]
+                srcv = xt[:].rearrange("p c u s -> p c s u")
+                if on_scalar:
+                    nc.scalar.copy(out=dst, in_=srcv)
+                else:
+                    nc.vector.tensor_copy(out=dst, in_=srcv)
+
+            def x_tp(g, half, on_scalar):
+                if not ok(g):
+                    return
+                if half == 0:
+                    live[("xg", g)] = stage.tile([P, GROUP * D], BF16, name="xg", tag="xg", align_bytes=64)
+                k_to_partitions(live[("x", g)], live[("xg", g)], half, on_scalar)
+
+            def x_q(g):
+                if not ok(g):
+                    return
+                xq = stage.tile([P, W], U32, name="xq", tag="xq", align_bytes=64)
+                xs = stage.tile([P, W], U8, name="xs", tag="xs", align_bytes=64)
+                nc.vector.quantize_mx(out=xq[:].bitcast(FP8X4), scales=xs[:], in_=live[("xg", g)][:])
+                live[("xq", g)] = (xq, xs)
+
+            def head(g):
+                if not ok(g):
+                    return
+                xq, xs = live[("xq", g)]
+                ss = small.tile([P, GROUP], F32, name="ss", tag="ss")
+                hbs = []
+                for c in range(GROUP):
+                    h_ps = ps_h.tile([P, C], F32, name="h_ps", tag="h_ps")
+                    nc.tensor.matmul_mx(out=h_ps[:], lhsT=xq[:, P * c:P * c + P].bitcast(FP8X4),
+                                        lhsT_scale=xs[:, P * c:P * c + P], rhs=wq[:].bitcast(FP8X4),
+                                        rhs_scale=ws[:], start=True, stop=True)
+                    hb = hbp.tile([P, C], F32, name="hb", tag="hb")
+                    nc.vector.tensor_tensor(out=hb[:], in0=h_ps[:], in1=b_bc[:], op=ALU.add)
+                    junk = stage.tile([P, C], BF16, name="junk", tag="junk")
+                    nc.scalar.activation(out=junk[:], in_=hb[:], func=ACT.Square, accum_out=ss[:, c:c + 1])
+                    hbs.append(hb)
+                live[("hb", g)] = (hbs, ss)
+
+            def normalise(g):
+                if not ok(g):
+                    return
+                hbs, ss = live[("hb", g)]
+                ssm = small.tile([P, GROUP], F32, name="ssm", tag="ssm")
+                nc.gpsimd.tensor_scalar_max(out=ssm[:], in0=ss[:], scalar1=1e-24)
+                rn = small.tile([P, GROUP], F32, name="rn", tag="rn")
+                nc.gpsimd.tensor_tensor(out=rn[:], in0=ssm[:], in1=neg_half[:], op=ALU.pow)
+                hn = stage.tile([P, GROUP * C], BF16, name="hn", tag="hn")
+                for c in range(GROUP):
+                    nc.gpsimd.tensor_scalar(out=hn[:, C * c:C * c + C], in0=hbs[c][:], scalar1=rn[:, c:c + 1],
+                                            scalar2=0.0, op0=ALU.mult, op1=ALU.add)
+                live[("hn", g)] = hn
+
+            def h_tp(g, half):
+                if not ok(g):
+                    return
+                if half == 0:
+                    live[("hg", g)] = stage.tile([P, GROUP * C], BF16, name="hg", tag="hg", align_bytes=64)
+                hn = live[("hn", g)]
+                hgv = live[("hg", g)][:].rearrange("p (c s t) -> p c s t", c=GROUP, t=4)
+                ht = ps_t.tile([P, 2, 4, P], BF16, name="ht", tag="ht")
+                for cc in range(2):
+                    for t in range(4):
+                        lo = C * (2 * half + cc) + 128 * t
+                        nc.tensor.transpose(ht[:, cc, t, :], hn[:, lo:lo + 128], ident_b[:])
+                nc.scalar.copy(out=hgv[:, 2 * half:2 * half + 2, :, :], in_=ht[:].rearrange("p c t s -> p c s t"))
+
+            def h_q(g):
+                if not ok(g):
+                    return
+                hq = stage.tile([P, W], U32, name="hq", tag="hq", align_bytes=64)
+                hs = stage.tile([P, W], U8, name="hs", tag="hs", align_bytes=64)
+                nc.vector.quantize_mx(out=hq[:].bitcast(FP8X4), scales=hs[:], in_=live[("hg", g)][:])
+                live[("hq", g)] = (hq, hs)
+
+            def logits(g):
+                if not ok(g):
+                    return
+                hq, hs = live[("hq", g)]
+                v = g // GROUPS
+                j = g % GROUPS
+                z_ps = ps_z.tile([P, W], F32, name="z_ps", tag="z_ps")
+                nc.tensor.matmul_mx(out=z_ps[:], lhsT=cq[:].bitcast(FP8X4), lhsT_scale=cs8[:],
+                                    rhs=hq[:].bitcast(FP8X4), rhs_scale=hs[:], start=True, stop=True)
+                nc.vector.tensor_scalar(out=zc[v][:, bank(j)], in0=z_ps[:], scalar1=1.0, scalar2=None,
+                                        op0=ALU.mult, op1=ALU.max, accum_out=zmax[v][:, j:j + 1])
+
+            w_sb = const.tile([P, GROUP * D], BF16, name="w_sb")
+            nc.sync.dma_start(out=w_sb[:].rearrange("p (c k) -> p c k", c=GROUP),
+                              in_=head_w.rearrange("(c p) k -> p c k", p=P))
+            for g in range(NX):
+                load(g)
+            b_bc = const.tile([P, C], BF16, name="b_bc")
+            nc.scalar.dma_start(out=b_bc[:], in_=head_b.partition_broadcast(P))
+            v_sb = const.tile([P, C], BF16, name="v_sb")
+            nc.scalar.dma_start(out=v_sb[:], in_=cb_v)
+            g_sb = const.tile([P, 1], BF16, name="g_sb")
+            with nc.allow_non_contiguous_dma(reason="one gain for each code's partition"):
+                nc.scalar.dma_start(out=g_sb[:], in_=cb_g.rearrange("(p o) -> p o", o=1))
+            ident_f = const.tile([P, P], F32, name="ident_f")
+            make_identity(nc, ident_f[:])
+            ident_b = const.tile([P, P], BF16, name="ident_b")
+            make_identity(nc, ident_b[:])
+            neg_half = const.tile([P, GROUP], F32, name="neg_half")
+            nc.vector.memset(neg_half[:], -0.5)
+
+            wgr = const.tile([P, GROUP * D], BF16, name="wgr", align_bytes=64)
+            k_to_partitions(w_sb, wgr, 0, False)
+            k_to_partitions(w_sb, wgr, 1, True)
+            x_tp(0, 0, False)
+            x_tp(0, 1, True)
+            wq = const.tile([P, C], U32, name="wq", align_bytes=64)
+            ws = const.tile([P, C], U8, name="ws", align_bytes=64)
+            nc.vector.quantize_mx(out=wq[:].bitcast(FP8X4), scales=ws[:], in_=wgr[:])
+            x_q(0)
+            x_tp(1, 0, False)
+            x_tp(1, 1, True)
+
+            junk0 = stage.tile([P, C], BF16, name="junk0", tag="junk")
+            vss = const.tile([P, 1], F32, name="vss")
+            nc.scalar.activation(out=junk0[:], in_=v_sb[:], func=ACT.Square, accum_out=vss[:, 0:1])
+            vrn = const.tile([P, 1], F32, name="vrn")
+            nc.gpsimd.tensor_tensor(out=vrn[:], in0=vss[:], in1=neg_half[:, 0:1], op=ALU.pow)
+            w_bf = const.tile([P, C], BF16, name="w_bf")
+            wg = const.tile([P, C], BF16, name="wg", align_bytes=64)
+
+            def codebook_a():
+                wsc = const.tile([P, 1], F32, name="wsc")
+                nc.vector.tensor_tensor(out=wsc[:], in0=vrn[:], in1=g_sb[:], op=ALU.mult)
+                nc.vector.tensor_scalar(out=w_bf[:], in0=v_sb[:], scalar1=wsc[:, 0:1], scalar2=None, op0=ALU.mult)
+                wt = ps_s.tile([P, 4, P], BF16, name="wt", tag="s2")
+                for t in range(4):
+                    nc.tensor.transpose(wt[:, t, :], w_bf[:, 128 * t:128 * t + 128], ident_b[:])
+                live["wt"] = wt
+
+            def codebook_b():
+                nc.vector.tensor_copy(out=wg[:].rearrange("p (s t) -> p s t", t=4),
+                                      in_=live["wt"][:].rearrange("p t s -> p s t"))
+
+            def codebook_c():
+                nc.vector.quantize_mx(out=cq[:].bitcast(FP8X4), scales=cs8[:], in_=wg[:])
+
+            cq = const.tile([P, K], U32, name="cq", align_bytes=64)
+            cs8 = const.tile([P, K], U8, name="cs8", align_bytes=64)
+
+            for i in range(NG + 3):
+                logits(i - 3)
+                head(i)
+                normalise(i)
+                load(i + NX)
+                x_tp(i + 2, 0, False)
+                h_tp(i - 1, 0)
+                x_tp(i + 2, 1, i % 2 == 1)
+                h_tp(i - 1, 1)
+                h_q(i - 2)
+                x_q(i + 1)
+                if i == 0:
+                    codebook_a()
+                if i == 1:
+                    codebook_b()
+                if i == 2:
+                    codebook_c()
+                if i == GROUPS + 2:
+                    shift(0)
+            e_pipe(0, ps_s, "s2", lambda k: k % 2 == 1, lambda k: True)
+            c_first(0)
+
+        late = ctx.enter_context(tc.tile_pool(name="late", bufs=1))
+        pp = ctx.enter_context(tc.tile_pool(name="pp", bufs=3))
+        ps_e = ctx.enter_context(tc.psum_pool(name="ps_e", bufs=2))
+        ps_v = ctx.enter_context(tc.psum_pool(name="ps_v", bufs=2))
+        ps_p = ctx.enter_context(tc.psum_pool(name="ps_p", bufs=2))
+        gh = [late.tile([P, CHUNKS * P], BF16, name="gh%d" % v) for v in range(VIEWS)]
+        gl = [late.tile([P, CHUNKS * P], BF16, name="gl%d" % v) for v in range(VIEWS)]
+
+        def g_max_a(v):
+            nc.vector.tensor_copy(out=mrep[v][:], in_=cmax[v][:, 0:1].to_broadcast([P, P]))
+            mt = ps_p.tile([P, P], F32, name="mt", tag="tp")
+            nc.tensor.transpose(mt[:], mrep[v][:], ident_f[:])
+            nc.vector.tensor_reduce(out=gmax[v][:], in_=mt[:], axis=AX.X, op=ALU.max)
+            nc.vector.tensor_scalar(out=nb_t[v][:], in0=gmax[v][:], scalar1=-INV_T, scalar2=None, op0=ALU.mult)
+
+        def p_exp(v, j):
+            pt = pp.tile([P, W], F32, name="pt", tag="pt")
+            nc.scalar.activation(out=pt[:], in_=zc[v][:, bank(j)], func=ACT.Exp, bias=nb_t[v][:, 0:1], scale=INV_T)
+            live[("pt", v, j)] = pt
+
+        def p_tp(v, j):
+            tp = ps_p.tile([P, GROUP, P], F32, name="tp", tag="tp")
+            pt = live[("pt", v, j)]
+            for q in range(GROUP):
+                nc.tensor.transpose(tp[:, q, :], pt[:, P * q:P * q + P], ident_f[:])
+            live[("tp", v, j)] = tp
+
+        def p_sum(v, j):
+            nc.vector.tensor_reduce(out=sump[v][:, GROUP * j:GROUP * j + GROUP], in_=live[("tp", v, j)][:],
+                                    axis=AX.X, op=ALU.add)
+
+        def g_mul(v, j):
+            nc.vector.tensor_tensor(out=ec[v][:, bank(j)], in0=ec[v][:, bank(j)], in1=zc[1 - v][:, bank(j)],
+                                    op=ALU.mult)
+
+        def g_hi(v, j):
+            nc.scalar.copy(out=gh[v][:, bank(j)], in_=ec[v][:, bank(j)])
+
+        def g_lo(v, j, eng):
+            eng.tensor_tensor(out=gl[v][:, bank(j)], in0=ec[v][:, bank(j)], in1=gh[v][:, bank(j)], op=ALU.subtract)
+
+        banks = [(v, j) for v in range(VIEWS) for j in range(GROUPS)]
+        nb = len(banks)
+        side = []
+
+        def p_step(k):
+            if k < nb:
+                p_exp(*banks[k])
+            if 0 <= k - 1 < nb:
+                p_tp(*banks[k - 1])
+            if 0 <= k - 2 < nb:
+                p_sum(*banks[k - 2])
+
+        def g_step(k):
+            if k < nb:
+                g_mul(*banks[k])
+            if 0 <= k - 1 < nb:
+                g_hi(*banks[k - 1])
+            if 0 <= k - 2 < nb:
+                g_lo(banks[k - 2][0], banks[k - 2][1], nc.vector if (k - 2) % 3 == 0 else nc.gpsimd)
+
+        for k in range(nb + 2):
+            side.append((p_step, k))
+        for k in range(nb + 2):
+            side.append((g_step, k))
+        done = [0]
+
+        def side_work(n):
+            for q in range(n):
+                if done[0] < len(side):
+                    f, k = side[done[0]]
+                    f(k)
+                    done[0] = done[0] + 1
+
+        shift(1)
+        e_pipe(1, ps_e, "et", lambda k: k % 2 == 1, lambda k: k % 2 == 1)
+        c_first(1)
+        for v in range(VIEWS):
+            g_max_a(v)
+        STEP = 4
+        for it in range(2):
+            u_pe(0, ps_v, "vec")
+            side_work(STEP)
+            u_pe(1, ps_v, "vec")
+            u_ve(0, True)
+            side_work(STEP)
+            c_pe(0, ps_v, "vec")
+            u_ve(1, True)
+            side_work(STEP)
+            c_pe(1, ps_v, "vec")
+            c_ve(0)
+            side_work(STEP)
+            c_ve(1)
+        u_pe(0, ps_v, "vec")
+        side_work(STEP)
+        u_pe(1, ps_v, "vec")
+        u_ve(0, False)
+        side_work(len(side))
+        u_ve(1, False)
 
         for v in range(VIEWS):
-            for j in range(GROUPS):
-                stage_one(v, j)
-            stage_two(v)
-
-        tq = []
-        lnp = []
+            f_ps = ps_e.tile([P, CHUNKS, 2], F32, name="f_ps", tag="et")
+            pair_matmuls(f_ps, lambda m: gh[v][:, P * m:P * m + P], lambda m: gl[v][:, P * m:P * m + P],
+                         live[("c2", v)])
+            live[("f_ps", v)] = f_ps
         for v in range(VIEWS):
-            o = 1 - v
-            for j in range(GROUPS):
-                w0 = GROUP * P * j
-                eng = nc.vector if v == 0 else nc.gpsimd
-                eng.tensor_tensor(
-                    out=zc[o][:, w0:w0 + GROUP * P], in0=ec[v][:, w0:w0 + GROUP * P],
-                    in1=zc[o][:, w0:w0 + GROUP * P], op=ALU.mult,
-                )
+            nc.scalar.activation(out=lnp[v][:], in_=sump[v][:], func=ACT.Ln)
         for v in range(VIEWS):
-            o = 1 - v
-            r_ps = over_codes(ec[v], code_w[v], "r3_ps")
-            rec = small.tile([P, CHUNKS], F32, name="rec", tag="rec")
-            nc.vector.reciprocal(out=rec[:], in_=r_ps[:])
-            f_ps = over_codes(zc[o], code_w[v], "f_ps")
-            t = const.tile([P, CHUNKS], F32, name="tq%d" % v)
-            nc.vector.tensor_tensor(out=t[:], in0=f_ps[:], in1=rec[:], op=ALU.mult)
-            tq.append(t)
-            ln = const.tile([P, CHUNKS], F32, name="lnp%d" % v)
-            nc.scalar.activation(out=ln[:], in_=sump[v][:], func=ACT.Ln)
-            lnp.append(ln)
+            fsum = small.tile([P, CHUNKS], F32, name="fsum", tag="r")
+            nc.vector.tensor_reduce(out=fsum[:], in_=live[("f_ps", v)][:], axis=AX.X, op=ALU.add)
+            nc.vector.tensor_tensor(out=tq[v][:], in0=fsum[:], in1=live[("u", v)][:], op=ALU.mult)
         tsum = const.tile([P, CHUNKS], F32, name="tsum")
         nc.vector.tensor_tensor(out=tsum[:], in0=tq[0][:], in1=tq[1][:], op=ALU.add)
         lsum = const.tile([P, CHUNKS], F32, name="lsum")
@@ -295,11 +467,8 @@ def tile_spin_pa_t_kernel(tc, x, head_w, head_b, cb_v, cb_g, out):
         msc = const.tile([P, 1], F32, name="msc")
         nc.vector.tensor_scalar(out=msc[:], in0=msum[:], scalar1=0.5 * INV_T, scalar2=None, op0=ALU.mult)
         part = const.tile([P, CHUNKS], F32, name="part")
-        nc.vector.tensor_scalar(
-            out=part[:], in0=tsum[:], scalar1=-0.5 * INV_T, scalar2=msc[:, 0:1], op0=ALU.mult, op1=ALU.add
-        )
+        nc.vector.tensor_scalar(out=part[:], in0=tsum[:], scalar1=-0.5 * INV_T, scalar2=msc[:, 0:1],
+                                op0=ALU.mult, op1=ALU.add)
         res = const.tile([P, CHUNKS], F32, name="res")
-        nc.vector.scalar_tensor_tensor(
-            out=res[:], in0=lsum[:], scalar=0.5, in1=part[:], op0=ALU.mult, op1=ALU.add
-        )
+        nc.vector.scalar_tensor_tensor(out=res[:], in0=lsum[:], scalar=0.5, in1=part[:], op0=ALU.mult, op1=ALU.add)
         nc.sync.dma_start(out=out.rearrange("(p m) -> p m", m=CHUNKS), in_=res[:])

@@ -21,6 +21,7 @@ GROUPS = CHUNKS // GROUP
 NG = VIEWS * GROUPS
 W = GROUP * P
 NX = 4
+REP = 8
 INV_EPS = 50.0
 INV_T = 10.0
 
@@ -34,7 +35,10 @@ def tile_spin_pa_t_kernel(tc, x, head_w, head_b, cb_v, cb_g, out):
         const = ctx.enter_context(tc.tile_pool(name="const", bufs=1))
         big = ctx.enter_context(tc.tile_pool(name="big", bufs=1))
         small = ctx.enter_context(tc.tile_pool(name="small", bufs=4))
-        ps_s = ctx.enter_context(tc.psum_pool(name="ps_s", bufs=2))
+        ps_x = ctx.enter_context(tc.psum_pool(name="ps_x", bufs=2))
+        ps_h = ctx.enter_context(tc.psum_pool(name="ps_h", bufs=3))
+        ps_t = ctx.enter_context(tc.psum_pool(name="ps_t", bufs=2))
+        ps_z = ctx.enter_context(tc.psum_pool(name="ps_z", bufs=1))
 
         zc = [big.tile([P, CHUNKS * P], F32, name="zc%d" % v) for v in range(VIEWS)]
         ec = [big.tile([P, CHUNKS * P], F32, name="ec%d" % v) for v in range(VIEWS)]
@@ -71,8 +75,8 @@ def tile_spin_pa_t_kernel(tc, x, head_w, head_b, cb_v, cb_g, out):
             eng.tensor_tensor(out=ecl[v][:, bank(j)], in0=ec[v][:, bank(j)], in1=ech[v][:, bank(j)],
                               op=ALU.subtract)
 
-        def e_tp(v, j, pool, tag):
-            et = pool.tile([P, GROUP, 2, P], BF16, name="et", tag=tag)
+        def e_tp(v, j):
+            et = ps_h.tile([P, GROUP, 2, P], BF16, name="et", tag="h_ps")
             for q in range(GROUP):
                 m = GROUP * j + q
                 nc.tensor.transpose(et[:, q, 0, :], ech[v][:, P * m:P * m + P], ident_b[:])
@@ -86,18 +90,28 @@ def tile_spin_pa_t_kernel(tc, x, head_w, head_b, cb_v, cb_g, out):
             else:
                 nc.vector.tensor_copy(out=dst, in_=live[("et", v, j)][:])
 
-        def e_pipe(v, pool, tag, lo_on_gpsimd, cp_on_scalar):
-            n = GROUPS
-            for k in range(n + 3):
-                if k < n:
-                    e_exp(v, k)
-                if 0 <= k - 1 < n:
-                    e_hi(v, k - 1)
-                    e_lo(v, k - 1, nc.gpsimd if lo_on_gpsimd(k - 1) else nc.vector)
-                if 0 <= k - 2 < n:
-                    e_tp(v, k - 2, pool, tag)
-                if 0 <= k - 3 < n:
-                    e_cp(v, k - 3, cp_on_scalar(k - 3))
+        banks = [(v, j) for v in range(VIEWS) for j in range(GROUPS)]
+        nb = len(banks)
+        e_done = [0]
+
+        def e_step(k):
+            if k < nb:
+                e_exp(*banks[k])
+            if 0 <= k - 2 < nb:
+                e_hi(*banks[k - 2])
+                e_lo(banks[k - 2][0], banks[k - 2][1], nc.gpsimd if (k - 2) % 2 == 1 else nc.vector)
+            if 0 <= k - 4 < nb:
+                e_tp(*banks[k - 4])
+            if 0 <= k - 6 < nb:
+                e_cp(banks[k - 6][0], banks[k - 6][1], True)
+                if (k - 6) % GROUPS == GROUPS - 1:
+                    c_first(banks[k - 6][0])
+
+        def e_steps(n, limit):
+            for q in range(n):
+                if e_done[0] < min(limit, nb + 6):
+                    e_step(e_done[0])
+                    e_done[0] = e_done[0] + 1
 
         def split_vec(src, cols, name):
             two = small.tile([P, cols, 2], BF16, name=name, tag=name)
@@ -112,38 +126,41 @@ def tile_spin_pa_t_kernel(tc, x, head_w, head_b, cb_v, cb_g, out):
             nc.vector.reciprocal(out=cvec[:], in_=ctot[:])
             live[("c2", v)] = split_vec(cvec[:], 1, "c2_%d" % v)
 
+        def wide(two):
+            return two.to_broadcast([P, REP, 2]) if REP > 1 else two
+
         def pair_matmuls(ps, hi, lo, vec2):
             for m in range(CHUNKS):
-                nc.tensor.matmul(out=ps[:, m, :], lhsT=hi(m), rhs=vec2[:, 0, :], start=True, stop=False)
-                nc.tensor.matmul(out=ps[:, m, :], lhsT=lo(m), rhs=vec2[:, 0, :], start=False, stop=True)
+                nc.tensor.matmul(out=ps[:, m, :, :], lhsT=hi(m), rhs=wide(vec2[:, 0:1, :]), start=True, stop=False)
+                nc.tensor.matmul(out=ps[:, m, :, :], lhsT=lo(m), rhs=wide(vec2[:, 0:1, :]), start=False, stop=True)
 
-        def u_pe(v, pool, tag):
-            ps = pool.tile([P, CHUNKS, 2], F32, name="u_ps", tag=tag)
+        def u_pe(v):
+            ps = ps_t.tile([P, CHUNKS, REP, 2], F32, name="u_ps", tag="ht")
             pair_matmuls(ps, lambda m: ech[v][:, P * m:P * m + P], lambda m: ecl[v][:, P * m:P * m + P],
                          live[("c2", v)])
             live[("u_ps", v)] = ps
 
         def u_ve(v, split):
             r = small.tile([P, CHUNKS], F32, name="r", tag="r")
-            nc.vector.tensor_reduce(out=r[:], in_=live[("u_ps", v)][:], axis=AX.X, op=ALU.add)
+            nc.vector.tensor_reduce(out=r[:], in_=live[("u_ps", v)][:, :, 0, :], axis=AX.X, op=ALU.add)
             u = small.tile([P, CHUNKS], F32, name="u", tag="u%d" % v)
             nc.vector.reciprocal(out=u[:], in_=r[:])
             live[("u", v)] = u
             if split:
                 live[("u2", v)] = split_vec(u[:], CHUNKS, "u2_%d" % v)
 
-        def c_pe(v, pool, tag):
-            ps = pool.tile([P, 2], F32, name="c_ps", tag=tag)
+        def c_pe(v):
+            ps = ps_t.tile([P, REP, 2], F32, name="c_ps", tag="ht")
             u2 = live[("u2", v)]
             for m in range(CHUNKS):
                 for h in range(2):
-                    nc.tensor.matmul(out=ps[:, 0:2], lhsT=es[v][:, m, h, :], rhs=u2[:, m, :],
+                    nc.tensor.matmul(out=ps[:], lhsT=es[v][:, m, h, :], rhs=wide(u2[:, m:m + 1, :]),
                                      start=(m == 0 and h == 0), stop=(m == CHUNKS - 1 and h == 1))
             live[("c_ps", v)] = ps
 
         def c_ve(v):
             r = small.tile([P, 1], F32, name="cr", tag="cr")
-            nc.vector.tensor_reduce(out=r[:], in_=live[("c_ps", v)][:], axis=AX.X, op=ALU.add)
+            nc.vector.tensor_reduce(out=r[:], in_=live[("c_ps", v)][:, 0, :], axis=AX.X, op=ALU.add)
             cvec = small.tile([P, 1], F32, name="cvec", tag="cvec")
             nc.vector.reciprocal(out=cvec[:], in_=r[:])
             live[("c2", v)] = split_vec(cvec[:], 1, "c2_%d" % v)
@@ -152,10 +169,6 @@ def tile_spin_pa_t_kernel(tc, x, head_w, head_b, cb_v, cb_g, out):
             xin = early.enter_context(tc.tile_pool(name="xin", bufs=NX))
             stage = early.enter_context(tc.tile_pool(name="stage", bufs=2))
             hbp = early.enter_context(tc.tile_pool(name="hbp", bufs=2 * GROUP))
-            ps_x = early.enter_context(tc.psum_pool(name="ps_x", bufs=1))
-            ps_h = early.enter_context(tc.psum_pool(name="ps_h", bufs=2))
-            ps_t = early.enter_context(tc.psum_pool(name="ps_t", bufs=2))
-            ps_z = early.enter_context(tc.psum_pool(name="ps_z", bufs=1))
 
             x_views = x.rearrange("(p m v) d -> v p m d", m=CHUNKS, v=VIEWS)
 
@@ -310,7 +323,7 @@ def tile_spin_pa_t_kernel(tc, x, head_w, head_b, cb_v, cb_g, out):
                 wsc = const.tile([P, 1], F32, name="wsc")
                 nc.vector.tensor_tensor(out=wsc[:], in0=vrn[:], in1=g_sb[:], op=ALU.mult)
                 nc.vector.tensor_scalar(out=w_bf[:], in0=v_sb[:], scalar1=wsc[:, 0:1], scalar2=None, op0=ALU.mult)
-                wt = ps_s.tile([P, 4, P], BF16, name="wt", tag="s2")
+                wt = ps_t.tile([P, 4, P], BF16, name="wt", tag="ht")
                 for t in range(4):
                     nc.tensor.transpose(wt[:, t, :], w_bf[:, 128 * t:128 * t + 128], ident_b[:])
                 live["wt"] = wt
@@ -330,11 +343,11 @@ def tile_spin_pa_t_kernel(tc, x, head_w, head_b, cb_v, cb_g, out):
                 head(i)
                 normalise(i)
                 load(i + NX)
+                h_q(i - 2)
                 x_tp(i + 2, 0, False)
                 h_tp(i - 1, 0)
                 x_tp(i + 2, 1, i % 2 == 1)
                 h_tp(i - 1, 1)
-                h_q(i - 2)
                 x_q(i + 1)
                 if i == 0:
                     codebook_a()
@@ -344,22 +357,25 @@ def tile_spin_pa_t_kernel(tc, x, head_w, head_b, cb_v, cb_g, out):
                     codebook_c()
                 if i == GROUPS + 2:
                     shift(0)
-            e_pipe(0, ps_s, "s2", lambda k: k % 2 == 1, lambda k: True)
-            c_first(0)
+                if i >= NG:
+                    e_steps(2 if i == NG else 3, GROUPS)
 
         late = ctx.enter_context(tc.tile_pool(name="late", bufs=1))
-        pp = ctx.enter_context(tc.tile_pool(name="pp", bufs=3))
-        ps_e = ctx.enter_context(tc.psum_pool(name="ps_e", bufs=2))
-        ps_v = ctx.enter_context(tc.psum_pool(name="ps_v", bufs=2))
-        ps_p = ctx.enter_context(tc.psum_pool(name="ps_p", bufs=2))
+        pp = ctx.enter_context(tc.tile_pool(name="pp", bufs=4))
         gh = [late.tile([P, CHUNKS * P], BF16, name="gh%d" % v) for v in range(VIEWS)]
         gl = [late.tile([P, CHUNKS * P], BF16, name="gl%d" % v) for v in range(VIEWS)]
 
         def g_max_a(v):
             nc.vector.tensor_copy(out=mrep[v][:], in_=cmax[v][:, 0:1].to_broadcast([P, P]))
-            mt = ps_p.tile([P, P], F32, name="mt", tag="tp")
+            if v == 0:
+                mt = ps_z.tile([P, P], F32, name="mt", tag="z_ps")
+            else:
+                mt = ps_x.tile([P, P], F32, name="mt", tag="xt")
             nc.tensor.transpose(mt[:], mrep[v][:], ident_f[:])
-            nc.vector.tensor_reduce(out=gmax[v][:], in_=mt[:], axis=AX.X, op=ALU.max)
+            live[("mt", v)] = mt
+
+        def g_max_b(v):
+            nc.vector.tensor_reduce(out=gmax[v][:], in_=live[("mt", v)][:], axis=AX.X, op=ALU.max)
             nc.vector.tensor_scalar(out=nb_t[v][:], in0=gmax[v][:], scalar1=-INV_T, scalar2=None, op0=ALU.mult)
 
         def p_exp(v, j):
@@ -368,7 +384,7 @@ def tile_spin_pa_t_kernel(tc, x, head_w, head_b, cb_v, cb_g, out):
             live[("pt", v, j)] = pt
 
         def p_tp(v, j):
-            tp = ps_p.tile([P, GROUP, P], F32, name="tp", tag="tp")
+            tp = ps_x.tile([P, GROUP, P], F32, name="tp", tag="xt")
             pt = live[("pt", v, j)]
             for q in range(GROUP):
                 nc.tensor.transpose(tp[:, q, :], pt[:, P * q:P * q + P], ident_f[:])
@@ -388,29 +404,27 @@ def tile_spin_pa_t_kernel(tc, x, head_w, head_b, cb_v, cb_g, out):
         def g_lo(v, j, eng):
             eng.tensor_tensor(out=gl[v][:, bank(j)], in0=ec[v][:, bank(j)], in1=gh[v][:, bank(j)], op=ALU.subtract)
 
-        banks = [(v, j) for v in range(VIEWS) for j in range(GROUPS)]
-        nb = len(banks)
         side = []
 
         def p_step(k):
             if k < nb:
                 p_exp(*banks[k])
-            if 0 <= k - 1 < nb:
-                p_tp(*banks[k - 1])
+            if 0 <= k - 3 < nb:
+                p_sum(*banks[k - 3])
             if 0 <= k - 2 < nb:
-                p_sum(*banks[k - 2])
+                p_tp(*banks[k - 2])
 
         def g_step(k):
             if k < nb:
                 g_mul(*banks[k])
-            if 0 <= k - 1 < nb:
-                g_hi(*banks[k - 1])
             if 0 <= k - 2 < nb:
-                g_lo(banks[k - 2][0], banks[k - 2][1], nc.vector if (k - 2) % 3 == 0 else nc.gpsimd)
+                g_hi(*banks[k - 2])
+            if 0 <= k - 4 < nb:
+                g_lo(banks[k - 4][0], banks[k - 4][1], nc.vector if (k - 4) % 3 == 0 else nc.gpsimd)
 
-        for k in range(nb + 2):
+        for k in range(nb + 3):
             side.append((p_step, k))
-        for k in range(nb + 2):
+        for k in range(nb + 4):
             side.append((g_step, k))
         done = [0]
 
@@ -421,42 +435,47 @@ def tile_spin_pa_t_kernel(tc, x, head_w, head_b, cb_v, cb_g, out):
                     f(k)
                     done[0] = done[0] + 1
 
-        shift(1)
-        e_pipe(1, ps_e, "et", lambda k: k % 2 == 1, lambda k: k % 2 == 1)
-        c_first(1)
-        for v in range(VIEWS):
-            g_max_a(v)
-        STEP = 4
-        for it in range(2):
-            u_pe(0, ps_v, "vec")
-            side_work(STEP)
-            u_pe(1, ps_v, "vec")
-            u_ve(0, True)
-            side_work(STEP)
-            c_pe(0, ps_v, "vec")
-            u_ve(1, True)
-            side_work(STEP)
-            c_pe(1, ps_v, "vec")
-            c_ve(0)
-            side_work(STEP)
-            c_ve(1)
-        u_pe(0, ps_v, "vec")
-        side_work(STEP)
-        u_pe(1, ps_v, "vec")
-        u_ve(0, False)
-        side_work(len(side))
-        u_ve(1, False)
-
-        for v in range(VIEWS):
-            f_ps = ps_e.tile([P, CHUNKS, 2], F32, name="f_ps", tag="et")
+        def f_pe(v):
+            f_ps = ps_h.tile([P, CHUNKS, REP, 2], F32, name="f_ps", tag="h_ps")
             pair_matmuls(f_ps, lambda m: gh[v][:, P * m:P * m + P], lambda m: gl[v][:, P * m:P * m + P],
                          live[("c2", v)])
             live[("f_ps", v)] = f_ps
+
+        shift(1)
+        for v in range(VIEWS):
+            g_max_a(v)
+        e_steps(4, nb + 6)
+        for v in range(VIEWS):
+            g_max_b(v)
+        e_steps(nb + 6, nb + 6)
+        STEP = 4
+        for it in range(2):
+            u_pe(0)
+            side_work(STEP)
+            u_pe(1)
+            u_ve(0, True)
+            side_work(STEP)
+            c_pe(0)
+            u_ve(1, True)
+            side_work(STEP)
+            c_pe(1)
+            c_ve(0)
+            side_work(STEP)
+            c_ve(1)
+        u_pe(0)
+        side_work(STEP)
+        f_pe(0)
+        u_ve(0, False)
+        side_work(len(side))
+        u_pe(1)
+        f_pe(1)
+        u_ve(1, False)
+
         for v in range(VIEWS):
             nc.scalar.activation(out=lnp[v][:], in_=sump[v][:], func=ACT.Ln)
         for v in range(VIEWS):
             fsum = small.tile([P, CHUNKS], F32, name="fsum", tag="r")
-            nc.vector.tensor_reduce(out=fsum[:], in_=live[("f_ps", v)][:], axis=AX.X, op=ALU.add)
+            nc.vector.tensor_reduce(out=fsum[:], in_=live[("f_ps", v)][:, :, 0, :], axis=AX.X, op=ALU.add)
             nc.vector.tensor_tensor(out=tq[v][:], in0=fsum[:], in1=live[("u", v)][:], op=ALU.mult)
         tsum = const.tile([P, CHUNKS], F32, name="tsum")
         nc.vector.tensor_tensor(out=tsum[:], in0=tq[0][:], in1=tq[1][:], op=ALU.add)

@@ -21,7 +21,8 @@ GROUPS = CHUNKS // GROUP
 NG = VIEWS * GROUPS
 W = GROUP * P
 NX = 4
-REP = 8
+REP = 12
+HALF = CHUNKS // 2
 INV_EPS = 50.0
 INV_T = 10.0
 
@@ -99,11 +100,11 @@ def tile_spin_pa_t_kernel(tc, x, head_w, head_b, cb_v, cb_g, out):
                 e_exp(*banks[k])
             if 0 <= k - 2 < nb:
                 e_hi(*banks[k - 2])
-                e_lo(banks[k - 2][0], banks[k - 2][1], nc.gpsimd if (k - 2) % 2 == 1 else nc.vector)
+                e_lo(banks[k - 2][0], banks[k - 2][1], nc.vector)
             if 0 <= k - 4 < nb:
                 e_tp(*banks[k - 4])
             if 0 <= k - 6 < nb:
-                e_cp(banks[k - 6][0], banks[k - 6][1], True)
+                e_cp(banks[k - 6][0], banks[k - 6][1], (k - 6) % 4 != 3)
                 if (k - 6) % GROUPS == GROUPS - 1:
                     c_first(banks[k - 6][0])
 
@@ -126,23 +127,33 @@ def tile_spin_pa_t_kernel(tc, x, head_w, head_b, cb_v, cb_g, out):
             nc.vector.reciprocal(out=cvec[:], in_=ctot[:])
             live[("c2", v)] = split_vec(cvec[:], 1, "c2_%d" % v)
 
-        def wide(two):
-            return two.to_broadcast([P, REP, 2]) if REP > 1 else two
+        def wide(two, rep):
+            return two.to_broadcast([P, rep, 2]) if rep > 1 else two
 
-        def pair_matmuls(ps, hi, lo, vec2):
-            for m in range(CHUNKS):
-                nc.tensor.matmul(out=ps[:, m, :, :], lhsT=hi(m), rhs=wide(vec2[:, 0:1, :]), start=True, stop=False)
-                nc.tensor.matmul(out=ps[:, m, :, :], lhsT=lo(m), rhs=wide(vec2[:, 0:1, :]), start=False, stop=True)
+        def pair_matmuls(ps, m0, n, rep, hi, lo, vec2):
+            for m in range(m0, m0 + n):
+                nc.tensor.matmul(out=ps[:, m - m0, :, :], lhsT=hi(m), rhs=wide(vec2[:, 0:1, :], rep),
+                                 start=True, stop=False)
+                nc.tensor.matmul(out=ps[:, m - m0, :, :], lhsT=lo(m), rhs=wide(vec2[:, 0:1, :], rep),
+                                 start=False, stop=True)
+
+        def vec_tile(v, shape, name):
+            if v == 0:
+                return ps_t.tile(shape, F32, name=name, tag="ht")
+            return ps_h.tile(shape, F32, name=name, tag="h_ps")
 
         def u_pe(v):
-            ps = ps_t.tile([P, CHUNKS, REP, 2], F32, name="u_ps", tag="ht")
-            pair_matmuls(ps, lambda m: ech[v][:, P * m:P * m + P], lambda m: ecl[v][:, P * m:P * m + P],
-                         live[("c2", v)])
-            live[("u_ps", v)] = ps
+            for half in range(2):
+                ps = vec_tile(v, [P, HALF, REP, 2], "u_ps")
+                pair_matmuls(ps, HALF * half, HALF, REP, lambda m: ech[v][:, P * m:P * m + P],
+                             lambda m: ecl[v][:, P * m:P * m + P], live[("c2", v)])
+                live[("u_ps", v, half)] = ps
 
         def u_ve(v, split):
             r = small.tile([P, CHUNKS], F32, name="r", tag="r")
-            nc.vector.tensor_reduce(out=r[:], in_=live[("u_ps", v)][:, :, 0, :], axis=AX.X, op=ALU.add)
+            for half in range(2):
+                nc.vector.tensor_reduce(out=r[:, HALF * half:HALF * half + HALF],
+                                        in_=live[("u_ps", v, half)][:, :, 0, :], axis=AX.X, op=ALU.add)
             u = small.tile([P, CHUNKS], F32, name="u", tag="u%d" % v)
             nc.vector.reciprocal(out=u[:], in_=r[:])
             live[("u", v)] = u
@@ -150,11 +161,14 @@ def tile_spin_pa_t_kernel(tc, x, head_w, head_b, cb_v, cb_g, out):
                 live[("u2", v)] = split_vec(u[:], CHUNKS, "u2_%d" % v)
 
         def c_pe(v):
-            ps = ps_t.tile([P, REP, 2], F32, name="c_ps", tag="ht")
+            if v == 0:
+                ps = ps_z.tile([P, REP, 2], F32, name="c_ps", tag="z_ps")
+            else:
+                ps = ps_h.tile([P, REP, 2], F32, name="c_ps", tag="h_ps")
             u2 = live[("u2", v)]
             for m in range(CHUNKS):
                 for h in range(2):
-                    nc.tensor.matmul(out=ps[:], lhsT=es[v][:, m, h, :], rhs=wide(u2[:, m:m + 1, :]),
+                    nc.tensor.matmul(out=ps[:], lhsT=es[v][:, m, h, :], rhs=wide(u2[:, m:m + 1, :], REP),
                                      start=(m == 0 and h == 0), stop=(m == CHUNKS - 1 and h == 1))
             live[("c_ps", v)] = ps
 
@@ -420,7 +434,7 @@ def tile_spin_pa_t_kernel(tc, x, head_w, head_b, cb_v, cb_g, out):
             if 0 <= k - 2 < nb:
                 g_hi(*banks[k - 2])
             if 0 <= k - 4 < nb:
-                g_lo(banks[k - 4][0], banks[k - 4][1], nc.vector if (k - 4) % 3 == 0 else nc.gpsimd)
+                g_lo(banks[k - 4][0], banks[k - 4][1], nc.vector if (k - 4) % 2 == 0 else nc.gpsimd)
 
         for k in range(nb + 3):
             side.append((p_step, k))
@@ -436,9 +450,9 @@ def tile_spin_pa_t_kernel(tc, x, head_w, head_b, cb_v, cb_g, out):
                     done[0] = done[0] + 1
 
         def f_pe(v):
-            f_ps = ps_h.tile([P, CHUNKS, REP, 2], F32, name="f_ps", tag="h_ps")
-            pair_matmuls(f_ps, lambda m: gh[v][:, P * m:P * m + P], lambda m: gl[v][:, P * m:P * m + P],
-                         live[("c2", v)])
+            f_ps = vec_tile(v, [P, CHUNKS, 1, 2], "f_ps")
+            pair_matmuls(f_ps, 0, CHUNKS, 1, lambda m: gh[v][:, P * m:P * m + P],
+                         lambda m: gl[v][:, P * m:P * m + P], live[("c2", v)])
             live[("f_ps", v)] = f_ps
 
         shift(1)
@@ -464,12 +478,12 @@ def tile_spin_pa_t_kernel(tc, x, head_w, head_b, cb_v, cb_g, out):
             c_ve(1)
         u_pe(0)
         side_work(STEP)
-        f_pe(0)
+        u_pe(1)
         u_ve(0, False)
         side_work(len(side))
-        u_pe(1)
-        f_pe(1)
+        f_pe(0)
         u_ve(1, False)
+        f_pe(1)
 
         for v in range(VIEWS):
             nc.scalar.activation(out=lnp[v][:], in_=sump[v][:], func=ACT.Ln)

@@ -255,10 +255,21 @@ def tile_spin_pa_t_kernel(tc, x, head_w, head_b, cb_v, cb_g, out):
                 rn = small.tile([P, GROUP], F32, name="rn", tag="rn")
                 nc.gpsimd.tensor_tensor(out=rn[:], in0=ssm[:], in1=neg_half[:], op=ALU.pow)
                 hn = stage.tile([P, GROUP * C], BF16, name="hn", tag="hn")
-                for c in range(GROUP):
+                for c in range(2):
                     nc.gpsimd.tensor_scalar(out=hn[:, C * c:C * c + C], in0=hbs[c][:], scalar1=rn[:, c:c + 1],
                                             scalar2=0.0, op0=ALU.mult, op1=ALU.add)
                 live[("hn", g)] = hn
+                live[("rn", g)] = rn
+
+            def normalise_rest(g):
+                if not ok(g):
+                    return
+                hbs, ss = live[("hb", g)]
+                hn = live[("hn", g)]
+                rn = live[("rn", g)]
+                nc.vector.tensor_scalar(out=hn[:, 2 * C:3 * C], in0=hbs[2][:], scalar1=rn[:, 2:3], scalar2=None,
+                                        op0=ALU.mult)
+                nc.scalar.activation(out=hn[:, 3 * C:4 * C], in_=hbs[3][:], func=ACT.Copy, scale=rn[:, 3:4])
 
             def h_tp(g, half):
                 if not ok(g):
@@ -354,6 +365,7 @@ def tile_spin_pa_t_kernel(tc, x, head_w, head_b, cb_v, cb_g, out):
 
             for i in range(NG + 3):
                 logits(i - 3)
+                normalise_rest(i - 1)
                 head(i)
                 normalise(i)
                 load(i + NX)

@@ -23,6 +23,7 @@ W = GROUP * P
 NX = 4
 REP = 12
 HALF = CHUNKS // 2
+E_START = 12
 INV_EPS = 50.0
 INV_T = 10.0
 
@@ -47,7 +48,7 @@ def tile_spin_pa_t_kernel(tc, x, head_w, head_b, cb_v, cb_g, out):
         ecl = [big.tile([P, CHUNKS * P], BF16, name="ecl%d" % v) for v in range(VIEWS)]
         es = [big.tile([P, CHUNKS, 2, P], BF16, name="es%d" % v) for v in range(VIEWS)]
         zmax = [const.tile([P, GROUPS], F32, name="zmax%d" % v) for v in range(VIEWS)]
-        csum = [const.tile([P, GROUPS], F32, name="csum%d" % v) for v in range(VIEWS)]
+        csum = [const.tile([P, GROUPS // 2], F32, name="csum%d" % v) for v in range(VIEWS)]
         cmax = [const.tile([P, 1], F32, name="cmax%d" % v) for v in range(VIEWS)]
         nb_e = [const.tile([P, 1], F32, name="nb_e%d" % v) for v in range(VIEWS)]
         nb_t = [const.tile([P, 1], F32, name="nb_t%d" % v) for v in range(VIEWS)]
@@ -61,19 +62,22 @@ def tile_spin_pa_t_kernel(tc, x, head_w, head_b, cb_v, cb_g, out):
         def bank(j):
             return slice(W * j, W * j + W)
 
+        def unit(j2):
+            return slice(2 * W * j2, 2 * W * j2 + 2 * W)
+
         def shift(v):
             nc.vector.tensor_reduce(out=cmax[v][:], in_=zmax[v][:], axis=AX.X, op=ALU.max)
             nc.vector.tensor_scalar(out=nb_e[v][:], in0=cmax[v][:], scalar1=-INV_EPS, scalar2=None, op0=ALU.mult)
 
         def e_exp(v, j):
-            nc.scalar.activation(out=ec[v][:, bank(j)], in_=zc[v][:, bank(j)], func=ACT.Exp,
+            nc.scalar.activation(out=ec[v][:, unit(j)], in_=zc[v][:, unit(j)], func=ACT.Exp,
                                  bias=nb_e[v][:, 0:1], scale=INV_EPS, accum_out=csum[v][:, j:j + 1])
 
         def e_hi(v, j):
-            nc.vector.tensor_copy(out=ech[v][:, bank(j)], in_=ec[v][:, bank(j)])
+            nc.vector.tensor_copy(out=ech[v][:, unit(j)], in_=ec[v][:, unit(j)])
 
         def e_lo(v, j, eng):
-            eng.tensor_tensor(out=ecl[v][:, bank(j)], in0=ec[v][:, bank(j)], in1=ech[v][:, bank(j)],
+            eng.tensor_tensor(out=ecl[v][:, unit(j)], in0=ec[v][:, unit(j)], in1=ech[v][:, unit(j)],
                               op=ALU.subtract)
 
         def e_tp(v, j):
@@ -91,28 +95,36 @@ def tile_spin_pa_t_kernel(tc, x, head_w, head_b, cb_v, cb_g, out):
             else:
                 nc.vector.tensor_copy(out=dst, in_=live[("et", v, j)][:])
 
-        banks = [(v, j) for v in range(VIEWS) for j in range(GROUPS)]
-        nb = len(banks)
-        e_done = [0]
+        units = [(v, j) for v in range(VIEWS) for j in range(GROUPS // 2)]
+        nu = len(units)
+        x_done = [0]
+        h_done = [0]
+        b_done = [0]
+        c_done = [0]
 
-        def e_step(k):
-            if k < nb:
-                e_exp(*banks[k])
-            if 0 <= k - 2 < nb:
-                e_hi(*banks[k - 2])
-                e_lo(banks[k - 2][0], banks[k - 2][1], nc.vector)
-            if 0 <= k - 4 < nb:
-                e_tp(*banks[k - 4])
-            if 0 <= k - 6 < nb:
-                e_cp(banks[k - 6][0], banks[k - 6][1], (k - 6) % 4 != 3)
-                if (k - 6) % GROUPS == GROUPS - 1:
-                    c_first(banks[k - 6][0])
+        def e_front(limit):
+            if h_done[0] < x_done[0]:
+                v, j = units[h_done[0]]
+                e_hi(v, j)
+                e_lo(v, j, nc.vector)
+                h_done[0] = h_done[0] + 1
+            if x_done[0] < limit:
+                e_exp(*units[x_done[0]])
+                x_done[0] = x_done[0] + 1
 
-        def e_steps(n, limit):
-            for q in range(n):
-                if e_done[0] < min(limit, nb + 6):
-                    e_step(e_done[0])
-                    e_done[0] = e_done[0] + 1
+        def e_back():
+            if c_done[0] < b_done[0]:
+                v, j = units[c_done[0]]
+                e_cp(v, 2 * j, True)
+                e_cp(v, 2 * j + 1, c_done[0] % 2 == 1)
+                if j == GROUPS // 2 - 1:
+                    c_first(v)
+                c_done[0] = c_done[0] + 1
+            if b_done[0] < h_done[0]:
+                v, j = units[b_done[0]]
+                e_tp(v, 2 * j)
+                e_tp(v, 2 * j + 1)
+                b_done[0] = b_done[0] + 1
 
         def split_vec(src, cols, name):
             two = small.tile([P, cols, 2], BF16, name=name, tag=name)
@@ -255,21 +267,10 @@ def tile_spin_pa_t_kernel(tc, x, head_w, head_b, cb_v, cb_g, out):
                 rn = small.tile([P, GROUP], F32, name="rn", tag="rn")
                 nc.gpsimd.tensor_tensor(out=rn[:], in0=ssm[:], in1=neg_half[:], op=ALU.pow)
                 hn = stage.tile([P, GROUP * C], BF16, name="hn", tag="hn")
-                for c in range(2):
+                for c in range(GROUP):
                     nc.gpsimd.tensor_scalar(out=hn[:, C * c:C * c + C], in0=hbs[c][:], scalar1=rn[:, c:c + 1],
                                             scalar2=0.0, op0=ALU.mult, op1=ALU.add)
                 live[("hn", g)] = hn
-                live[("rn", g)] = rn
-
-            def normalise_rest(g):
-                if not ok(g):
-                    return
-                hbs, ss = live[("hb", g)]
-                hn = live[("hn", g)]
-                rn = live[("rn", g)]
-                nc.vector.tensor_scalar(out=hn[:, 2 * C:3 * C], in0=hbs[2][:], scalar1=rn[:, 2:3], scalar2=None,
-                                        op0=ALU.mult)
-                nc.scalar.activation(out=hn[:, 3 * C:4 * C], in_=hbs[3][:], func=ACT.Copy, scale=rn[:, 3:4])
 
             def h_tp(g, half):
                 if not ok(g):
@@ -365,7 +366,6 @@ def tile_spin_pa_t_kernel(tc, x, head_w, head_b, cb_v, cb_g, out):
 
             for i in range(NG + 3):
                 logits(i - 3)
-                normalise_rest(i - 1)
                 head(i)
                 normalise(i)
                 load(i + NX)
@@ -383,11 +383,14 @@ def tile_spin_pa_t_kernel(tc, x, head_w, head_b, cb_v, cb_g, out):
                     codebook_c()
                 if i == GROUPS + 2:
                     shift(0)
+                if i >= E_START:
+                    e_front(GROUPS // 2)
                 if i >= NG:
-                    e_steps(2 if i == NG else 3, GROUPS)
+                    e_back()
+                    e_back()
 
         late = ctx.enter_context(tc.tile_pool(name="late", bufs=1))
-        pp = ctx.enter_context(tc.tile_pool(name="pp", bufs=4))
+        pp = ctx.enter_context(tc.tile_pool(name="pp", bufs=3))
         gh = [late.tile([P, CHUNKS * P], BF16, name="gh%d" % v) for v in range(VIEWS)]
         gl = [late.tile([P, CHUNKS * P], BF16, name="gl%d" % v) for v in range(VIEWS)]
 
@@ -405,15 +408,16 @@ def tile_spin_pa_t_kernel(tc, x, head_w, head_b, cb_v, cb_g, out):
             nc.vector.tensor_scalar(out=nb_t[v][:], in0=gmax[v][:], scalar1=-INV_T, scalar2=None, op0=ALU.mult)
 
         def p_exp(v, j):
-            pt = pp.tile([P, W], F32, name="pt", tag="pt")
-            nc.scalar.activation(out=pt[:], in_=zc[v][:, bank(j)], func=ACT.Exp, bias=nb_t[v][:, 0:1], scale=INV_T)
+            pt = pp.tile([P, 2 * W], F32, name="pt", tag="pt")
+            nc.scalar.activation(out=pt[:], in_=zc[v][:, unit(j)], func=ACT.Exp, bias=nb_t[v][:, 0:1], scale=INV_T)
             live[("pt", v, j)] = pt
 
         def p_tp(v, j):
             tp = ps_x.tile([P, GROUP, P], F32, name="tp", tag="xt")
-            pt = live[("pt", v, j)]
+            pt = live[("pt", v, j // 2)]
             for q in range(GROUP):
-                nc.tensor.transpose(tp[:, q, :], pt[:, P * q:P * q + P], ident_f[:])
+                lo = W * (j % 2) + P * q
+                nc.tensor.transpose(tp[:, q, :], pt[:, lo:lo + P], ident_f[:])
             live[("tp", v, j)] = tp
 
         def p_sum(v, j):
@@ -421,37 +425,37 @@ def tile_spin_pa_t_kernel(tc, x, head_w, head_b, cb_v, cb_g, out):
                                     axis=AX.X, op=ALU.add)
 
         def g_mul(v, j):
-            nc.vector.tensor_tensor(out=ec[v][:, bank(j)], in0=ec[v][:, bank(j)], in1=zc[1 - v][:, bank(j)],
+            nc.vector.tensor_tensor(out=ec[v][:, unit(j)], in0=ec[v][:, unit(j)], in1=zc[1 - v][:, unit(j)],
                                     op=ALU.mult)
 
         def g_hi(v, j):
-            nc.scalar.copy(out=gh[v][:, bank(j)], in_=ec[v][:, bank(j)])
+            nc.scalar.copy(out=gh[v][:, unit(j)], in_=ec[v][:, unit(j)])
 
         def g_lo(v, j, eng):
-            eng.tensor_tensor(out=gl[v][:, bank(j)], in0=ec[v][:, bank(j)], in1=gh[v][:, bank(j)], op=ALU.subtract)
+            eng.tensor_tensor(out=gl[v][:, unit(j)], in0=ec[v][:, unit(j)], in1=gh[v][:, unit(j)], op=ALU.subtract)
 
         side = []
 
         def p_step(k):
-            if k < nb:
-                p_exp(*banks[k])
-            if 0 <= k - 3 < nb:
-                p_sum(*banks[k - 3])
-            if 0 <= k - 2 < nb:
-                p_tp(*banks[k - 2])
+            if k < nu:
+                p_exp(*units[k])
+            for half in range(2):
+                if 0 <= k - 2 < nu:
+                    p_sum(units[k - 2][0], 2 * units[k - 2][1] + half)
+                if 0 <= k - 1 < nu:
+                    p_tp(units[k - 1][0], 2 * units[k - 1][1] + half)
 
         def g_step(k):
-            if k < nb:
-                g_mul(*banks[k])
-            if 0 <= k - 2 < nb:
-                g_hi(*banks[k - 2])
-            if 0 <= k - 4 < nb:
-                g_lo(banks[k - 4][0], banks[k - 4][1], nc.vector if (k - 4) % 2 == 0 else nc.gpsimd)
+            if k < nu:
+                g_mul(*units[k])
+            if 0 <= k - 1 < nu:
+                g_hi(*units[k - 1])
+            if 0 <= k - 2 < nu:
+                g_lo(units[k - 2][0], units[k - 2][1], nc.vector if (k - 2) % 2 == 0 else nc.gpsimd)
 
-        for k in range(nb + 3):
-            side.append((p_step, k))
-        for k in range(nb + 4):
+        for k in range(nu + 2):
             side.append((g_step, k))
+            side.append((p_step, k))
         done = [0]
 
         def side_work(n):
@@ -467,44 +471,56 @@ def tile_spin_pa_t_kernel(tc, x, head_w, head_b, cb_v, cb_g, out):
                          lambda m: gl[v][:, P * m:P * m + P], live[("c2", v)])
             live[("f_ps", v)] = f_ps
 
+        STEP = 2
         shift(1)
         for v in range(VIEWS):
             g_max_a(v)
-        e_steps(4, nb + 6)
+        e_front(nu)
+        u_pe(0)
+        e_front(nu)
+        e_back()
         for v in range(VIEWS):
             g_max_b(v)
-        e_steps(nb + 6, nb + 6)
-        STEP = 4
-        for it in range(2):
-            u_pe(0)
-            side_work(STEP)
-            u_pe(1)
-            u_ve(0, True)
-            side_work(STEP)
-            c_pe(0)
-            u_ve(1, True)
-            side_work(STEP)
-            c_pe(1)
-            c_ve(0)
-            side_work(STEP)
-            c_ve(1)
+        u_ve(0, True)
+        e_front(nu)
+        e_back()
+        c_pe(0)
+        e_front(nu)
+        e_back()
+        c_ve(0)
+        e_front(nu)
+        e_back()
+        e_back()
+        e_back()
+        u_pe(1)
         u_pe(0)
         side_work(STEP)
+        u_ve(1, True)
+        u_ve(0, True)
+        side_work(STEP)
+        c_pe(1)
+        c_pe(0)
+        side_work(STEP)
+        c_ve(1)
+        c_ve(0)
+        side_work(STEP)
         u_pe(1)
+        u_pe(0)
+        side_work(STEP)
+        u_ve(1, True)
         u_ve(0, False)
-        side_work(len(side))
+        side_work(STEP)
+        c_pe(1)
+        side_work(STEP)
         f_pe(0)
-        u_ve(1, False)
+        c_ve(1)
+        side_work(len(side))
+        u_pe(1)
         f_pe(1)
+        u_ve(1, False)
 
         for v in range(VIEWS):
             nc.scalar.activation(out=lnp[v][:], in_=sump[v][:], func=ACT.Ln)
-        for v in range(VIEWS):
-            fsum = small.tile([P, CHUNKS], F32, name="fsum", tag="r")
-            nc.vector.tensor_reduce(out=fsum[:], in_=live[("f_ps", v)][:, :, 0, :], axis=AX.X, op=ALU.add)
-            nc.vector.tensor_tensor(out=tq[v][:], in0=fsum[:], in1=live[("u", v)][:], op=ALU.mult)
-        tsum = const.tile([P, CHUNKS], F32, name="tsum")
-        nc.vector.tensor_tensor(out=tsum[:], in0=tq[0][:], in1=tq[1][:], op=ALU.add)
         lsum = const.tile([P, CHUNKS], F32, name="lsum")
         nc.vector.tensor_tensor(out=lsum[:], in0=lnp[0][:], in1=lnp[1][:], op=ALU.add)
         msum = const.tile([P, 1], F32, name="msum")
@@ -512,8 +528,15 @@ def tile_spin_pa_t_kernel(tc, x, head_w, head_b, cb_v, cb_g, out):
         msc = const.tile([P, 1], F32, name="msc")
         nc.vector.tensor_scalar(out=msc[:], in0=msum[:], scalar1=0.5 * INV_T, scalar2=None, op0=ALU.mult)
         part = const.tile([P, CHUNKS], F32, name="part")
-        nc.vector.tensor_scalar(out=part[:], in0=tsum[:], scalar1=-0.5 * INV_T, scalar2=msc[:, 0:1],
+        nc.vector.tensor_scalar(out=part[:], in0=lsum[:], scalar1=0.5, scalar2=msc[:, 0:1],
                                 op0=ALU.mult, op1=ALU.add)
+        for v in range(VIEWS):
+            fsum = small.tile([P, CHUNKS], F32, name="fsum", tag="r")
+            nc.vector.tensor_reduce(out=fsum[:], in_=live[("f_ps", v)][:, :, 0, :], axis=AX.X, op=ALU.add)
+            nc.vector.tensor_tensor(out=tq[v][:], in0=fsum[:], in1=live[("u", v)][:], op=ALU.mult)
+        tsum = const.tile([P, CHUNKS], F32, name="tsum")
+        nc.vector.tensor_tensor(out=tsum[:], in0=tq[0][:], in1=tq[1][:], op=ALU.add)
         res = const.tile([P, CHUNKS], F32, name="res")
-        nc.vector.scalar_tensor_tensor(out=res[:], in0=lsum[:], scalar=0.5, in1=part[:], op0=ALU.mult, op1=ALU.add)
+        nc.vector.scalar_tensor_tensor(out=res[:], in0=tsum[:], scalar=-0.5 * INV_T, in1=part[:],
+                                       op0=ALU.mult, op1=ALU.add)
         nc.sync.dma_start(out=out.rearrange("(p m) -> p m", m=CHUNKS), in_=res[:])

@@ -23,7 +23,8 @@ W = GROUP * P
 NX = 4
 REP = 12
 HALF = CHUNKS // 2
-E_START = 12
+NT = 2 * NG
+E_START = NT - NG + 12
 INV_EPS = 50.0
 INV_T = 10.0
 
@@ -199,7 +200,7 @@ def tile_spin_pa_t_kernel(tc, x, head_w, head_b, cb_v, cb_g, out):
             x_views = x.rearrange("(p m v) d -> v p m d", m=CHUNKS, v=VIEWS)
 
             def ok(g):
-                return 0 <= g < NG
+                return 0 <= g < NT
 
             def load(g):
                 if not ok(g):
@@ -207,7 +208,7 @@ def tile_spin_pa_t_kernel(tc, x, head_w, head_b, cb_v, cb_g, out):
                 x_sb = xin.tile([P, GROUP * D], BF16, name="x_sb", tag="x_sb")
                 j = g % GROUPS
                 nc.sync.dma_start(out=x_sb[:].rearrange("p (m d) -> p m d", m=GROUP),
-                                  in_=x_views[g // GROUPS][:, GROUP * j:GROUP * j + GROUP, :])
+                                  in_=x_views[(g % NG) // GROUPS][:, GROUP * j:GROUP * j + GROUP, :])
                 live[("x", g)] = x_sb
 
             def k_to_partitions(src, grouped, half, on_scalar):
@@ -298,7 +299,7 @@ def tile_spin_pa_t_kernel(tc, x, head_w, head_b, cb_v, cb_g, out):
                 if not ok(g):
                     return
                 hq, hs = live[("hq", g)]
-                v = g // GROUPS
+                v = (g % NG) // GROUPS
                 j = g % GROUPS
                 z_ps = ps_z.tile([P, W], F32, name="z_ps", tag="z_ps")
                 nc.tensor.matmul_mx(out=z_ps[:], lhsT=cq[:].bitcast(FP8X4), lhsT_scale=cs8[:],
@@ -364,7 +365,7 @@ def tile_spin_pa_t_kernel(tc, x, head_w, head_b, cb_v, cb_g, out):
             cq = const.tile([P, K], U32, name="cq", align_bytes=64)
             cs8 = const.tile([P, K], U8, name="cs8", align_bytes=64)
 
-            for i in range(NG + 3):
+            for i in range(NT + 3):
                 logits(i - 3)
                 head(i)
                 normalise(i)
@@ -381,11 +382,11 @@ def tile_spin_pa_t_kernel(tc, x, head_w, head_b, cb_v, cb_g, out):
                     codebook_b()
                 if i == 2:
                     codebook_c()
-                if i == GROUPS + 2:
+                if i == NT - NG + GROUPS + 2:
                     shift(0)
                 if i >= E_START:
                     e_front(GROUPS // 2)
-                if i >= NG:
+                if i >= NT:
                     e_back()
                     e_back()
 

@@ -23,8 +23,7 @@ W = GROUP * P
 NX = 4
 REP = 12
 HALF = CHUNKS // 2
-NT = 2 * NG
-E_START = NT - NG + 12
+E_START = 12
 INV_EPS = 50.0
 INV_T = 10.0
 
@@ -107,7 +106,14 @@ def tile_spin_pa_t_kernel(tc, x, head_w, head_b, cb_v, cb_g, out):
             if h_done[0] < x_done[0]:
                 v, j = units[h_done[0]]
                 e_hi(v, j)
-                e_lo(v, j, nc.vector)
+                if v == 0:
+                    e_lo(v, j, nc.vector)
+                else:
+                    for half in range(2):
+                        cols = bank(2 * j + half)
+                        eng = nc.vector if half == 0 else nc.gpsimd
+                        eng.tensor_tensor(out=ecl[v][:, cols], in0=ec[v][:, cols], in1=ech[v][:, cols],
+                                          op=ALU.subtract)
                 h_done[0] = h_done[0] + 1
             if x_done[0] < limit:
                 e_exp(*units[x_done[0]])
@@ -200,7 +206,7 @@ def tile_spin_pa_t_kernel(tc, x, head_w, head_b, cb_v, cb_g, out):
             x_views = x.rearrange("(p m v) d -> v p m d", m=CHUNKS, v=VIEWS)
 
             def ok(g):
-                return 0 <= g < NT
+                return 0 <= g < NG
 
             def load(g):
                 if not ok(g):
@@ -208,7 +214,7 @@ def tile_spin_pa_t_kernel(tc, x, head_w, head_b, cb_v, cb_g, out):
                 x_sb = xin.tile([P, GROUP * D], BF16, name="x_sb", tag="x_sb")
                 j = g % GROUPS
                 nc.sync.dma_start(out=x_sb[:].rearrange("p (m d) -> p m d", m=GROUP),
-                                  in_=x_views[(g % NG) // GROUPS][:, GROUP * j:GROUP * j + GROUP, :])
+                                  in_=x_views[g // GROUPS][:, GROUP * j:GROUP * j + GROUP, :])
                 live[("x", g)] = x_sb
 
             def k_to_partitions(src, grouped, half, on_scalar):
@@ -268,9 +274,13 @@ def tile_spin_pa_t_kernel(tc, x, head_w, head_b, cb_v, cb_g, out):
                 rn = small.tile([P, GROUP], F32, name="rn", tag="rn")
                 nc.gpsimd.tensor_tensor(out=rn[:], in0=ssm[:], in1=neg_half[:], op=ALU.pow)
                 hn = stage.tile([P, GROUP * C], BF16, name="hn", tag="hn")
-                for c in range(GROUP):
+                for c in range(2 if g == NG - 1 else GROUP):
                     nc.gpsimd.tensor_scalar(out=hn[:, C * c:C * c + C], in0=hbs[c][:], scalar1=rn[:, c:c + 1],
                                             scalar2=0.0, op0=ALU.mult, op1=ALU.add)
+                if g == NG - 1:
+                    nc.vector.tensor_scalar(out=hn[:, 2 * C:3 * C], in0=hbs[2][:], scalar1=rn[:, 2:3],
+                                            scalar2=None, op0=ALU.mult)
+                    nc.scalar.activation(out=hn[:, 3 * C:4 * C], in_=hbs[3][:], func=ACT.Copy, scale=rn[:, 3:4])
                 live[("hn", g)] = hn
 
             def h_tp(g, half):
@@ -285,7 +295,11 @@ def tile_spin_pa_t_kernel(tc, x, head_w, head_b, cb_v, cb_g, out):
                     for t in range(4):
                         lo = C * (2 * half + cc) + 128 * t
                         nc.tensor.transpose(ht[:, cc, t, :], hn[:, lo:lo + 128], ident_b[:])
-                nc.scalar.copy(out=hgv[:, 2 * half:2 * half + 2, :, :], in_=ht[:].rearrange("p c t s -> p c s t"))
+                if g == NG - 1 and half == 1:
+                    nc.vector.tensor_copy(out=hgv[:, 2:4, :, :], in_=ht[:].rearrange("p c t s -> p c s t"))
+                else:
+                    nc.scalar.copy(out=hgv[:, 2 * half:2 * half + 2, :, :],
+                                   in_=ht[:].rearrange("p c t s -> p c s t"))
 
             def h_q(g):
                 if not ok(g):
@@ -299,7 +313,7 @@ def tile_spin_pa_t_kernel(tc, x, head_w, head_b, cb_v, cb_g, out):
                 if not ok(g):
                     return
                 hq, hs = live[("hq", g)]
-                v = (g % NG) // GROUPS
+                v = g // GROUPS
                 j = g % GROUPS
                 z_ps = ps_z.tile([P, W], F32, name="z_ps", tag="z_ps")
                 nc.tensor.matmul_mx(out=z_ps[:], lhsT=cq[:].bitcast(FP8X4), lhsT_scale=cs8[:],
@@ -308,9 +322,16 @@ def tile_spin_pa_t_kernel(tc, x, head_w, head_b, cb_v, cb_g, out):
                                         op0=ALU.mult, op1=ALU.max, accum_out=zmax[v][:, j:j + 1])
 
             w_sb = const.tile([P, GROUP * D], BF16, name="w_sb")
-            nc.sync.dma_start(out=w_sb[:].rearrange("p (c k) -> p c k", c=GROUP),
-                              in_=head_w.rearrange("(c p) k -> p c k", p=P))
-            for g in range(NX):
+            w_rows = head_w.rearrange("(c p) k -> p c k", p=P)
+            x0_sb = xin.tile([P, GROUP * D], BF16, name="x_sb", tag="x_sb")
+            live[("x", 0)] = x0_sb
+            for half in range(2):
+                cols = slice(2 * D * half, 2 * D * half + 2 * D)
+                nc.sync.dma_start(out=w_sb[:, cols].rearrange("p (c k) -> p c k", c=2),
+                                  in_=w_rows[:, 2 * half:2 * half + 2, :])
+                nc.sync.dma_start(out=x0_sb[:, cols].rearrange("p (m d) -> p m d", m=2),
+                                  in_=x_views[0][:, 2 * half:2 * half + 2, :])
+            for g in range(1, NX):
                 load(g)
             b_bc = const.tile([P, C], BF16, name="b_bc")
             nc.scalar.dma_start(out=b_bc[:], in_=head_b.partition_broadcast(P))
@@ -328,8 +349,8 @@ def tile_spin_pa_t_kernel(tc, x, head_w, head_b, cb_v, cb_g, out):
 
             wgr = const.tile([P, GROUP * D], BF16, name="wgr", align_bytes=64)
             k_to_partitions(w_sb, wgr, 0, False)
-            k_to_partitions(w_sb, wgr, 1, True)
-            x_tp(0, 0, False)
+            x_tp(0, 0, True)
+            k_to_partitions(w_sb, wgr, 1, False)
             x_tp(0, 1, True)
             wq = const.tile([P, C], U32, name="wq", align_bytes=64)
             ws = const.tile([P, C], U8, name="ws", align_bytes=64)
@@ -365,28 +386,28 @@ def tile_spin_pa_t_kernel(tc, x, head_w, head_b, cb_v, cb_g, out):
             cq = const.tile([P, K], U32, name="cq", align_bytes=64)
             cs8 = const.tile([P, K], U8, name="cs8", align_bytes=64)
 
-            for i in range(NT + 3):
+            for i in range(NG + 3):
                 logits(i - 3)
                 head(i)
                 normalise(i)
                 load(i + NX)
+                x_q(i + 1)
                 h_q(i - 2)
                 x_tp(i + 2, 0, False)
                 h_tp(i - 1, 0)
                 x_tp(i + 2, 1, i % 2 == 1)
                 h_tp(i - 1, 1)
-                x_q(i + 1)
                 if i == 0:
                     codebook_a()
                 if i == 1:
                     codebook_b()
                 if i == 2:
                     codebook_c()
-                if i == NT - NG + GROUPS + 2:
+                if i == GROUPS + 2:
                     shift(0)
                 if i >= E_START:
                     e_front(GROUPS // 2)
-                if i >= NT:
+                if i >= NG:
                     e_back()
                     e_back()
 

@@ -288,18 +288,18 @@ def tile_spin_pa_t_kernel(tc, x, head_w, head_b, cb_v, cb_g, out):
                     return
                 if half == 0:
                     live[("hg", g)] = stage.tile([P, GROUP * C], BF16, name="hg", tag="hg", align_bytes=64)
-                hn = live[("hn", g)]
-                hgv = live[("hg", g)][:].rearrange("p (c s t) -> p c s t", c=GROUP, t=4)
-                ht = ps_t.tile([P, 2, 4, P], BF16, name="ht", tag="ht")
+                hn32 = live[("hn", g)][:].bitcast(F32)
+                hgv = live[("hg", g)][:].bitcast(F32).rearrange("p (c s u) -> p c s u", c=GROUP, u=2)
+                ht = ps_t.tile([P, 2, 2, P], F32, name="ht", tag="ht")
                 for cc in range(2):
-                    for t in range(4):
-                        lo = C * (2 * half + cc) + 128 * t
-                        nc.tensor.transpose(ht[:, cc, t, :], hn[:, lo:lo + 128], ident_b[:])
+                    for u in range(2):
+                        lo = 256 * (2 * half + cc) + 128 * u
+                        nc.tensor.transpose(ht[:, cc, u, :], hn32[:, lo:lo + 128], ident_f[:])
                 if g == NG - 1 and half == 1:
-                    nc.vector.tensor_copy(out=hgv[:, 2:4, :, :], in_=ht[:].rearrange("p c t s -> p c s t"))
+                    nc.vector.tensor_copy(out=hgv[:, 2:4, :, :], in_=ht[:].rearrange("p c u s -> p c s u"))
                 else:
                     nc.scalar.copy(out=hgv[:, 2 * half:2 * half + 2, :, :],
-                                   in_=ht[:].rearrange("p c t s -> p c s t"))
+                                   in_=ht[:].rearrange("p c u s -> p c s u"))
 
             def h_q(g):
                 if not ok(g):
@@ -371,14 +371,14 @@ def tile_spin_pa_t_kernel(tc, x, head_w, head_b, cb_v, cb_g, out):
                 wsc = const.tile([P, 1], F32, name="wsc")
                 nc.vector.tensor_tensor(out=wsc[:], in0=vrn[:], in1=g_sb[:], op=ALU.mult)
                 nc.vector.tensor_scalar(out=w_bf[:], in0=v_sb[:], scalar1=wsc[:, 0:1], scalar2=None, op0=ALU.mult)
-                wt = ps_t.tile([P, 4, P], BF16, name="wt", tag="ht")
-                for t in range(4):
-                    nc.tensor.transpose(wt[:, t, :], w_bf[:, 128 * t:128 * t + 128], ident_b[:])
+                wt = ps_t.tile([P, 2, P], F32, name="wt", tag="ht")
+                for u in range(2):
+                    nc.tensor.transpose(wt[:, u, :], w_bf[:].bitcast(F32)[:, 128 * u:128 * u + 128], ident_f[:])
                 live["wt"] = wt
 
             def codebook_b():
-                nc.vector.tensor_copy(out=wg[:].rearrange("p (s t) -> p s t", t=4),
-                                      in_=live["wt"][:].rearrange("p t s -> p s t"))
+                nc.vector.tensor_copy(out=wg[:].bitcast(F32).rearrange("p (s u) -> p s u", u=2),
+                                      in_=live["wt"][:].rearrange("p u s -> p s u"))
 
             def codebook_c():
                 nc.vector.quantize_mx(out=cq[:].bitcast(FP8X4), scales=cs8[:], in_=wg[:])
@@ -393,9 +393,9 @@ def tile_spin_pa_t_kernel(tc, x, head_w, head_b, cb_v, cb_g, out):
                 load(i + NX)
                 x_q(i + 1)
                 h_q(i - 2)
-                x_tp(i + 2, 0, False)
+                x_tp(i + 2, 0, True)
                 h_tp(i - 1, 0)
-                x_tp(i + 2, 1, i % 2 == 1)
+                x_tp(i + 2, 1, True)
                 h_tp(i - 1, 1)
                 if i == 0:
                     codebook_a()

@@ -23,6 +23,7 @@ W = GROUP * P
 NX = 4
 REP = 12
 HALF = CHUNKS // 2
+ON_VECTOR = 2
 E_START = 12
 INV_EPS = 50.0
 INV_T = 10.0
@@ -217,20 +218,26 @@ def tile_spin_pa_t_kernel(tc, x, head_w, head_b, cb_v, cb_g, out):
                                   in_=x_views[g // GROUPS][:, GROUP * j:GROUP * j + GROUP, :])
                 live[("x", g)] = x_sb
 
-            def k_to_partitions(src, grouped, half, on_scalar):
+            def words_tp(src, pool, tag, half):
                 src32 = src[:].bitcast(F32)
-                g32 = grouped[:].bitcast(F32).rearrange("p (c s u) -> p c s u", c=GROUP, u=2)
-                xt = ps_x.tile([P, 2, 2, P], F32, name="xt", tag="xt")
+                xt = pool.tile([P, 2, 2, P], F32, name=tag, tag=tag)
                 for cc in range(2):
                     for u in range(2):
                         lo = 256 * (2 * half + cc) + 128 * u
                         nc.tensor.transpose(xt[:, cc, u, :], src32[:, lo:lo + 128], ident_f[:])
+                return xt
+
+            def words_cp(xt, grouped, half, on_scalar):
+                g32 = grouped[:].bitcast(F32).rearrange("p (c s u) -> p c s u", c=GROUP, u=2)
                 dst = g32[:, 2 * half:2 * half + 2, :, :]
                 srcv = xt[:].rearrange("p c u s -> p c s u")
                 if on_scalar:
                     nc.scalar.copy(out=dst, in_=srcv)
                 else:
                     nc.vector.tensor_copy(out=dst, in_=srcv)
+
+            def k_to_partitions(src, grouped, half, on_scalar):
+                words_cp(words_tp(src, ps_x, "xt", half), grouped, half, on_scalar)
 
             def x_tp(g, half, on_scalar):
                 if not ok(g):
@@ -247,59 +254,63 @@ def tile_spin_pa_t_kernel(tc, x, head_w, head_b, cb_v, cb_g, out):
                 nc.vector.quantize_mx(out=xq[:].bitcast(FP8X4), scales=xs[:], in_=live[("xg", g)][:])
                 live[("xq", g)] = (xq, xs)
 
-            def head(g):
+            def head_pe(g, c):
                 if not ok(g):
                     return
                 xq, xs = live[("xq", g)]
-                ss = small.tile([P, GROUP], F32, name="ss", tag="ss")
-                hbs = []
-                for c in range(GROUP):
-                    h_ps = ps_h.tile([P, C], F32, name="h_ps", tag="h_ps")
-                    nc.tensor.matmul_mx(out=h_ps[:], lhsT=xq[:, P * c:P * c + P].bitcast(FP8X4),
-                                        lhsT_scale=xs[:, P * c:P * c + P], rhs=wq[:].bitcast(FP8X4),
-                                        rhs_scale=ws[:], start=True, stop=True)
-                    hb = hbp.tile([P, C], F32, name="hb", tag="hb")
-                    nc.vector.tensor_tensor(out=hb[:], in0=h_ps[:], in1=b_bc[:], op=ALU.add)
-                    junk = stage.tile([P, C], BF16, name="junk", tag="junk")
-                    nc.scalar.activation(out=junk[:], in_=hb[:], func=ACT.Square, accum_out=ss[:, c:c + 1])
-                    hbs.append(hb)
-                live[("hb", g)] = (hbs, ss)
+                h_ps = ps_h.tile([P, C], F32, name="h_ps", tag="h_ps")
+                nc.tensor.matmul_mx(out=h_ps[:], lhsT=xq[:, P * c:P * c + P].bitcast(FP8X4),
+                                    lhsT_scale=xs[:, P * c:P * c + P], rhs=wq[:].bitcast(FP8X4),
+                                    rhs_scale=ws[:], start=True, stop=True)
+                live[("h_ps", g, c)] = h_ps
 
-            def normalise(g):
+            def head_out(g, c):
                 if not ok(g):
                     return
-                hbs, ss = live[("hb", g)]
+                if c == 0:
+                    live[("ss", g)] = small.tile([P, GROUP], F32, name="ss", tag="ss")
+                ss = live[("ss", g)]
+                hb = hbp.tile([P, C], F32, name="hb", tag="hb")
+                nc.vector.tensor_tensor(out=hb[:], in0=live[("h_ps", g, c)][:], in1=b_bc[:], op=ALU.add)
+                junk = stage.tile([P, C], BF16, name="junk", tag="junk")
+                nc.scalar.activation(out=junk[:], in_=hb[:], func=ACT.Square, accum_out=ss[:, c:c + 1])
+                live[("hb", g, c)] = hb
+
+            def rnorm(g):
+                if not ok(g):
+                    return
                 ssm = small.tile([P, GROUP], F32, name="ssm", tag="ssm")
-                nc.gpsimd.tensor_scalar_max(out=ssm[:], in0=ss[:], scalar1=1e-24)
+                nc.gpsimd.tensor_scalar_max(out=ssm[:], in0=live[("ss", g)][:], scalar1=1e-24)
                 rn = small.tile([P, GROUP], F32, name="rn", tag="rn")
                 nc.gpsimd.tensor_tensor(out=rn[:], in0=ssm[:], in1=neg_half[:], op=ALU.pow)
-                hn = stage.tile([P, GROUP * C], BF16, name="hn", tag="hn")
-                for c in range(2 if g == NG - 1 else GROUP):
-                    nc.gpsimd.tensor_scalar(out=hn[:, C * c:C * c + C], in0=hbs[c][:], scalar1=rn[:, c:c + 1],
-                                            scalar2=0.0, op0=ALU.mult, op1=ALU.add)
-                if g == NG - 1:
-                    nc.vector.tensor_scalar(out=hn[:, 2 * C:3 * C], in0=hbs[2][:], scalar1=rn[:, 2:3],
-                                            scalar2=None, op0=ALU.mult)
-                    nc.scalar.activation(out=hn[:, 3 * C:4 * C], in_=hbs[3][:], func=ACT.Copy, scale=rn[:, 3:4])
-                live[("hn", g)] = hn
+                live[("rn", g)] = rn
+                live[("hn", g)] = stage.tile([P, GROUP * C], BF16, name="hn", tag="hn")
+
+            def scale(g, c, eng):
+                if not ok(g):
+                    return
+                dst = live[("hn", g)][:, C * c:C * c + C]
+                hb = live[("hb", g, c)]
+                rn = live[("rn", g)]
+                if eng == "g":
+                    nc.gpsimd.tensor_scalar(out=dst, in0=hb[:], scalar1=rn[:, c:c + 1], scalar2=0.0,
+                                            op0=ALU.mult, op1=ALU.add)
+                elif eng == "v":
+                    nc.vector.tensor_scalar(out=dst, in0=hb[:], scalar1=rn[:, c:c + 1], scalar2=None, op0=ALU.mult)
+                else:
+                    nc.scalar.activation(out=dst, in_=hb[:], func=ACT.Copy, scale=rn[:, c:c + 1])
 
             def h_tp(g, half):
                 if not ok(g):
                     return
+                live[("ht", g, half)] = words_tp(live[("hn", g)], ps_t, "ht", half)
+
+            def h_cp(g, half, on_scalar):
+                if not ok(g):
+                    return
                 if half == 0:
                     live[("hg", g)] = stage.tile([P, GROUP * C], BF16, name="hg", tag="hg", align_bytes=64)
-                hn32 = live[("hn", g)][:].bitcast(F32)
-                hgv = live[("hg", g)][:].bitcast(F32).rearrange("p (c s u) -> p c s u", c=GROUP, u=2)
-                ht = ps_t.tile([P, 2, 2, P], F32, name="ht", tag="ht")
-                for cc in range(2):
-                    for u in range(2):
-                        lo = 256 * (2 * half + cc) + 128 * u
-                        nc.tensor.transpose(ht[:, cc, u, :], hn32[:, lo:lo + 128], ident_f[:])
-                if g == NG - 1 and half == 1:
-                    nc.vector.tensor_copy(out=hgv[:, 2:4, :, :], in_=ht[:].rearrange("p c u s -> p c s u"))
-                else:
-                    nc.scalar.copy(out=hgv[:, 2 * half:2 * half + 2, :, :],
-                                   in_=ht[:].rearrange("p c u s -> p c s u"))
+                words_cp(live[("ht", g, half)], live[("hg", g)], half, on_scalar)
 
             def h_q(g):
                 if not ok(g):
@@ -309,16 +320,21 @@ def tile_spin_pa_t_kernel(tc, x, head_w, head_b, cb_v, cb_g, out):
                 nc.vector.quantize_mx(out=hq[:].bitcast(FP8X4), scales=hs[:], in_=live[("hg", g)][:])
                 live[("hq", g)] = (hq, hs)
 
-            def logits(g):
+            def logits_pe(g):
                 if not ok(g):
                     return
                 hq, hs = live[("hq", g)]
-                v = g // GROUPS
-                j = g % GROUPS
                 z_ps = ps_z.tile([P, W], F32, name="z_ps", tag="z_ps")
                 nc.tensor.matmul_mx(out=z_ps[:], lhsT=cq[:].bitcast(FP8X4), lhsT_scale=cs8[:],
                                     rhs=hq[:].bitcast(FP8X4), rhs_scale=hs[:], start=True, stop=True)
-                nc.vector.tensor_scalar(out=zc[v][:, bank(j)], in0=z_ps[:], scalar1=1.0, scalar2=None,
+                live[("z_ps", g)] = z_ps
+
+            def logits_out(g):
+                if not ok(g):
+                    return
+                v = g // GROUPS
+                j = g % GROUPS
+                nc.vector.tensor_scalar(out=zc[v][:, bank(j)], in0=live[("z_ps", g)][:], scalar1=1.0, scalar2=None,
                                         op0=ALU.mult, op1=ALU.max, accum_out=zmax[v][:, j:j + 1])
 
             w_sb = const.tile([P, GROUP * D], BF16, name="w_sb")
@@ -386,23 +402,37 @@ def tile_spin_pa_t_kernel(tc, x, head_w, head_b, cb_v, cb_g, out):
             cq = const.tile([P, K], U32, name="cq", align_bytes=64)
             cs8 = const.tile([P, K], U8, name="cs8", align_bytes=64)
 
+            for c in range(GROUP - 1):
+                head_pe(0, c)
             for i in range(NG + 3):
-                logits(i - 3)
-                head(i)
-                normalise(i)
+                if i == 2:
+                    codebook_c()
+                logits_out(i - 3)
+                h_cp(i - 2, 0, True)
+                h_cp(i - 2, 1, True)
+                for c in range(ON_VECTOR, GROUP):
+                    scale(i - 1, c, "g")
+                for c in range(GROUP):
+                    if c == GROUP - 1:
+                        head_pe(i, c)
+                    head_out(i, c)
+                rnorm(i)
                 load(i + NX)
-                x_q(i + 1)
-                h_q(i - 2)
                 x_tp(i + 2, 0, True)
-                h_tp(i - 1, 0)
                 x_tp(i + 2, 1, True)
+                h_q(i - 2)
+                logits_pe(i - 2)
+                x_q(i + 1)
+                for c in range(GROUP - 1):
+                    head_pe(i + 1, c)
+                for c in range(ON_VECTOR):
+                    scale(i - 1, c, "v")
+                h_tp(i - 1, 0)
                 h_tp(i - 1, 1)
                 if i == 0:
                     codebook_a()
                 if i == 1:
                     codebook_b()
-                if i == 2:
-                    codebook_c()
                 if i == GROUPS + 2:
                     shift(0)
                 if i >= E_START:

@@ -20,11 +20,21 @@ GROUP = 4
 GROUPS = CHUNKS // GROUP
 NG = VIEWS * GROUPS
 W = GROUP * P
+UNITS = GROUPS // 2
+NU = VIEWS * UNITS
 NX = 4
-REP = 12
+REPS = (1, 12)
 HALF = CHUNKS // 2
 ON_VECTOR = 2
-E_START = 12
+BUDGET = {"a": 2, "b": 0, "c": 3, "d": 1}
+WHEN = (("exp", 0, "a"), ("hi", 0, "d"), ("lo", 1, "d"), ("tp", 2, "d"), ("cp", 3, "a"))
+G_FROM = 2 * UNITS + 4
+P_FROM = 16
+G_SIDE = {"a": 0, "b": 1, "c": 0, "d": 0}
+P_SIDE = {"a": 0, "b": 1, "c": 0, "d": 1}
+FILL0 = 5
+FILL = 2
+G_TAIL = 3
 INV_EPS = 50.0
 INV_T = 10.0
 
@@ -38,166 +48,250 @@ def tile_spin_pa_t_kernel(tc, x, head_w, head_b, cb_v, cb_g, out):
         const = ctx.enter_context(tc.tile_pool(name="const", bufs=1))
         big = ctx.enter_context(tc.tile_pool(name="big", bufs=1))
         small = ctx.enter_context(tc.tile_pool(name="small", bufs=4))
-        ps_x = ctx.enter_context(tc.psum_pool(name="ps_x", bufs=2))
-        ps_h = ctx.enter_context(tc.psum_pool(name="ps_h", bufs=3))
-        ps_t = ctx.enter_context(tc.psum_pool(name="ps_t", bufs=2))
-        ps_z = ctx.enter_context(tc.psum_pool(name="ps_z", bufs=1))
+        ring = ctx.enter_context(tc.psum_pool(name="ring", bufs=7))
+        aux = ctx.enter_context(tc.psum_pool(name="aux", bufs=1))
 
         zc = [big.tile([P, CHUNKS * P], F32, name="zc%d" % v) for v in range(VIEWS)]
         ec = [big.tile([P, CHUNKS * P], F32, name="ec%d" % v) for v in range(VIEWS)]
         ech = [big.tile([P, CHUNKS * P], BF16, name="ech%d" % v) for v in range(VIEWS)]
         ecl = [big.tile([P, CHUNKS * P], BF16, name="ecl%d" % v) for v in range(VIEWS)]
         es = [big.tile([P, CHUNKS, 2, P], BF16, name="es%d" % v) for v in range(VIEWS)]
+        gh = [big.tile([P, CHUNKS * P], BF16, name="gh0")]
+        gl = [big.tile([P, CHUNKS * P], BF16, name="gl0")]
         zmax = [const.tile([P, GROUPS], F32, name="zmax%d" % v) for v in range(VIEWS)]
-        csum = [const.tile([P, GROUPS // 2], F32, name="csum%d" % v) for v in range(VIEWS)]
-        cmax = [const.tile([P, 1], F32, name="cmax%d" % v) for v in range(VIEWS)]
-        nb_e = [const.tile([P, 1], F32, name="nb_e%d" % v) for v in range(VIEWS)]
+        nb_e = [const.tile([P, UNITS], F32, name="nb_e%d" % v) for v in range(VIEWS)]
+        csum = [const.tile([P, UNITS, 1], F32, name="csum%d" % v) for v in range(VIEWS)]
+        fac = [const.tile([P, UNITS, 1], F32, name="fac%d" % v) for v in range(VIEWS)]
+        nb_c = [const.tile([P, 1], F32, name="nb_c%d" % v) for v in range(VIEWS)]
         nb_t = [const.tile([P, 1], F32, name="nb_t%d" % v) for v in range(VIEWS)]
-        gmax = [const.tile([P, 1], F32, name="gmax%d" % v) for v in range(VIEWS)]
+        gmin = [const.tile([P, 1], F32, name="gmin%d" % v) for v in range(VIEWS)]
         mrep = [const.tile([P, P], F32, name="mrep%d" % v) for v in range(VIEWS)]
         sump = [const.tile([P, CHUNKS], F32, name="sump%d" % v) for v in range(VIEWS)]
         lnp = [const.tile([P, CHUNKS], F32, name="lnp%d" % v) for v in range(VIEWS)]
         tq = [const.tile([P, CHUNKS], F32, name="tq%d" % v) for v in range(VIEWS)]
         live = {}
+        split_groups = [0, 0]
+        turned_groups = [0, 0]
 
         def bank(j):
             return slice(W * j, W * j + W)
 
-        def unit(j2):
-            return slice(2 * W * j2, 2 * W * j2 + 2 * W)
+        def unit(j):
+            return slice(2 * W * j, 2 * W * j + 2 * W)
 
-        def shift(v):
-            nc.vector.tensor_reduce(out=cmax[v][:], in_=zmax[v][:], axis=AX.X, op=ALU.max)
-            nc.vector.tensor_scalar(out=nb_e[v][:], in0=cmax[v][:], scalar1=-INV_EPS, scalar2=None, op0=ALU.mult)
+        def unit_shift(v, j):
+            nc.vector.tensor_scalar(out=nb_e[v][:, j:j + 1], in0=zmax[v][:, 2 * j:2 * j + 1],
+                                    scalar1=zmax[v][:, 2 * j + 1:2 * j + 2], scalar2=-INV_EPS, op0=ALU.max, op1=ALU.mult)
 
         def e_exp(v, j):
             nc.scalar.activation(out=ec[v][:, unit(j)], in_=zc[v][:, unit(j)], func=ACT.Exp,
-                                 bias=nb_e[v][:, 0:1], scale=INV_EPS, accum_out=csum[v][:, j:j + 1])
+                                 bias=nb_e[v][:, j:j + 1], scale=INV_EPS, accum_out=csum[v][:, j, :])
 
         def e_hi(v, j):
             nc.vector.tensor_copy(out=ech[v][:, unit(j)], in_=ec[v][:, unit(j)])
 
-        def e_lo(v, j, eng):
-            eng.tensor_tensor(out=ecl[v][:, unit(j)], in0=ec[v][:, unit(j)], in1=ech[v][:, unit(j)],
-                              op=ALU.subtract)
+        def e_lo(v, j):
+            nc.vector.tensor_tensor(out=ecl[v][:, unit(j)], in0=ec[v][:, unit(j)], in1=ech[v][:, unit(j)],
+                                    op=ALU.subtract)
+            split_groups[v] = 2 * j + 2
 
-        def e_tp(v, j):
-            et = ps_h.tile([P, GROUP, 2, P], BF16, name="et", tag="h_ps")
+        def e_tp(v, g):
+            et = ring.tile([P, GROUP, 2, P], BF16, name="et", tag="b")
             for q in range(GROUP):
-                m = GROUP * j + q
+                m = GROUP * g + q
                 nc.tensor.transpose(et[:, q, 0, :], ech[v][:, P * m:P * m + P], ident_b[:])
                 nc.tensor.transpose(et[:, q, 1, :], ecl[v][:, P * m:P * m + P], ident_b[:])
-            live[("et", v, j)] = et
+            live[("et", v, g)] = et
 
-        def e_cp(v, j, on_scalar):
-            dst = es[v][:, GROUP * j:GROUP * j + GROUP, :, :]
-            if on_scalar:
-                nc.scalar.copy(out=dst, in_=live[("et", v, j)][:])
-            else:
-                nc.vector.tensor_copy(out=dst, in_=live[("et", v, j)][:])
+        def e_cp(v, g):
+            nc.scalar.copy(out=es[v][:, GROUP * g:GROUP * g + GROUP, :, :], in_=live[("et", v, g)][:])
+            turned_groups[v] = g + 1
 
-        units = [(v, j) for v in range(VIEWS) for j in range(GROUPS // 2)]
-        nu = len(units)
-        x_done = [0]
-        h_done = [0]
-        b_done = [0]
-        c_done = [0]
+        def factors_a(v):
+            nc.vector.tensor_reduce(out=nb_c[v][:], in_=nb_e[v][:], axis=AX.X, op=ALU.min)
 
-        def e_front(limit):
-            if h_done[0] < x_done[0]:
-                v, j = units[h_done[0]]
-                e_hi(v, j)
-                if v == 0:
-                    e_lo(v, j, nc.vector)
-                else:
-                    for half in range(2):
-                        cols = bank(2 * j + half)
-                        eng = nc.vector if half == 0 else nc.gpsimd
-                        eng.tensor_tensor(out=ecl[v][:, cols], in0=ec[v][:, cols], in1=ech[v][:, cols],
-                                          op=ALU.subtract)
-                h_done[0] = h_done[0] + 1
-            if x_done[0] < limit:
-                e_exp(*units[x_done[0]])
-                x_done[0] = x_done[0] + 1
+        def factors_b(v):
+            nc.scalar.activation(out=fac[v][:, :, 0], in_=nb_e[v][:], func=ACT.Exp, bias=nb_c[v][:, 0:1], scale=-1.0)
 
-        def e_back():
-            if c_done[0] < b_done[0]:
-                v, j = units[c_done[0]]
-                e_cp(v, 2 * j, True)
-                e_cp(v, 2 * j + 1, c_done[0] % 2 == 1)
-                if j == GROUPS // 2 - 1:
-                    c_first(v)
-                c_done[0] = c_done[0] + 1
-            if b_done[0] < h_done[0]:
-                v, j = units[b_done[0]]
-                e_tp(v, 2 * j)
-                e_tp(v, 2 * j + 1)
-                b_done[0] = b_done[0] + 1
-
-        def split_vec(src, cols, name):
-            two = small.tile([P, cols, 2], BF16, name=name, tag=name)
-            nc.vector.tensor_copy(out=two[:, :, 0], in_=src)
-            nc.vector.tensor_tensor(out=two[:, :, 1], in0=src, in1=two[:, :, 0], op=ALU.subtract)
-            return two
-
-        def c_first(v):
+        def c_from(v, sums, cols):
+            t = small.tile([P, UNITS, cols], F32, name="ct", tag="ct%d" % cols)
             ctot = small.tile([P, 1], F32, name="ctot", tag="cr")
-            nc.vector.tensor_reduce(out=ctot[:], in_=csum[v][:], axis=AX.X, op=ALU.add)
+            nc.vector.scalar_tensor_tensor(out=t[:], in0=sums, scalar=1.0, in1=fac[v][:].to_broadcast([P, UNITS, cols]),
+                                           op0=ALU.mult, op1=ALU.mult, accum_out=ctot[:, 0:1])
             cvec = small.tile([P, 1], F32, name="cvec", tag="cvec")
             nc.vector.reciprocal(out=cvec[:], in_=ctot[:])
-            live[("c2", v)] = split_vec(cvec[:], 1, "c2_%d" % v)
+            two = small.tile([P, UNITS, 2], BF16, name="c2_%d" % v, tag="c2_%d" % v)
+            with nc.allow_low_precision(reason="the bf16 part of c fac, and what its rounding leaves"):
+                nc.vector.tensor_scalar(out=two[:, :, 0], in0=fac[v][:, :, 0], scalar1=cvec[:, 0:1], scalar2=None,
+                                        op0=ALU.mult)
+                nc.vector.scalar_tensor_tensor(out=two[:, :, 1], in0=fac[v][:, :, 0], scalar=cvec[:, 0:1],
+                                               in1=two[:, :, 0], op0=ALU.mult, op1=ALU.subtract)
+            live[("c2", v)] = two
 
         def wide(two, rep):
             return two.to_broadcast([P, rep, 2]) if rep > 1 else two
 
-        def pair_matmuls(ps, m0, n, rep, hi, lo, vec2):
-            for m in range(m0, m0 + n):
-                nc.tensor.matmul(out=ps[:, m - m0, :, :], lhsT=hi(m), rhs=wide(vec2[:, 0:1, :], rep),
-                                 start=True, stop=False)
-                nc.tensor.matmul(out=ps[:, m - m0, :, :], lhsT=lo(m), rhs=wide(vec2[:, 0:1, :], rep),
-                                 start=False, stop=True)
-
-        def vec_tile(v, shape, name):
+        def chain_tile(v, shape, name):
             if v == 0:
-                return ps_t.tile(shape, F32, name=name, tag="ht")
-            return ps_h.tile(shape, F32, name=name, tag="h_ps")
+                return aux.tile(shape, F32, name=name + "0", tag="aux")
+            return ring.tile(shape, F32, name=name, tag="b")
 
-        def u_pe(v):
-            for half in range(2):
-                ps = vec_tile(v, [P, HALF, REP, 2], "u_ps")
-                pair_matmuls(ps, HALF * half, HALF, REP, lambda m: ech[v][:, P * m:P * m + P],
-                             lambda m: ecl[v][:, P * m:P * m + P], live[("c2", v)])
-                live[("u_ps", v, half)] = ps
+        def u_block(v, b):
+            per = CHUNKS if v == 0 else HALF
+            if (GROUP * b) % per == 0:
+                live[("u_ps", v, (GROUP * b) // per)] = chain_tile(v, [P, per, REPS[v], 2], "u_ps")
+            ps = live[("u_ps", v, (GROUP * b) // per)]
+            c2 = live[("c2", v)]
+            for m in range(GROUP * b, GROUP * b + GROUP):
+                nc.tensor.matmul(out=ps[:, m % per, :, :], lhsT=ech[v][:, P * m:P * m + P],
+                                 rhs=wide(c2[:, b // 2:b // 2 + 1, :], REPS[v]), start=True, stop=False)
+                nc.tensor.matmul(out=ps[:, m % per, :, :], lhsT=ecl[v][:, P * m:P * m + P],
+                                 rhs=wide(c2[:, b // 2:b // 2 + 1, :], REPS[v]), start=False, stop=True)
 
         def u_ve(v, split):
+            per = CHUNKS if v == 0 else HALF
             r = small.tile([P, CHUNKS], F32, name="r", tag="r")
-            for half in range(2):
-                nc.vector.tensor_reduce(out=r[:, HALF * half:HALF * half + HALF],
-                                        in_=live[("u_ps", v, half)][:, :, 0, :], axis=AX.X, op=ALU.add)
+            for t in range(CHUNKS // per):
+                nc.vector.tensor_reduce(out=r[:, per * t:per * t + per], in_=live[("u_ps", v, t)][:, :, 0, :],
+                                        axis=AX.X, op=ALU.add)
             u = small.tile([P, CHUNKS], F32, name="u", tag="u%d" % v)
             nc.vector.reciprocal(out=u[:], in_=r[:])
             live[("u", v)] = u
             if split:
-                live[("u2", v)] = split_vec(u[:], CHUNKS, "u2_%d" % v)
+                two = small.tile([P, CHUNKS, 2], BF16, name="u2_%d" % v, tag="u2_%d" % v)
+                with nc.allow_low_precision(reason="the bf16 part of u; the lo column takes what the rounding leaves"):
+                    nc.vector.reciprocal(out=two[:, :, 0], in_=r[:])
+                nc.vector.tensor_tensor(out=two[:, :, 1], in0=u[:], in1=two[:, :, 0], op=ALU.subtract)
+                live[("u2", v)] = two
 
-        def c_pe(v):
-            if v == 0:
-                ps = ps_z.tile([P, REP, 2], F32, name="c_ps", tag="z_ps")
-            else:
-                ps = ps_h.tile([P, REP, 2], F32, name="c_ps", tag="h_ps")
+        def c_block(v, b):
+            if b == 0:
+                live[("c_ps", v)] = chain_tile(v, [P, UNITS, REPS[v], 2], "c_ps")
+            ps = live[("c_ps", v)]
             u2 = live[("u2", v)]
-            for m in range(CHUNKS):
-                for h in range(2):
-                    nc.tensor.matmul(out=ps[:], lhsT=es[v][:, m, h, :], rhs=wide(u2[:, m:m + 1, :], REP),
-                                     start=(m == 0 and h == 0), stop=(m == CHUNKS - 1 and h == 1))
-            live[("c_ps", v)] = ps
+            for m in range(GROUP * b, GROUP * b + GROUP):
+                for hl in range(2):
+                    nc.tensor.matmul(out=ps[:, b // 2, :, :], lhsT=es[v][:, m, hl, :],
+                                     rhs=wide(u2[:, m:m + 1, :], REPS[v]),
+                                     start=(m % (2 * GROUP) == 0 and hl == 0),
+                                     stop=(m % (2 * GROUP) == 2 * GROUP - 1 and hl == 1))
 
         def c_ve(v):
-            r = small.tile([P, 1], F32, name="cr", tag="cr")
-            nc.vector.tensor_reduce(out=r[:], in_=live[("c_ps", v)][:, 0, :], axis=AX.X, op=ALU.add)
-            cvec = small.tile([P, 1], F32, name="cvec", tag="cvec")
-            nc.vector.reciprocal(out=cvec[:], in_=r[:])
-            live[("c2", v)] = split_vec(cvec[:], 1, "c2_%d" % v)
+            c_from(v, live[("c_ps", v)][:, :, 0, :], 2)
+
+        def f_block(v, b):
+            if b == 0:
+                live[("f_ps", v)] = chain_tile(v, [P, CHUNKS, 1, 2], "f_ps")
+            ps = live[("f_ps", v)]
+            c2 = live[("c2", v)]
+            for m in range(GROUP * b, GROUP * b + GROUP):
+                nc.tensor.matmul(out=ps[:, m, :, :], lhsT=gh[v][:, P * m:P * m + P], rhs=c2[:, b // 2:b // 2 + 1, :],
+                                 start=True, stop=False)
+                nc.tensor.matmul(out=ps[:, m, :, :], lhsT=gl[v][:, P * m:P * m + P], rhs=c2[:, b // 2:b // 2 + 1, :],
+                                 start=False, stop=True)
+
+        def chain(v):
+            items = []
+            for sweep in range(3):
+                items.extend([("pe", lambda b=b: u_block(v, b), lambda b=b: b < split_groups[v]) for b in range(GROUPS)])
+                items.append(("ve", lambda closing=(sweep == 2): u_ve(v, not closing), lambda: True))
+                if sweep < 2:
+                    items.extend([("pe", lambda b=b: c_block(v, b), lambda b=b: b < turned_groups[v])
+                                  for b in range(GROUPS)])
+                    items.append(("ve", lambda: c_ve(v), lambda: True))
+            return items
+
+        todo = [chain(v) for v in range(VIEWS)]
+        at = [0, 0]
+
+        def advance(v, budget):
+            n = 0
+            while at[v] < len(todo[v]):
+                kind, piece, written = todo[v][at[v]]
+                if kind == "ve" and n > 0:
+                    return
+                if kind == "pe" and n == budget:
+                    return
+                if not written():
+                    return
+                piece()
+                at[v] = at[v] + 1
+                n = n + 1
+                if kind == "ve":
+                    return
+
+        def g_max_a(v):
+            nc.vector.tensor_copy(out=mrep[v][:], in_=nb_c[v][:, 0:1].to_broadcast([P, P]))
+            mt = chain_tile(v, [P, P], "mt")
+            nc.tensor.transpose(mt[:], mrep[v][:], ident_f[:])
+            live[("mt", v)] = mt
+
+        def g_max_b(v):
+            nc.vector.tensor_reduce(out=gmin[v][:], in_=live[("mt", v)][:], axis=AX.X, op=ALU.min)
+            nc.vector.tensor_scalar(out=nb_t[v][:], in0=gmin[v][:], scalar1=INV_T / INV_EPS, scalar2=None, op0=ALU.mult)
+
+        def p_tp(v, g):
+            tp = ring.tile([P, GROUP, P], F32, name="tp", tag="b")
+            for q in range(GROUP):
+                m = GROUP * g + q
+                nc.tensor.transpose(tp[:, q, :], zc[v][:, P * m:P * m + P], ident_f[:])
+            live[("tp", v, g)] = tp
+
+        def p_exp(v, g):
+            for q in reversed(range(GROUP)):
+                pj = small.tile([P, P], BF16, name="pj", tag="pj")
+                nc.scalar.activation(out=pj[:], in_=live[("tp", v, g)][:, q, :], func=ACT.Exp, bias=nb_t[v][:, 0:1],
+                                     scale=INV_T, accum_out=sump[v][:, GROUP * g + q:GROUP * g + q + 1])
+
+        def g_mul(v, j):
+            nc.vector.tensor_tensor(out=ec[v][:, unit(j)], in0=ec[v][:, unit(j)], in1=zc[1 - v][:, unit(j)],
+                                    op=ALU.mult)
+
+        def g_hi(v, j):
+            nc.scalar.copy(out=gh[v][:, unit(j)], in_=ec[v][:, unit(j)])
+
+        def g_lo(v, j):
+            nc.vector.tensor_tensor(out=gl[v][:, unit(j)], in0=ec[v][:, unit(j)], in1=gh[v][:, unit(j)],
+                                    op=ALU.subtract)
+
+        units = [(v, j) for v in range(VIEWS) for j in range(UNITS)]
+
+        g_items = []
+        for k in range(NU + 2):
+            if k < NU:
+                g_items.append(("v", g_mul, k))
+            if 0 <= k - 1 < NU:
+                g_items.append(("s", g_hi, k - 1))
+            if 0 <= k - 2 < NU:
+                g_items.append(("v", g_lo, k - 2))
+
+        def p_step(k):
+            if k < NG:
+                p_tp(k // GROUPS, k % GROUPS)
+            if 0 <= k - 1 < NG:
+                p_exp((k - 1) // GROUPS, (k - 1) % GROUPS)
+
+        g_at = [0]
+        g_split = [0]
+        p_at = [0]
+
+        def g_work(n, limit):
+            while g_at[0] < len(g_items):
+                eng, piece, k = g_items[g_at[0]]
+                if k >= limit or (eng == "v" and n == 0):
+                    return
+                piece(*units[k])
+                if piece == g_lo:
+                    g_split[0] = k + 1
+                g_at[0] = g_at[0] + 1
+                if eng == "v":
+                    n = n - 1
+
+        def p_work(n, limit):
+            for q in range(n):
+                if p_at[0] < min(limit, NG + 1):
+                    p_step(p_at[0])
+                    p_at[0] = p_at[0] + 1
 
         with ExitStack() as early:
             xin = early.enter_context(tc.tile_pool(name="xin", bufs=NX))
@@ -218,9 +312,9 @@ def tile_spin_pa_t_kernel(tc, x, head_w, head_b, cb_v, cb_g, out):
                                   in_=x_views[g // GROUPS][:, GROUP * j:GROUP * j + GROUP, :])
                 live[("x", g)] = x_sb
 
-            def words_tp(src, pool, tag, half):
+            def words_tp(src, half):
                 src32 = src[:].bitcast(F32)
-                xt = pool.tile([P, 2, 2, P], F32, name=tag, tag=tag)
+                xt = ring.tile([P, 2, 2, P], F32, name="wt", tag="b")
                 for cc in range(2):
                     for u in range(2):
                         lo = 256 * (2 * half + cc) + 128 * u
@@ -237,7 +331,7 @@ def tile_spin_pa_t_kernel(tc, x, head_w, head_b, cb_v, cb_g, out):
                     nc.vector.tensor_copy(out=dst, in_=srcv)
 
             def k_to_partitions(src, grouped, half, on_scalar):
-                words_cp(words_tp(src, ps_x, "xt", half), grouped, half, on_scalar)
+                words_cp(words_tp(src, half), grouped, half, on_scalar)
 
             def x_tp(g, half, on_scalar):
                 if not ok(g):
@@ -258,7 +352,7 @@ def tile_spin_pa_t_kernel(tc, x, head_w, head_b, cb_v, cb_g, out):
                 if not ok(g):
                     return
                 xq, xs = live[("xq", g)]
-                h_ps = ps_h.tile([P, C], F32, name="h_ps", tag="h_ps")
+                h_ps = ring.tile([P, C], F32, name="h_ps", tag="b")
                 nc.tensor.matmul_mx(out=h_ps[:], lhsT=xq[:, P * c:P * c + P].bitcast(FP8X4),
                                     lhsT_scale=xs[:, P * c:P * c + P], rhs=wq[:].bitcast(FP8X4),
                                     rhs_scale=ws[:], start=True, stop=True)
@@ -295,15 +389,13 @@ def tile_spin_pa_t_kernel(tc, x, head_w, head_b, cb_v, cb_g, out):
                 if eng == "g":
                     nc.gpsimd.tensor_scalar(out=dst, in0=hb[:], scalar1=rn[:, c:c + 1], scalar2=0.0,
                                             op0=ALU.mult, op1=ALU.add)
-                elif eng == "v":
-                    nc.vector.tensor_scalar(out=dst, in0=hb[:], scalar1=rn[:, c:c + 1], scalar2=None, op0=ALU.mult)
                 else:
-                    nc.scalar.activation(out=dst, in_=hb[:], func=ACT.Copy, scale=rn[:, c:c + 1])
+                    nc.vector.tensor_scalar(out=dst, in0=hb[:], scalar1=rn[:, c:c + 1], scalar2=None, op0=ALU.mult)
 
             def h_tp(g, half):
                 if not ok(g):
                     return
-                live[("ht", g, half)] = words_tp(live[("hn", g)], ps_t, "ht", half)
+                live[("ht", g, half)] = words_tp(live[("hn", g)], half)
 
             def h_cp(g, half, on_scalar):
                 if not ok(g):
@@ -324,7 +416,7 @@ def tile_spin_pa_t_kernel(tc, x, head_w, head_b, cb_v, cb_g, out):
                 if not ok(g):
                     return
                 hq, hs = live[("hq", g)]
-                z_ps = ps_z.tile([P, W], F32, name="z_ps", tag="z_ps")
+                z_ps = ring.tile([P, W], F32, name="z_ps", tag="b")
                 nc.tensor.matmul_mx(out=z_ps[:], lhsT=cq[:].bitcast(FP8X4), lhsT_scale=cs8[:],
                                     rhs=hq[:].bitcast(FP8X4), rhs_scale=hs[:], start=True, stop=True)
                 live[("z_ps", g)] = z_ps
@@ -337,7 +429,13 @@ def tile_spin_pa_t_kernel(tc, x, head_w, head_b, cb_v, cb_g, out):
                 nc.vector.tensor_scalar(out=zc[v][:, bank(j)], in0=live[("z_ps", g)][:], scalar1=1.0, scalar2=None,
                                         op0=ALU.mult, op1=ALU.max, accum_out=zmax[v][:, j:j + 1])
 
-            w_sb = const.tile([P, GROUP * D], BF16, name="w_sb")
+            def shifts(g):
+                if ok(g) and g % 2 == 1:
+                    unit_shift(g // GROUPS, (g % GROUPS) // 2)
+                    if g % GROUPS == GROUPS - 1:
+                        factors_a(g // GROUPS)
+
+            w_sb = stage.tile([P, GROUP * D], BF16, name="w_sb", tag="hn")
             w_rows = head_w.rearrange("(c p) k -> p c k", p=P)
             x0_sb = xin.tile([P, GROUP * D], BF16, name="x_sb", tag="x_sb")
             live[("x", 0)] = x0_sb
@@ -363,7 +461,7 @@ def tile_spin_pa_t_kernel(tc, x, head_w, head_b, cb_v, cb_g, out):
             neg_half = const.tile([P, GROUP], F32, name="neg_half")
             nc.vector.memset(neg_half[:], -0.5)
 
-            wgr = const.tile([P, GROUP * D], BF16, name="wgr", align_bytes=64)
+            wgr = stage.tile([P, GROUP * D], BF16, name="wgr", tag="hg", align_bytes=64)
             k_to_partitions(w_sb, wgr, 0, False)
             x_tp(0, 0, True)
             k_to_partitions(w_sb, wgr, 1, False)
@@ -387,7 +485,7 @@ def tile_spin_pa_t_kernel(tc, x, head_w, head_b, cb_v, cb_g, out):
                 wsc = const.tile([P, 1], F32, name="wsc")
                 nc.vector.tensor_tensor(out=wsc[:], in0=vrn[:], in1=g_sb[:], op=ALU.mult)
                 nc.vector.tensor_scalar(out=w_bf[:], in0=v_sb[:], scalar1=wsc[:, 0:1], scalar2=None, op0=ALU.mult)
-                wt = ps_t.tile([P, 2, P], F32, name="wt", tag="ht")
+                wt = aux.tile([P, 2, P], F32, name="cbt", tag="aux")
                 for u in range(2):
                     nc.tensor.transpose(wt[:, u, :], w_bf[:].bitcast(F32)[:, 128 * u:128 * u + 128], ident_f[:])
                 live["wt"] = wt
@@ -402,14 +500,51 @@ def tile_spin_pa_t_kernel(tc, x, head_w, head_b, cb_v, cb_g, out):
             cq = const.tile([P, K], U32, name="cq", align_bytes=64)
             cs8 = const.tile([P, K], U8, name="cs8", align_bytes=64)
 
+            def unit_at(i, rounds_later):
+                n, odd = divmod(i - 4 - rounds_later, 2)
+                return n if (odd == 0 and 0 <= n < NU - 1) else None
+
+            def stop(i, where):
+                for what, rounds_later, place in WHEN:
+                    n = unit_at(i, rounds_later)
+                    if n is None or place != where:
+                        continue
+                    v, j = units[n]
+                    if what == "exp":
+                        e_exp(v, j)
+                        if j == UNITS - 1:
+                            factors_b(v)
+                    if what == "hi":
+                        e_hi(v, j)
+                        if j == UNITS - 1:
+                            c_from(v, csum[v][:], 1)
+                            g_max_a(v)
+                    if what == "lo":
+                        e_lo(v, j)
+                    if what == "tp":
+                        e_tp(v, 2 * j)
+                        e_tp(v, 2 * j + 1)
+                    if what == "cp":
+                        e_cp(v, 2 * j)
+                        e_cp(v, 2 * j + 1)
+                if i == 2 * UNITS + 3 and where == "a":
+                    g_max_b(0)
+                if i > 2 * UNITS + 2:
+                    advance(0, BUDGET[where])
+                if i >= P_FROM:
+                    g_work(G_SIDE[where], (i - G_FROM) // 2 + 1)
+                    p_work(P_SIDE[where], GROUPS)
+
             for c in range(GROUP - 1):
                 head_pe(0, c)
-            for i in range(NG + 3):
+            for i in range(NG + 2):
                 if i == 2:
                     codebook_c()
                 logits_out(i - 3)
+                shifts(i - 3)
                 h_cp(i - 2, 0, True)
                 h_cp(i - 2, 1, True)
+                stop(i, "a")
                 for c in range(ON_VECTOR, GROUP):
                     scale(i - 1, c, "g")
                 for c in range(GROUP):
@@ -418,8 +553,10 @@ def tile_spin_pa_t_kernel(tc, x, head_w, head_b, cb_v, cb_g, out):
                     head_out(i, c)
                 rnorm(i)
                 load(i + NX)
+                stop(i, "b")
                 x_tp(i + 2, 0, True)
                 x_tp(i + 2, 1, True)
+                stop(i, "c")
                 h_q(i - 2)
                 logits_pe(i - 2)
                 x_q(i + 1)
@@ -429,156 +566,75 @@ def tile_spin_pa_t_kernel(tc, x, head_w, head_b, cb_v, cb_g, out):
                     scale(i - 1, c, "v")
                 h_tp(i - 1, 0)
                 h_tp(i - 1, 1)
+                stop(i, "d")
                 if i == 0:
                     codebook_a()
                 if i == 1:
                     codebook_b()
-                if i == GROUPS + 2:
-                    shift(0)
-                if i >= E_START:
-                    e_front(GROUPS // 2)
-                if i >= NG:
-                    e_back()
-                    e_back()
+            logits_out(NG - 1)
+            shifts(NG - 1)
 
         late = ctx.enter_context(tc.tile_pool(name="late", bufs=1))
-        pp = ctx.enter_context(tc.tile_pool(name="pp", bufs=3))
-        gh = [late.tile([P, CHUNKS * P], BF16, name="gh%d" % v) for v in range(VIEWS)]
-        gl = [late.tile([P, CHUNKS * P], BF16, name="gl%d" % v) for v in range(VIEWS)]
+        gh.append(late.tile([P, CHUNKS * P], BF16, name="gh1"))
+        gl.append(late.tile([P, CHUNKS * P], BF16, name="gl1"))
+        f_at = [0]
 
-        def g_max_a(v):
-            nc.vector.tensor_copy(out=mrep[v][:], in_=cmax[v][:, 0:1].to_broadcast([P, P]))
-            if v == 0:
-                mt = ps_z.tile([P, P], F32, name="mt", tag="z_ps")
-            else:
-                mt = ps_x.tile([P, P], F32, name="mt", tag="xt")
-            nc.tensor.transpose(mt[:], mrep[v][:], ident_f[:])
-            live[("mt", v)] = mt
-
-        def g_max_b(v):
-            nc.vector.tensor_reduce(out=gmax[v][:], in_=live[("mt", v)][:], axis=AX.X, op=ALU.max)
-            nc.vector.tensor_scalar(out=nb_t[v][:], in0=gmax[v][:], scalar1=-INV_T, scalar2=None, op0=ALU.mult)
-
-        def p_exp(v, j):
-            pt = pp.tile([P, 2 * W], F32, name="pt", tag="pt")
-            nc.scalar.activation(out=pt[:], in_=zc[v][:, unit(j)], func=ACT.Exp, bias=nb_t[v][:, 0:1], scale=INV_T)
-            live[("pt", v, j)] = pt
-
-        def p_tp(v, j):
-            tp = ps_x.tile([P, GROUP, P], F32, name="tp", tag="xt")
-            pt = live[("pt", v, j // 2)]
-            for q in range(GROUP):
-                lo = W * (j % 2) + P * q
-                nc.tensor.transpose(tp[:, q, :], pt[:, lo:lo + P], ident_f[:])
-            live[("tp", v, j)] = tp
-
-        def p_sum(v, j):
-            nc.vector.tensor_reduce(out=sump[v][:, GROUP * j:GROUP * j + GROUP], in_=live[("tp", v, j)][:],
-                                    axis=AX.X, op=ALU.add)
-
-        def g_mul(v, j):
-            nc.vector.tensor_tensor(out=ec[v][:, unit(j)], in0=ec[v][:, unit(j)], in1=zc[1 - v][:, unit(j)],
-                                    op=ALU.mult)
-
-        def g_hi(v, j):
-            nc.scalar.copy(out=gh[v][:, unit(j)], in_=ec[v][:, unit(j)])
-
-        def g_lo(v, j, eng):
-            eng.tensor_tensor(out=gl[v][:, unit(j)], in0=ec[v][:, unit(j)], in1=gh[v][:, unit(j)], op=ALU.subtract)
-
-        side = []
-
-        def p_step(k):
-            if k < nu:
-                p_exp(*units[k])
-            for half in range(2):
-                if 0 <= k - 2 < nu:
-                    p_sum(units[k - 2][0], 2 * units[k - 2][1] + half)
-                if 0 <= k - 1 < nu:
-                    p_tp(units[k - 1][0], 2 * units[k - 1][1] + half)
-
-        def g_step(k):
-            if k < nu:
-                g_mul(*units[k])
-            if 0 <= k - 1 < nu:
-                g_hi(*units[k - 1])
-            if 0 <= k - 2 < nu:
-                g_lo(units[k - 2][0], units[k - 2][1], nc.vector if (k - 2) % 2 == 0 else nc.gpsimd)
-
-        for k in range(nu + 2):
-            side.append((g_step, k))
-            side.append((p_step, k))
-        done = [0]
-
-        def side_work(n):
+        def fill(n):
+            if at[0] < len(todo[0]):
+                advance(0, n)
+                return
             for q in range(n):
-                if done[0] < len(side):
-                    f, k = side[done[0]]
-                    f(k)
-                    done[0] = done[0] + 1
+                if f_at[0] < min(GROUPS, 2 * g_split[0]):
+                    f_block(0, f_at[0])
+                    f_at[0] = f_at[0] + 1
 
-        def f_pe(v):
-            f_ps = vec_tile(v, [P, CHUNKS, 1, 2], "f_ps")
-            pair_matmuls(f_ps, 0, CHUNKS, 1, lambda m: gh[v][:, P * m:P * m + P],
-                         lambda m: gl[v][:, P * m:P * m + P], live[("c2", v)])
-            live[("f_ps", v)] = f_ps
-
-        STEP = 2
-        shift(1)
-        for v in range(VIEWS):
-            g_max_a(v)
-        e_front(nu)
-        u_pe(0)
-        e_front(nu)
-        e_back()
-        for v in range(VIEWS):
-            g_max_b(v)
-        u_ve(0, True)
-        e_front(nu)
-        e_back()
-        c_pe(0)
-        e_front(nu)
-        e_back()
-        c_ve(0)
-        e_front(nu)
-        e_back()
-        e_back()
-        e_back()
-        u_pe(1)
-        u_pe(0)
-        side_work(STEP)
-        u_ve(1, True)
-        u_ve(0, True)
-        side_work(STEP)
-        c_pe(1)
-        c_pe(0)
-        side_work(STEP)
-        c_ve(1)
-        c_ve(0)
-        side_work(STEP)
-        u_pe(1)
-        u_pe(0)
-        side_work(STEP)
-        u_ve(1, True)
-        u_ve(0, False)
-        side_work(STEP)
-        c_pe(1)
-        side_work(STEP)
-        f_pe(0)
-        c_ve(1)
-        side_work(len(side))
-        u_pe(1)
-        f_pe(1)
-        u_ve(1, False)
+        last = UNITS - 1
+        e_exp(1, last)
+        factors_b(1)
+        c_from(1, csum[1][:], 1)
+        e_hi(1, last)
+        e_lo(1, last)
+        e_tp(1, 2 * last - 2)
+        e_tp(1, 2 * last - 1)
+        e_cp(1, 2 * last - 2)
+        e_cp(1, 2 * last - 1)
+        fill(FILL0)
+        for sweep in range(5):
+            advance(1, 4)
+            p_work(1, NG + 1)
+            advance(1, 4)
+            if sweep == 0:
+                e_tp(1, 2 * last)
+                e_tp(1, 2 * last + 1)
+                e_cp(1, 2 * last)
+                e_cp(1, 2 * last + 1)
+                g_max_a(1)
+            else:
+                fill(FILL)
+                p_work(1, NG + 1)
+            advance(1, 1)
+            if sweep == 0:
+                g_max_b(1)
+            g_work(G_TAIL, NU)
+        g_work(len(g_items), NU)
+        for b in range(GROUPS):
+            f_block(1, b)
+            if b % 2 == 1:
+                p_work(1, NG + 1)
+        p_work(NG + 1, NG + 1)
+        for q in range(6):
+            fill(GROUPS)
+        assert at[0] == len(todo[0]) and at[1] == len(todo[1]) and f_at[0] == GROUPS
+        assert g_at[0] == len(g_items) and p_at[0] == NG + 1
 
         for v in range(VIEWS):
             nc.scalar.activation(out=lnp[v][:], in_=sump[v][:], func=ACT.Ln)
         lsum = const.tile([P, CHUNKS], F32, name="lsum")
         nc.vector.tensor_tensor(out=lsum[:], in0=lnp[0][:], in1=lnp[1][:], op=ALU.add)
         msum = const.tile([P, 1], F32, name="msum")
-        nc.vector.tensor_tensor(out=msum[:], in0=gmax[0][:], in1=gmax[1][:], op=ALU.add)
+        nc.vector.tensor_tensor(out=msum[:], in0=nb_t[0][:], in1=nb_t[1][:], op=ALU.add)
         msc = const.tile([P, 1], F32, name="msc")
-        nc.vector.tensor_scalar(out=msc[:], in0=msum[:], scalar1=0.5 * INV_T, scalar2=None, op0=ALU.mult)
+        nc.vector.tensor_scalar(out=msc[:], in0=msum[:], scalar1=-0.5, scalar2=None, op0=ALU.mult)
         part = const.tile([P, CHUNKS], F32, name="part")
         nc.vector.tensor_scalar(out=part[:], in0=lsum[:], scalar1=0.5, scalar2=msc[:, 0:1],
                                 op0=ALU.mult, op1=ALU.add)

@@ -25,16 +25,18 @@ NU = VIEWS * UNITS
 NX = 4
 REPS = (1, 12)
 HALF = CHUNKS // 2
+ON_GPSIMD = (True, False)
 ON_VECTOR = 2
 BUDGET = {"a": 2, "b": 0, "c": 3, "d": 1}
-WHEN = (("exp", 0, "a"), ("hi", 0, "d"), ("lo", 1, "d"), ("tp", 2, "d"), ("cp", 3, "a"))
+WHEN = (("hi", 0, "d"), ("lo", 1, "d"), ("tp", 2, "d"), ("cp", 3, "a"))
 G_FROM = 2 * UNITS + 4
 P_FROM = 16
 G_SIDE = {"a": 0, "b": 1, "c": 0, "d": 0}
 P_SIDE = {"a": 0, "b": 1, "c": 0, "d": 1}
 FILL0 = 5
 FILL = 2
-G_TAIL = 3
+G_TAIL = (3, 3, 3, 3, 3)
+P_GAP = 2
 INV_EPS = 50.0
 INV_T = 10.0
 
@@ -58,10 +60,9 @@ def tile_spin_pa_t_kernel(tc, x, head_w, head_b, cb_v, cb_g, out):
         es = [big.tile([P, CHUNKS, 2, P], BF16, name="es%d" % v) for v in range(VIEWS)]
         gh = [big.tile([P, CHUNKS * P], BF16, name="gh0")]
         gl = [big.tile([P, CHUNKS * P], BF16, name="gl0")]
-        zmax = [const.tile([P, GROUPS], F32, name="zmax%d" % v) for v in range(VIEWS)]
-        nb_e = [const.tile([P, UNITS], F32, name="nb_e%d" % v) for v in range(VIEWS)]
-        csum = [const.tile([P, UNITS, 1], F32, name="csum%d" % v) for v in range(VIEWS)]
-        fac = [const.tile([P, UNITS, 1], F32, name="fac%d" % v) for v in range(VIEWS)]
+        nb_e = [const.tile([P, GROUPS], F32, name="nb_e%d" % v) for v in range(VIEWS)]
+        csum = [const.tile([P, GROUPS, 1], F32, name="csum%d" % v) for v in range(VIEWS)]
+        fac = [const.tile([P, GROUPS, 1], F32, name="fac%d" % v) for v in range(VIEWS)]
         nb_c = [const.tile([P, 1], F32, name="nb_c%d" % v) for v in range(VIEWS)]
         nb_t = [const.tile([P, 1], F32, name="nb_t%d" % v) for v in range(VIEWS)]
         gmin = [const.tile([P, 1], F32, name="gmin%d" % v) for v in range(VIEWS)]
@@ -69,6 +70,7 @@ def tile_spin_pa_t_kernel(tc, x, head_w, head_b, cb_v, cb_g, out):
         sump = [const.tile([P, CHUNKS], F32, name="sump%d" % v) for v in range(VIEWS)]
         lnp = [const.tile([P, CHUNKS], F32, name="lnp%d" % v) for v in range(VIEWS)]
         tq = [const.tile([P, CHUNKS], F32, name="tq%d" % v) for v in range(VIEWS)]
+        neg_one = const.tile([P, CHUNKS], F32, name="neg_one")
         live = {}
         split_groups = [0, 0]
         turned_groups = [0, 0]
@@ -79,13 +81,9 @@ def tile_spin_pa_t_kernel(tc, x, head_w, head_b, cb_v, cb_g, out):
         def unit(j):
             return slice(2 * W * j, 2 * W * j + 2 * W)
 
-        def unit_shift(v, j):
-            nc.vector.tensor_scalar(out=nb_e[v][:, j:j + 1], in0=zmax[v][:, 2 * j:2 * j + 1],
-                                    scalar1=zmax[v][:, 2 * j + 1:2 * j + 2], scalar2=-INV_EPS, op0=ALU.max, op1=ALU.mult)
-
-        def e_exp(v, j):
-            nc.scalar.activation(out=ec[v][:, unit(j)], in_=zc[v][:, unit(j)], func=ACT.Exp,
-                                 bias=nb_e[v][:, j:j + 1], scale=INV_EPS, accum_out=csum[v][:, j, :])
+        def e_exp(v, g):
+            nc.scalar.activation(out=ec[v][:, bank(g)], in_=zc[v][:, bank(g)], func=ACT.Exp,
+                                 bias=nb_e[v][:, g:g + 1], scale=-1.0, accum_out=csum[v][:, g, :])
 
         def e_hi(v, j):
             nc.vector.tensor_copy(out=ech[v][:, unit(j)], in_=ec[v][:, unit(j)])
@@ -114,18 +112,26 @@ def tile_spin_pa_t_kernel(tc, x, head_w, head_b, cb_v, cb_g, out):
             nc.scalar.activation(out=fac[v][:, :, 0], in_=nb_e[v][:], func=ACT.Exp, bias=nb_c[v][:, 0:1], scale=-1.0)
 
         def c_from(v, sums, cols):
-            t = small.tile([P, UNITS, cols], F32, name="ct", tag="ct%d" % cols)
+            t = small.tile([P, GROUPS, cols], F32, name="ct", tag="ct%d" % cols)
             ctot = small.tile([P, 1], F32, name="ctot", tag="cr")
-            nc.vector.scalar_tensor_tensor(out=t[:], in0=sums, scalar=1.0, in1=fac[v][:].to_broadcast([P, UNITS, cols]),
+            nc.vector.scalar_tensor_tensor(out=t[:], in0=sums, scalar=1.0, in1=fac[v][:].to_broadcast([P, GROUPS, cols]),
                                            op0=ALU.mult, op1=ALU.mult, accum_out=ctot[:, 0:1])
             cvec = small.tile([P, 1], F32, name="cvec", tag="cvec")
-            nc.vector.reciprocal(out=cvec[:], in_=ctot[:])
-            two = small.tile([P, UNITS, 2], BF16, name="c2_%d" % v, tag="c2_%d" % v)
-            with nc.allow_low_precision(reason="the bf16 part of c fac, and what its rounding leaves"):
-                nc.vector.tensor_scalar(out=two[:, :, 0], in0=fac[v][:, :, 0], scalar1=cvec[:, 0:1], scalar2=None,
-                                        op0=ALU.mult)
-                nc.vector.scalar_tensor_tensor(out=two[:, :, 1], in0=fac[v][:, :, 0], scalar=cvec[:, 0:1],
-                                               in1=two[:, :, 0], op0=ALU.mult, op1=ALU.subtract)
+            two = small.tile([P, GROUPS, 2], BF16, name="c2_%d" % v, tag="c2_%d" % v)
+            if ON_GPSIMD[v]:
+                nc.gpsimd.tensor_tensor(out=cvec[:], in0=ctot[:], in1=neg_one[:, 0:1], op=ALU.pow)
+                cf = small.tile([P, GROUPS], F32, name="cf", tag="cf")
+                nc.gpsimd.tensor_scalar(out=cf[:], in0=fac[v][:, :, 0], scalar1=cvec[:, 0:1], scalar2=0.0,
+                                        op0=ALU.mult, op1=ALU.add)
+                nc.gpsimd.tensor_copy(out=two[:, :, 0], in_=cf[:])
+                nc.gpsimd.tensor_tensor(out=two[:, :, 1], in0=cf[:], in1=two[:, :, 0], op=ALU.subtract)
+            else:
+                nc.vector.reciprocal(out=cvec[:], in_=ctot[:])
+                with nc.allow_low_precision(reason="the bf16 part of c fac, and what its rounding leaves"):
+                    nc.vector.tensor_scalar(out=two[:, :, 0], in0=fac[v][:, :, 0], scalar1=cvec[:, 0:1], scalar2=None,
+                                            op0=ALU.mult)
+                    nc.vector.scalar_tensor_tensor(out=two[:, :, 1], in0=fac[v][:, :, 0], scalar=cvec[:, 0:1],
+                                                   in1=two[:, :, 0], op0=ALU.mult, op1=ALU.subtract)
             live[("c2", v)] = two
 
         def wide(two, rep):
@@ -144,9 +150,9 @@ def tile_spin_pa_t_kernel(tc, x, head_w, head_b, cb_v, cb_g, out):
             c2 = live[("c2", v)]
             for m in range(GROUP * b, GROUP * b + GROUP):
                 nc.tensor.matmul(out=ps[:, m % per, :, :], lhsT=ech[v][:, P * m:P * m + P],
-                                 rhs=wide(c2[:, b // 2:b // 2 + 1, :], REPS[v]), start=True, stop=False)
+                                 rhs=wide(c2[:, b:b + 1, :], REPS[v]), start=True, stop=False)
                 nc.tensor.matmul(out=ps[:, m % per, :, :], lhsT=ecl[v][:, P * m:P * m + P],
-                                 rhs=wide(c2[:, b // 2:b // 2 + 1, :], REPS[v]), start=False, stop=True)
+                                 rhs=wide(c2[:, b:b + 1, :], REPS[v]), start=False, stop=True)
 
         def u_ve(v, split):
             per = CHUNKS if v == 0 else HALF
@@ -155,26 +161,31 @@ def tile_spin_pa_t_kernel(tc, x, head_w, head_b, cb_v, cb_g, out):
                 nc.vector.tensor_reduce(out=r[:, per * t:per * t + per], in_=live[("u_ps", v, t)][:, :, 0, :],
                                         axis=AX.X, op=ALU.add)
             u = small.tile([P, CHUNKS], F32, name="u", tag="u%d" % v)
-            nc.vector.reciprocal(out=u[:], in_=r[:])
             live[("u", v)] = u
-            if split:
-                two = small.tile([P, CHUNKS, 2], BF16, name="u2_%d" % v, tag="u2_%d" % v)
-                with nc.allow_low_precision(reason="the bf16 part of u; the lo column takes what the rounding leaves"):
-                    nc.vector.reciprocal(out=two[:, :, 0], in_=r[:])
-                nc.vector.tensor_tensor(out=two[:, :, 1], in0=u[:], in1=two[:, :, 0], op=ALU.subtract)
-                live[("u2", v)] = two
+            two = small.tile([P, CHUNKS, 2], BF16, name="u2_%d" % v, tag="u2_%d" % v)
+            live[("u2", v)] = two
+            if ON_GPSIMD[v]:
+                nc.gpsimd.tensor_tensor(out=u[:], in0=r[:], in1=neg_one[:], op=ALU.pow)
+                if split:
+                    nc.gpsimd.tensor_copy(out=two[:, :, 0], in_=u[:])
+                    nc.gpsimd.tensor_tensor(out=two[:, :, 1], in0=u[:], in1=two[:, :, 0], op=ALU.subtract)
+            else:
+                nc.vector.reciprocal(out=u[:], in_=r[:])
+                if split:
+                    with nc.allow_low_precision(reason="the bf16 part of u; the lo column takes what the rounding leaves"):
+                        nc.vector.reciprocal(out=two[:, :, 0], in_=r[:])
+                    nc.vector.tensor_tensor(out=two[:, :, 1], in0=u[:], in1=two[:, :, 0], op=ALU.subtract)
 
         def c_block(v, b):
             if b == 0:
-                live[("c_ps", v)] = chain_tile(v, [P, UNITS, REPS[v], 2], "c_ps")
+                live[("c_ps", v)] = chain_tile(v, [P, GROUPS, REPS[v], 2], "c_ps")
             ps = live[("c_ps", v)]
             u2 = live[("u2", v)]
             for m in range(GROUP * b, GROUP * b + GROUP):
                 for hl in range(2):
-                    nc.tensor.matmul(out=ps[:, b // 2, :, :], lhsT=es[v][:, m, hl, :],
+                    nc.tensor.matmul(out=ps[:, b, :, :], lhsT=es[v][:, m, hl, :],
                                      rhs=wide(u2[:, m:m + 1, :], REPS[v]),
-                                     start=(m % (2 * GROUP) == 0 and hl == 0),
-                                     stop=(m % (2 * GROUP) == 2 * GROUP - 1 and hl == 1))
+                                     start=(m % GROUP == 0 and hl == 0), stop=(m % GROUP == GROUP - 1 and hl == 1))
 
         def c_ve(v):
             c_from(v, live[("c_ps", v)][:, :, 0, :], 2)
@@ -185,9 +196,9 @@ def tile_spin_pa_t_kernel(tc, x, head_w, head_b, cb_v, cb_g, out):
             ps = live[("f_ps", v)]
             c2 = live[("c2", v)]
             for m in range(GROUP * b, GROUP * b + GROUP):
-                nc.tensor.matmul(out=ps[:, m, :, :], lhsT=gh[v][:, P * m:P * m + P], rhs=c2[:, b // 2:b // 2 + 1, :],
+                nc.tensor.matmul(out=ps[:, m, :, :], lhsT=gh[v][:, P * m:P * m + P], rhs=c2[:, b:b + 1, :],
                                  start=True, stop=False)
-                nc.tensor.matmul(out=ps[:, m, :, :], lhsT=gl[v][:, P * m:P * m + P], rhs=c2[:, b // 2:b // 2 + 1, :],
+                nc.tensor.matmul(out=ps[:, m, :, :], lhsT=gl[v][:, P * m:P * m + P], rhs=c2[:, b:b + 1, :],
                                  start=False, stop=True)
 
         def chain(v):
@@ -241,7 +252,7 @@ def tile_spin_pa_t_kernel(tc, x, head_w, head_b, cb_v, cb_g, out):
             for q in reversed(range(GROUP)):
                 pj = small.tile([P, P], BF16, name="pj", tag="pj")
                 nc.scalar.activation(out=pj[:], in_=live[("tp", v, g)][:, q, :], func=ACT.Exp, bias=nb_t[v][:, 0:1],
-                                     scale=INV_T, accum_out=sump[v][:, GROUP * g + q:GROUP * g + q + 1])
+                                     scale=-INV_T / INV_EPS, accum_out=sump[v][:, GROUP * g + q:GROUP * g + q + 1])
 
         def g_mul(v, j):
             nc.vector.tensor_tensor(out=ec[v][:, unit(j)], in0=ec[v][:, unit(j)], in1=zc[1 - v][:, unit(j)],
@@ -266,10 +277,8 @@ def tile_spin_pa_t_kernel(tc, x, head_w, head_b, cb_v, cb_g, out):
                 g_items.append(("v", g_lo, k - 2))
 
         def p_step(k):
-            if k < NG:
-                p_tp(k // GROUPS, k % GROUPS)
-            if 0 <= k - 1 < NG:
-                p_exp((k - 1) // GROUPS, (k - 1) % GROUPS)
+            p_tp(k // GROUPS, k % GROUPS)
+            p_exp(k // GROUPS, k % GROUPS)
 
         g_at = [0]
         g_split = [0]
@@ -289,7 +298,7 @@ def tile_spin_pa_t_kernel(tc, x, head_w, head_b, cb_v, cb_g, out):
 
         def p_work(n, limit):
             for q in range(n):
-                if p_at[0] < min(limit, NG + 1):
+                if p_at[0] < min(limit, NG):
                     p_step(p_at[0])
                     p_at[0] = p_at[0] + 1
 
@@ -374,7 +383,7 @@ def tile_spin_pa_t_kernel(tc, x, head_w, head_b, cb_v, cb_g, out):
                 if not ok(g):
                     return
                 ssm = small.tile([P, GROUP], F32, name="ssm", tag="ssm")
-                nc.gpsimd.tensor_scalar_max(out=ssm[:], in0=live[("ss", g)][:], scalar1=1e-24)
+                nc.vector.tensor_scalar_max(out=ssm[:], in0=live[("ss", g)][:], scalar1=1e-24)
                 rn = small.tile([P, GROUP], F32, name="rn", tag="rn")
                 nc.gpsimd.tensor_tensor(out=rn[:], in0=ssm[:], in1=neg_half[:], op=ALU.pow)
                 live[("rn", g)] = rn
@@ -426,14 +435,10 @@ def tile_spin_pa_t_kernel(tc, x, head_w, head_b, cb_v, cb_g, out):
                     return
                 v = g // GROUPS
                 j = g % GROUPS
-                nc.vector.tensor_scalar(out=zc[v][:, bank(j)], in0=live[("z_ps", g)][:], scalar1=1.0, scalar2=None,
-                                        op0=ALU.mult, op1=ALU.max, accum_out=zmax[v][:, j:j + 1])
-
-            def shifts(g):
-                if ok(g) and g % 2 == 1:
-                    unit_shift(g // GROUPS, (g % GROUPS) // 2)
-                    if g % GROUPS == GROUPS - 1:
-                        factors_a(g // GROUPS)
+                nc.vector.tensor_scalar(out=zc[v][:, bank(j)], in0=live[("z_ps", g)][:], scalar1=-INV_EPS, scalar2=None,
+                                        op0=ALU.mult, op1=ALU.min, accum_out=nb_e[v][:, j:j + 1])
+                if j == GROUPS - 1:
+                    factors_a(v)
 
             w_sb = stage.tile([P, GROUP * D], BF16, name="w_sb", tag="hn")
             w_rows = head_w.rearrange("(c p) k -> p c k", p=P)
@@ -460,6 +465,7 @@ def tile_spin_pa_t_kernel(tc, x, head_w, head_b, cb_v, cb_g, out):
             make_identity(nc, ident_b[:])
             neg_half = const.tile([P, GROUP], F32, name="neg_half")
             nc.vector.memset(neg_half[:], -0.5)
+            nc.vector.memset(neg_one[:], -1.0)
 
             wgr = stage.tile([P, GROUP * D], BF16, name="wgr", tag="hg", align_bytes=64)
             k_to_partitions(w_sb, wgr, 0, False)
@@ -505,15 +511,15 @@ def tile_spin_pa_t_kernel(tc, x, head_w, head_b, cb_v, cb_g, out):
                 return n if (odd == 0 and 0 <= n < NU - 1) else None
 
             def stop(i, where):
+                if where == "a" and 0 <= i - 3 < NG - 1:
+                    e_exp((i - 3) // GROUPS, (i - 3) % GROUPS)
+                    if (i - 3) % GROUPS == GROUPS - 1:
+                        factors_b((i - 3) // GROUPS)
                 for what, rounds_later, place in WHEN:
                     n = unit_at(i, rounds_later)
                     if n is None or place != where:
                         continue
                     v, j = units[n]
-                    if what == "exp":
-                        e_exp(v, j)
-                        if j == UNITS - 1:
-                            factors_b(v)
                     if what == "hi":
                         e_hi(v, j)
                         if j == UNITS - 1:
@@ -533,25 +539,22 @@ def tile_spin_pa_t_kernel(tc, x, head_w, head_b, cb_v, cb_g, out):
                     advance(0, BUDGET[where])
                 if i >= P_FROM:
                     g_work(G_SIDE[where], (i - G_FROM) // 2 + 1)
-                    p_work(P_SIDE[where], GROUPS)
+                    if i < NG + 1 or where != "d":
+                        p_work(P_SIDE[where], GROUPS)
 
-            for c in range(GROUP - 1):
+            for c in range(GROUP):
                 head_pe(0, c)
             for i in range(NG + 2):
                 if i == 2:
                     codebook_c()
                 logits_out(i - 3)
-                shifts(i - 3)
                 h_cp(i - 2, 0, True)
                 h_cp(i - 2, 1, True)
                 stop(i, "a")
                 for c in range(ON_VECTOR, GROUP):
                     scale(i - 1, c, "g")
                 for c in range(GROUP):
-                    if c == GROUP - 1:
-                        head_pe(i, c)
                     head_out(i, c)
-                rnorm(i)
                 load(i + NX)
                 stop(i, "b")
                 x_tp(i + 2, 0, True)
@@ -560,19 +563,19 @@ def tile_spin_pa_t_kernel(tc, x, head_w, head_b, cb_v, cb_g, out):
                 h_q(i - 2)
                 logits_pe(i - 2)
                 x_q(i + 1)
-                for c in range(GROUP - 1):
+                for c in range(GROUP):
                     head_pe(i + 1, c)
                 for c in range(ON_VECTOR):
                     scale(i - 1, c, "v")
                 h_tp(i - 1, 0)
                 h_tp(i - 1, 1)
                 stop(i, "d")
+                rnorm(i)
                 if i == 0:
                     codebook_a()
                 if i == 1:
                     codebook_b()
             logits_out(NG - 1)
-            shifts(NG - 1)
 
         late = ctx.enter_context(tc.tile_pool(name="late", bufs=1))
         gh.append(late.tile([P, CHUNKS * P], BF16, name="gh1"))
@@ -588,8 +591,34 @@ def tile_spin_pa_t_kernel(tc, x, head_w, head_b, cb_v, cb_g, out):
                     f_block(0, f_at[0])
                     f_at[0] = f_at[0] + 1
 
+        def loss_logs():
+            for v in range(VIEWS):
+                nc.scalar.activation(out=lnp[v][:], in_=sump[v][:], func=ACT.Ln)
+            lsum = const.tile([P, CHUNKS], F32, name="lsum")
+            nc.vector.tensor_tensor(out=lsum[:], in0=lnp[0][:], in1=lnp[1][:], op=ALU.add)
+            msum = const.tile([P, 1], F32, name="msum")
+            nc.vector.tensor_tensor(out=msum[:], in0=nb_t[0][:], in1=nb_t[1][:], op=ALU.add)
+            msc = const.tile([P, 1], F32, name="msc")
+            nc.vector.tensor_scalar(out=msc[:], in0=msum[:], scalar1=-0.5, scalar2=None, op0=ALU.mult)
+            part = const.tile([P, CHUNKS], F32, name="part")
+            nc.vector.tensor_scalar(out=part[:], in0=lsum[:], scalar1=0.5, scalar2=msc[:, 0:1],
+                                    op0=ALU.mult, op1=ALU.add)
+            live["res"] = part
+
+        def loss_view(v):
+            fsum = small.tile([P, CHUNKS], F32, name="fsum", tag="r")
+            nc.vector.tensor_reduce(out=fsum[:], in_=live[("f_ps", v)][:, :, 0, :], axis=AX.X, op=ALU.add)
+            nc.vector.tensor_tensor(out=tq[v][:], in0=fsum[:], in1=live[("u", v)][:], op=ALU.mult)
+            res = const.tile([P, CHUNKS], F32, name="res%d" % v)
+            nc.vector.scalar_tensor_tensor(out=res[:], in0=tq[v][:], scalar=0.5 * INV_T / INV_EPS, in1=live["res"][:],
+                                           op0=ALU.mult, op1=ALU.add)
+            live["res"] = res
+
+        def loss_tail():
+            loss_view(1)
+
         last = UNITS - 1
-        e_exp(1, last)
+        e_exp(1, GROUPS - 1)
         factors_b(1)
         c_from(1, csum[1][:], 1)
         e_hi(1, last)
@@ -599,10 +628,9 @@ def tile_spin_pa_t_kernel(tc, x, head_w, head_b, cb_v, cb_g, out):
         e_cp(1, 2 * last - 2)
         e_cp(1, 2 * last - 1)
         fill(FILL0)
+        p_work(GROUPS, GROUPS)
         for sweep in range(5):
-            advance(1, 4)
-            p_work(1, NG + 1)
-            advance(1, 4)
+            advance(1, GROUPS)
             if sweep == 0:
                 e_tp(1, 2 * last)
                 e_tp(1, 2 * last + 1)
@@ -611,40 +639,21 @@ def tile_spin_pa_t_kernel(tc, x, head_w, head_b, cb_v, cb_g, out):
                 g_max_a(1)
             else:
                 fill(FILL)
-                p_work(1, NG + 1)
+                p_work(P_GAP, NG)
             advance(1, 1)
             if sweep == 0:
                 g_max_b(1)
-            g_work(G_TAIL, NU)
+            g_work(G_TAIL[sweep], NU)
+        p_work(NG, NG)
+        loss_logs()
         g_work(len(g_items), NU)
-        for b in range(GROUPS):
-            f_block(1, b)
-            if b % 2 == 1:
-                p_work(1, NG + 1)
-        p_work(NG + 1, NG + 1)
         for q in range(6):
             fill(GROUPS)
+        for b in range(GROUPS):
+            f_block(1, b)
+        loss_view(0)
         assert at[0] == len(todo[0]) and at[1] == len(todo[1]) and f_at[0] == GROUPS
-        assert g_at[0] == len(g_items) and p_at[0] == NG + 1
+        assert g_at[0] == len(g_items) and p_at[0] == NG
 
-        for v in range(VIEWS):
-            nc.scalar.activation(out=lnp[v][:], in_=sump[v][:], func=ACT.Ln)
-        lsum = const.tile([P, CHUNKS], F32, name="lsum")
-        nc.vector.tensor_tensor(out=lsum[:], in0=lnp[0][:], in1=lnp[1][:], op=ALU.add)
-        msum = const.tile([P, 1], F32, name="msum")
-        nc.vector.tensor_tensor(out=msum[:], in0=nb_t[0][:], in1=nb_t[1][:], op=ALU.add)
-        msc = const.tile([P, 1], F32, name="msc")
-        nc.vector.tensor_scalar(out=msc[:], in0=msum[:], scalar1=-0.5, scalar2=None, op0=ALU.mult)
-        part = const.tile([P, CHUNKS], F32, name="part")
-        nc.vector.tensor_scalar(out=part[:], in0=lsum[:], scalar1=0.5, scalar2=msc[:, 0:1],
-                                op0=ALU.mult, op1=ALU.add)
-        for v in range(VIEWS):
-            fsum = small.tile([P, CHUNKS], F32, name="fsum", tag="r")
-            nc.vector.tensor_reduce(out=fsum[:], in_=live[("f_ps", v)][:, :, 0, :], axis=AX.X, op=ALU.add)
-            nc.vector.tensor_tensor(out=tq[v][:], in0=fsum[:], in1=live[("u", v)][:], op=ALU.mult)
-        tsum = const.tile([P, CHUNKS], F32, name="tsum")
-        nc.vector.tensor_tensor(out=tsum[:], in0=tq[0][:], in1=tq[1][:], op=ALU.add)
-        res = const.tile([P, CHUNKS], F32, name="res")
-        nc.vector.scalar_tensor_tensor(out=res[:], in0=tsum[:], scalar=-0.5 * INV_T, in1=part[:],
-                                       op0=ALU.mult, op1=ALU.add)
-        nc.sync.dma_start(out=out.rearrange("(p m) -> p m", m=CHUNKS), in_=res[:])
+        loss_tail()
+        nc.sync.dma_start(out=out.rearrange("(p m) -> p m", m=CHUNKS), in_=live["res"][:])

@@ -25,7 +25,7 @@ NU = VIEWS * UNITS
 NX = 4
 REPS = (1, 12)
 HALF = CHUNKS // 2
-ON_GPSIMD = (True, False)
+ON_GPSIMD = (False, False)
 ON_VECTOR = 2
 BUDGET = {"a": 2, "b": 0, "c": 3, "d": 1}
 WHEN = (("hi", 0, "d"), ("lo", 1, "d"), ("tp", 2, "d"), ("cp", 3, "a"))

@@ -25,9 +25,8 @@ NU = VIEWS * UNITS
 NX = 4
 REPS = (1, 12)
 HALF = CHUNKS // 2
-ON_GPSIMD = (False, False)
 ON_VECTOR = 2
-BUDGET = {"a": 2, "b": 0, "c": 3, "d": 1}
+BUDGET = {"a": 2, "b": 1, "c": 3, "d": 2}
 WHEN = (("hi", 0, "d"), ("lo", 1, "d"), ("tp", 2, "d"), ("cp", 3, "a"))
 G_FROM = 2 * UNITS + 4
 P_FROM = 16
@@ -70,7 +69,6 @@ def tile_spin_pa_t_kernel(tc, x, head_w, head_b, cb_v, cb_g, out):
         sump = [const.tile([P, CHUNKS], F32, name="sump%d" % v) for v in range(VIEWS)]
         lnp = [const.tile([P, CHUNKS], F32, name="lnp%d" % v) for v in range(VIEWS)]
         tq = [const.tile([P, CHUNKS], F32, name="tq%d" % v) for v in range(VIEWS)]
-        neg_one = const.tile([P, CHUNKS], F32, name="neg_one")
         live = {}
         split_groups = [0, 0]
         turned_groups = [0, 0]
@@ -114,25 +112,29 @@ def tile_spin_pa_t_kernel(tc, x, head_w, head_b, cb_v, cb_g, out):
         def c_from(v, sums, cols):
             t = small.tile([P, GROUPS, cols], F32, name="ct", tag="ct%d" % cols)
             ctot = small.tile([P, 1], F32, name="ctot", tag="cr")
-            nc.vector.scalar_tensor_tensor(out=t[:], in0=sums, scalar=1.0, in1=fac[v][:].to_broadcast([P, GROUPS, cols]),
-                                           op0=ALU.mult, op1=ALU.mult, accum_out=ctot[:, 0:1])
             cvec = small.tile([P, 1], F32, name="cvec", tag="cvec")
             two = small.tile([P, GROUPS, 2], BF16, name="c2_%d" % v, tag="c2_%d" % v)
-            if ON_GPSIMD[v]:
-                nc.gpsimd.tensor_tensor(out=cvec[:], in0=ctot[:], in1=neg_one[:, 0:1], op=ALU.pow)
-                cf = small.tile([P, GROUPS], F32, name="cf", tag="cf")
-                nc.gpsimd.tensor_scalar(out=cf[:], in0=fac[v][:, :, 0], scalar1=cvec[:, 0:1], scalar2=0.0,
-                                        op0=ALU.mult, op1=ALU.add)
-                nc.gpsimd.tensor_copy(out=two[:, :, 0], in_=cf[:])
-                nc.gpsimd.tensor_tensor(out=two[:, :, 1], in0=cf[:], in1=two[:, :, 0], op=ALU.subtract)
-            else:
+            live[("c2", v)] = two
+
+            def total():
+                nc.vector.scalar_tensor_tensor(out=t[:], in0=sums, scalar=1.0,
+                                               in1=fac[v][:].to_broadcast([P, GROUPS, cols]),
+                                               op0=ALU.mult, op1=ALU.mult, accum_out=ctot[:, 0:1])
+
+            def invert():
                 nc.vector.reciprocal(out=cvec[:], in_=ctot[:])
-                with nc.allow_low_precision(reason="the bf16 part of c fac, and what its rounding leaves"):
+
+            def hi_part():
+                with nc.allow_low_precision(reason="the bf16 part of c fac"):
                     nc.vector.tensor_scalar(out=two[:, :, 0], in0=fac[v][:, :, 0], scalar1=cvec[:, 0:1], scalar2=None,
                                             op0=ALU.mult)
+
+            def lo_part():
+                with nc.allow_low_precision(reason="what the rounding of c fac to bf16 leaves"):
                     nc.vector.scalar_tensor_tensor(out=two[:, :, 1], in0=fac[v][:, :, 0], scalar=cvec[:, 0:1],
                                                    in1=two[:, :, 0], op0=ALU.mult, op1=ALU.subtract)
-            live[("c2", v)] = two
+
+            return [total, invert, hi_part, lo_part]
 
         def wide(two, rep):
             return two.to_broadcast([P, rep, 2]) if rep > 1 else two
@@ -157,24 +159,27 @@ def tile_spin_pa_t_kernel(tc, x, head_w, head_b, cb_v, cb_g, out):
         def u_ve(v, split):
             per = CHUNKS if v == 0 else HALF
             r = small.tile([P, CHUNKS], F32, name="r", tag="r")
-            for t in range(CHUNKS // per):
-                nc.vector.tensor_reduce(out=r[:, per * t:per * t + per], in_=live[("u_ps", v, t)][:, :, 0, :],
-                                        axis=AX.X, op=ALU.add)
             u = small.tile([P, CHUNKS], F32, name="u", tag="u%d" % v)
             live[("u", v)] = u
             two = small.tile([P, CHUNKS, 2], BF16, name="u2_%d" % v, tag="u2_%d" % v)
             live[("u2", v)] = two
-            if ON_GPSIMD[v]:
-                nc.gpsimd.tensor_tensor(out=u[:], in0=r[:], in1=neg_one[:], op=ALU.pow)
-                if split:
-                    nc.gpsimd.tensor_copy(out=two[:, :, 0], in_=u[:])
-                    nc.gpsimd.tensor_tensor(out=two[:, :, 1], in0=u[:], in1=two[:, :, 0], op=ALU.subtract)
-            else:
+
+            def total(t):
+                nc.vector.tensor_reduce(out=r[:, per * t:per * t + per], in_=live[("u_ps", v, t)][:, :, 0, :],
+                                        axis=AX.X, op=ALU.add)
+
+            def invert():
                 nc.vector.reciprocal(out=u[:], in_=r[:])
-                if split:
-                    with nc.allow_low_precision(reason="the bf16 part of u; the lo column takes what the rounding leaves"):
-                        nc.vector.reciprocal(out=two[:, :, 0], in_=r[:])
-                    nc.vector.tensor_tensor(out=two[:, :, 1], in0=u[:], in1=two[:, :, 0], op=ALU.subtract)
+
+            def hi_part():
+                with nc.allow_low_precision(reason="the bf16 part of u"):
+                    nc.vector.reciprocal(out=two[:, :, 0], in_=r[:])
+
+            def lo_part():
+                nc.vector.tensor_tensor(out=two[:, :, 1], in0=u[:], in1=two[:, :, 0], op=ALU.subtract)
+
+            ops = [lambda t=t: total(t) for t in range(CHUNKS // per)]
+            return ops + ([invert, hi_part, lo_part] if split else [invert])
 
         def c_block(v, b):
             if b == 0:
@@ -188,7 +193,7 @@ def tile_spin_pa_t_kernel(tc, x, head_w, head_b, cb_v, cb_g, out):
                                      start=(m % GROUP == 0 and hl == 0), stop=(m % GROUP == GROUP - 1 and hl == 1))
 
         def c_ve(v):
-            c_from(v, live[("c_ps", v)][:, :, 0, :], 2)
+            return c_from(v, live[("c_ps", v)][:, :, 0, :], 2)
 
         def f_block(v, b):
             if b == 0:
@@ -214,10 +219,26 @@ def tile_spin_pa_t_kernel(tc, x, head_w, head_b, cb_v, cb_g, out):
 
         todo = [chain(v) for v in range(VIEWS)]
         at = [0, 0]
+        pending = []
+        dripped = [0]
+        in_rounds = [True]
+
+        def drip():
+            if dripped[0] < len(pending):
+                pending[dripped[0]]()
+                dripped[0] = dripped[0] + 1
+
+        def small_ops(v, ops):
+            if v == 0 and in_rounds[0]:
+                pending.extend(ops)
+                drip()
+            else:
+                for op in ops:
+                    op()
 
         def advance(v, budget):
             n = 0
-            while at[v] < len(todo[v]):
+            while at[v] < len(todo[v]) and (v == 1 or dripped[0] == len(pending)):
                 kind, piece, written = todo[v][at[v]]
                 if kind == "ve" and n > 0:
                     return
@@ -225,7 +246,10 @@ def tile_spin_pa_t_kernel(tc, x, head_w, head_b, cb_v, cb_g, out):
                     return
                 if not written():
                     return
-                piece()
+                if kind == "ve":
+                    small_ops(v, piece())
+                else:
+                    piece()
                 at[v] = at[v] + 1
                 n = n + 1
                 if kind == "ve":
@@ -355,6 +379,7 @@ def tile_spin_pa_t_kernel(tc, x, head_w, head_b, cb_v, cb_g, out):
                 xq = stage.tile([P, W], U32, name="xq", tag="xq", align_bytes=64)
                 xs = stage.tile([P, W], U8, name="xs", tag="xs", align_bytes=64)
                 nc.vector.quantize_mx(out=xq[:].bitcast(FP8X4), scales=xs[:], in_=live[("xg", g)][:])
+                drip()
                 live[("xq", g)] = (xq, xs)
 
             def head_pe(g, c):
@@ -375,6 +400,7 @@ def tile_spin_pa_t_kernel(tc, x, head_w, head_b, cb_v, cb_g, out):
                 ss = live[("ss", g)]
                 hb = hbp.tile([P, C], F32, name="hb", tag="hb")
                 nc.vector.tensor_tensor(out=hb[:], in0=live[("h_ps", g, c)][:], in1=b_bc[:], op=ALU.add)
+                drip()
                 junk = stage.tile([P, C], BF16, name="junk", tag="junk")
                 nc.scalar.activation(out=junk[:], in_=hb[:], func=ACT.Square, accum_out=ss[:, c:c + 1])
                 live[("hb", g, c)] = hb
@@ -400,6 +426,7 @@ def tile_spin_pa_t_kernel(tc, x, head_w, head_b, cb_v, cb_g, out):
                                             op0=ALU.mult, op1=ALU.add)
                 else:
                     nc.vector.tensor_scalar(out=dst, in0=hb[:], scalar1=rn[:, c:c + 1], scalar2=None, op0=ALU.mult)
+                    drip()
 
             def h_tp(g, half):
                 if not ok(g):
@@ -419,6 +446,7 @@ def tile_spin_pa_t_kernel(tc, x, head_w, head_b, cb_v, cb_g, out):
                 hq = stage.tile([P, W], U32, name="hq", tag="hq", align_bytes=64)
                 hs = stage.tile([P, W], U8, name="hs", tag="hs", align_bytes=64)
                 nc.vector.quantize_mx(out=hq[:].bitcast(FP8X4), scales=hs[:], in_=live[("hg", g)][:])
+                drip()
                 live[("hq", g)] = (hq, hs)
 
             def logits_pe(g):
@@ -437,6 +465,7 @@ def tile_spin_pa_t_kernel(tc, x, head_w, head_b, cb_v, cb_g, out):
                 j = g % GROUPS
                 nc.vector.tensor_scalar(out=zc[v][:, bank(j)], in0=live[("z_ps", g)][:], scalar1=-INV_EPS, scalar2=None,
                                         op0=ALU.mult, op1=ALU.min, accum_out=nb_e[v][:, j:j + 1])
+                drip()
                 if j == GROUPS - 1:
                     factors_a(v)
 
@@ -465,7 +494,6 @@ def tile_spin_pa_t_kernel(tc, x, head_w, head_b, cb_v, cb_g, out):
             make_identity(nc, ident_b[:])
             neg_half = const.tile([P, GROUP], F32, name="neg_half")
             nc.vector.memset(neg_half[:], -0.5)
-            nc.vector.memset(neg_one[:], -1.0)
 
             wgr = stage.tile([P, GROUP * D], BF16, name="wgr", tag="hg", align_bytes=64)
             k_to_partitions(w_sb, wgr, 0, False)
@@ -523,7 +551,7 @@ def tile_spin_pa_t_kernel(tc, x, head_w, head_b, cb_v, cb_g, out):
                     if what == "hi":
                         e_hi(v, j)
                         if j == UNITS - 1:
-                            c_from(v, csum[v][:], 1)
+                            small_ops(v, c_from(v, csum[v][:], 1))
                             g_max_a(v)
                     if what == "lo":
                         e_lo(v, j)
@@ -576,6 +604,7 @@ def tile_spin_pa_t_kernel(tc, x, head_w, head_b, cb_v, cb_g, out):
                 if i == 1:
                     codebook_b()
             logits_out(NG - 1)
+            in_rounds[0] = False
 
         late = ctx.enter_context(tc.tile_pool(name="late", bufs=1))
         gh.append(late.tile([P, CHUNKS * P], BF16, name="gh1"))
@@ -620,13 +649,15 @@ def tile_spin_pa_t_kernel(tc, x, head_w, head_b, cb_v, cb_g, out):
         last = UNITS - 1
         e_exp(1, GROUPS - 1)
         factors_b(1)
-        c_from(1, csum[1][:], 1)
+        small_ops(1, c_from(1, csum[1][:], 1))
         e_hi(1, last)
         e_lo(1, last)
         e_tp(1, 2 * last - 2)
         e_tp(1, 2 * last - 1)
         e_cp(1, 2 * last - 2)
         e_cp(1, 2 * last - 1)
+        while dripped[0] < len(pending):
+            drip()
         fill(FILL0)
         p_work(GROUPS, GROUPS)
         for sweep in range(5):

@@ -588,15 +588,15 @@ def tile_spin_pa_t_kernel(tc, x, head_w, head_b, cb_v, cb_g, out):
                 x_tp(i + 2, 0, True)
                 x_tp(i + 2, 1, True)
                 stop(i, "c")
+                for c in range(ON_VECTOR):
+                    scale(i - 1, c, "v")
+                h_tp(i - 1, 0)
+                h_tp(i - 1, 1)
                 h_q(i - 2)
                 logits_pe(i - 2)
                 x_q(i + 1)
                 for c in range(GROUP):
                     head_pe(i + 1, c)
-                for c in range(ON_VECTOR):
-                    scale(i - 1, c, "v")
-                h_tp(i - 1, 0)
-                h_tp(i - 1, 1)
                 stop(i, "d")
                 rnorm(i)
                 if i == 0:

@@ -23,7 +23,7 @@ W = GROUP * P
 UNITS = GROUPS // 2
 NU = VIEWS * UNITS
 NX = 4
-REPS = (1, 12)
+REPS = (8, 12)
 HALF = CHUNKS // 2
 ON_VECTOR = 2
 BUDGET = {"a": 2, "b": 1, "c": 3, "d": 2}

from contextlib import ExitStack

import concourse.mybir as mybir
from concourse.masks import make_identity

F32 = mybir.dt.float32
BF16 = mybir.dt.bfloat16
U32 = mybir.dt.uint32
U8 = mybir.dt.uint8
FP8X4 = mybir.dt.float8_e4m3fn_x4
ALU = mybir.AluOpType
ACT = mybir.ActivationFunctionType
AX = mybir.AxisListType

P = 128
N2, D, C, K = 8192, 512, 512, 128
VIEWS = 2
CHUNKS = 32
GROUP = 4
GROUPS = CHUNKS // GROUP
NG = VIEWS * GROUPS
W = GROUP * P
UNITS = GROUPS // 2
NU = VIEWS * UNITS
NX = 4
REPS = (8, 12)
HALF = CHUNKS // 2
ON_VECTOR = 2
BUDGET = {"a": 2, "b": 1, "c": 3, "d": 2}
WHEN = (("hi", 0, "d"), ("lo", 1, "d"), ("tp", 2, "d"), ("cp", 3, "a"))
G_FROM = 2 * UNITS + 4
P_FROM = 16
G_SIDE = {"a": 0, "b": 1, "c": 0, "d": 0}
P_SIDE = {"a": 0, "b": 1, "c": 0, "d": 1}
FILL0 = 5
FILL = 2
G_TAIL = (3, 3, 3, 3, 3)
P_GAP = 2
INV_EPS = 50.0
INV_T = 10.0

FLOPS = 2 * N2 * D * C + 2 * N2 * C * K


def tile_spin_pa_t_kernel(tc, x, head_w, head_b, cb_v, cb_g, out):
    nc = tc.nc
    with ExitStack() as ctx:
        ctx.enter_context(tc.manual_schedule())
        const = ctx.enter_context(tc.tile_pool(name="const", bufs=1))
        big = ctx.enter_context(tc.tile_pool(name="big", bufs=1))
        small = ctx.enter_context(tc.tile_pool(name="small", bufs=4))
        ring = ctx.enter_context(tc.psum_pool(name="ring", bufs=7))
        aux = ctx.enter_context(tc.psum_pool(name="aux", bufs=1))

        zc = [big.tile([P, CHUNKS * P], F32, name="zc%d" % v) for v in range(VIEWS)]
        ec = [big.tile([P, CHUNKS * P], F32, name="ec%d" % v) for v in range(VIEWS)]
        ech = [big.tile([P, CHUNKS * P], BF16, name="ech%d" % v) for v in range(VIEWS)]
        ecl = [big.tile([P, CHUNKS * P], BF16, name="ecl%d" % v) for v in range(VIEWS)]
        es = [big.tile([P, CHUNKS, 2, P], BF16, name="es%d" % v) for v in range(VIEWS)]
        gh = [big.tile([P, CHUNKS * P], BF16, name="gh0")]
        gl = [big.tile([P, CHUNKS * P], BF16, name="gl0")]
        nb_e = [const.tile([P, GROUPS], F32, name="nb_e%d" % v) for v in range(VIEWS)]
        csum = [const.tile([P, GROUPS, 1], F32, name="csum%d" % v) for v in range(VIEWS)]
        fac = [const.tile([P, GROUPS, 1], F32, name="fac%d" % v) for v in range(VIEWS)]
        nb_c = [const.tile([P, 1], F32, name="nb_c%d" % v) for v in range(VIEWS)]
        nb_t = [const.tile([P, 1], F32, name="nb_t%d" % v) for v in range(VIEWS)]
        gmin = [const.tile([P, 1], F32, name="gmin%d" % v) for v in range(VIEWS)]
        mrep = [const.tile([P, P], F32, name="mrep%d" % v) for v in range(VIEWS)]
        sump = [const.tile([P, CHUNKS], F32, name="sump%d" % v) for v in range(VIEWS)]
        lnp = [const.tile([P, CHUNKS], F32, name="lnp%d" % v) for v in range(VIEWS)]
        tq = [const.tile([P, CHUNKS], F32, name="tq%d" % v) for v in range(VIEWS)]
        live = {}
        split_groups = [0, 0]
        turned_groups = [0, 0]

        def bank(j):
            return slice(W * j, W * j + W)

        def unit(j):
            return slice(2 * W * j, 2 * W * j + 2 * W)

        def e_exp(v, g):
            nc.scalar.activation(out=ec[v][:, bank(g)], in_=zc[v][:, bank(g)], func=ACT.Exp,
                                 bias=nb_e[v][:, g:g + 1], scale=-1.0, accum_out=csum[v][:, g, :])

        def e_hi(v, j):
            nc.vector.tensor_copy(out=ech[v][:, unit(j)], in_=ec[v][:, unit(j)])

        def e_lo(v, j):
            nc.vector.tensor_tensor(out=ecl[v][:, unit(j)], in0=ec[v][:, unit(j)], in1=ech[v][:, unit(j)],
                                    op=ALU.subtract)
            split_groups[v] = 2 * j + 2

        def e_tp(v, g):
            et = ring.tile([P, GROUP, 2, P], BF16, name="et", tag="b")
            for q in range(GROUP):
                m = GROUP * g + q
                nc.tensor.transpose(et[:, q, 0, :], ech[v][:, P * m:P * m + P], ident_b[:])
                nc.tensor.transpose(et[:, q, 1, :], ecl[v][:, P * m:P * m + P], ident_b[:])
            live[("et", v, g)] = et

        def e_cp(v, g):
            nc.scalar.copy(out=es[v][:, GROUP * g:GROUP * g + GROUP, :, :], in_=live[("et", v, g)][:])
            turned_groups[v] = g + 1

        def factors_a(v):
            nc.vector.tensor_reduce(out=nb_c[v][:], in_=nb_e[v][:], axis=AX.X, op=ALU.min)

        def factors_b(v):
            nc.scalar.activation(out=fac[v][:, :, 0], in_=nb_e[v][:], func=ACT.Exp, bias=nb_c[v][:, 0:1], scale=-1.0)

        def c_from(v, sums, cols):
            t = small.tile([P, GROUPS, cols], F32, name="ct", tag="ct%d" % cols)
            ctot = small.tile([P, 1], F32, name="ctot", tag="cr")
            cvec = small.tile([P, 1], F32, name="cvec", tag="cvec")
            two = small.tile([P, GROUPS, 2], BF16, name="c2_%d" % v, tag="c2_%d" % v)
            live[("c2", v)] = two

            def total():
                nc.vector.scalar_tensor_tensor(out=t[:], in0=sums, scalar=1.0,
                                               in1=fac[v][:].to_broadcast([P, GROUPS, cols]),
                                               op0=ALU.mult, op1=ALU.mult, accum_out=ctot[:, 0:1])

            def invert():
                nc.vector.reciprocal(out=cvec[:], in_=ctot[:])

            def hi_part():
                with nc.allow_low_precision(reason="the bf16 part of c fac"):
                    nc.vector.tensor_scalar(out=two[:, :, 0], in0=fac[v][:, :, 0], scalar1=cvec[:, 0:1], scalar2=None,
                                            op0=ALU.mult)

            def lo_part():
                with nc.allow_low_precision(reason="what the rounding of c fac to bf16 leaves"):
                    nc.vector.scalar_tensor_tensor(out=two[:, :, 1], in0=fac[v][:, :, 0], scalar=cvec[:, 0:1],
                                                   in1=two[:, :, 0], op0=ALU.mult, op1=ALU.subtract)

            return [total, invert, hi_part, lo_part]

        def wide(two, rep):
            return two.to_broadcast([P, rep, 2]) if rep > 1 else two

        def chain_tile(v, shape, name):
            if v == 0:
                return aux.tile(shape, F32, name=name + "0", tag="aux")
            return ring.tile(shape, F32, name=name, tag="b")

        def u_block(v, b):
            per = CHUNKS if v == 0 else HALF
            if (GROUP * b) % per == 0:
                live[("u_ps", v, (GROUP * b) // per)] = chain_tile(v, [P, per, REPS[v], 2], "u_ps")
            ps = live[("u_ps", v, (GROUP * b) // per)]
            c2 = live[("c2", v)]
            for m in range(GROUP * b, GROUP * b + GROUP):
                nc.tensor.matmul(out=ps[:, m % per, :, :], lhsT=ech[v][:, P * m:P * m + P],
                                 rhs=wide(c2[:, b:b + 1, :], REPS[v]), start=True, stop=False)
                nc.tensor.matmul(out=ps[:, m % per, :, :], lhsT=ecl[v][:, P * m:P * m + P],
                                 rhs=wide(c2[:, b:b + 1, :], REPS[v]), start=False, stop=True)

        def u_ve(v, split):
            per = CHUNKS if v == 0 else HALF
            r = small.tile([P, CHUNKS], F32, name="r", tag="r")
            u = small.tile([P, CHUNKS], F32, name="u", tag="u%d" % v)
            live[("u", v)] = u
            two = small.tile([P, CHUNKS, 2], BF16, name="u2_%d" % v, tag="u2_%d" % v)
            live[("u2", v)] = two

            def total(t):
                nc.vector.tensor_reduce(out=r[:, per * t:per * t + per], in_=live[("u_ps", v, t)][:, :, 0, :],
                                        axis=AX.X, op=ALU.add)

            def invert():
                nc.vector.reciprocal(out=u[:], in_=r[:])

            def hi_part():
                with nc.allow_low_precision(reason="the bf16 part of u"):
                    nc.vector.reciprocal(out=two[:, :, 0], in_=r[:])

            def lo_part():
                nc.vector.tensor_tensor(out=two[:, :, 1], in0=u[:], in1=two[:, :, 0], op=ALU.subtract)

            ops = [lambda t=t: total(t) for t in range(CHUNKS // per)]
            return ops + ([invert, hi_part, lo_part] if split else [invert])

        def c_block(v, b):
            if b == 0:
                live[("c_ps", v)] = chain_tile(v, [P, GROUPS, REPS[v], 2], "c_ps")
            ps = live[("c_ps", v)]
            u2 = live[("u2", v)]
            for m in range(GROUP * b, GROUP * b + GROUP):
                for hl in range(2):
                    nc.tensor.matmul(out=ps[:, b, :, :], lhsT=es[v][:, m, hl, :],
                                     rhs=wide(u2[:, m:m + 1, :], REPS[v]),
                                     start=(m % GROUP == 0 and hl == 0), stop=(m % GROUP == GROUP - 1 and hl == 1))

        def c_ve(v):
            return c_from(v, live[("c_ps", v)][:, :, 0, :], 2)

        def f_block(v, b):
            if b == 0:
                live[("f_ps", v)] = chain_tile(v, [P, CHUNKS, 1, 2], "f_ps")
            ps = live[("f_ps", v)]
            c2 = live[("c2", v)]
            for m in range(GROUP * b, GROUP * b + GROUP):
                nc.tensor.matmul(out=ps[:, m, :, :], lhsT=gh[v][:, P * m:P * m + P], rhs=c2[:, b:b + 1, :],
                                 start=True, stop=False)
                nc.tensor.matmul(out=ps[:, m, :, :], lhsT=gl[v][:, P * m:P * m + P], rhs=c2[:, b:b + 1, :],
                                 start=False, stop=True)

        def chain(v):
            items = []
            for sweep in range(3):
                items.extend([("pe", lambda b=b: u_block(v, b), lambda b=b: b < split_groups[v]) for b in range(GROUPS)])
                items.append(("ve", lambda closing=(sweep == 2): u_ve(v, not closing), lambda: True))
                if sweep < 2:
                    items.extend([("pe", lambda b=b: c_block(v, b), lambda b=b: b < turned_groups[v])
                                  for b in range(GROUPS)])
                    items.append(("ve", lambda: c_ve(v), lambda: True))
            return items

        todo = [chain(v) for v in range(VIEWS)]
        at = [0, 0]
        pending = []
        dripped = [0]
        in_rounds = [True]

        def drip():
            if dripped[0] < len(pending):
                pending[dripped[0]]()
                dripped[0] = dripped[0] + 1

        def small_ops(v, ops):
            if v == 0 and in_rounds[0]:
                pending.extend(ops)
                drip()
            else:
                for op in ops:
                    op()

        def advance(v, budget):
            n = 0
            while at[v] < len(todo[v]) and (v == 1 or dripped[0] == len(pending)):
                kind, piece, written = todo[v][at[v]]
                if kind == "ve" and n > 0:
                    return
                if kind == "pe" and n == budget:
                    return
                if not written():
                    return
                if kind == "ve":
                    small_ops(v, piece())
                else:
                    piece()
                at[v] = at[v] + 1
                n = n + 1
                if kind == "ve":
                    return

        def g_max_a(v):
            nc.vector.tensor_copy(out=mrep[v][:], in_=nb_c[v][:, 0:1].to_broadcast([P, P]))
            mt = chain_tile(v, [P, P], "mt")
            nc.tensor.transpose(mt[:], mrep[v][:], ident_f[:])
            live[("mt", v)] = mt

        def g_max_b(v):
            nc.vector.tensor_reduce(out=gmin[v][:], in_=live[("mt", v)][:], axis=AX.X, op=ALU.min)
            nc.vector.tensor_scalar(out=nb_t[v][:], in0=gmin[v][:], scalar1=INV_T / INV_EPS, scalar2=None, op0=ALU.mult)

        def p_tp(v, g):
            tp = ring.tile([P, GROUP, P], F32, name="tp", tag="b")
            for q in range(GROUP):
                m = GROUP * g + q
                nc.tensor.transpose(tp[:, q, :], zc[v][:, P * m:P * m + P], ident_f[:])
            live[("tp", v, g)] = tp

        def p_exp(v, g):
            for q in reversed(range(GROUP)):
                pj = small.tile([P, P], BF16, name="pj", tag="pj")
                nc.scalar.activation(out=pj[:], in_=live[("tp", v, g)][:, q, :], func=ACT.Exp, bias=nb_t[v][:, 0:1],
                                     scale=-INV_T / INV_EPS, accum_out=sump[v][:, GROUP * g + q:GROUP * g + q + 1])

        def g_mul(v, j):
            nc.vector.tensor_tensor(out=ec[v][:, unit(j)], in0=ec[v][:, unit(j)], in1=zc[1 - v][:, unit(j)],
                                    op=ALU.mult)

        def g_hi(v, j):
            nc.scalar.copy(out=gh[v][:, unit(j)], in_=ec[v][:, unit(j)])

        def g_lo(v, j):
            nc.vector.tensor_tensor(out=gl[v][:, unit(j)], in0=ec[v][:, unit(j)], in1=gh[v][:, unit(j)],
                                    op=ALU.subtract)

        units = [(v, j) for v in range(VIEWS) for j in range(UNITS)]

        g_items = []
        for k in range(NU + 2):
            if k < NU:
                g_items.append(("v", g_mul, k))
            if 0 <= k - 1 < NU:
                g_items.append(("s", g_hi, k - 1))
            if 0 <= k - 2 < NU:
                g_items.append(("v", g_lo, k - 2))

        def p_step(k):
            p_tp(k // GROUPS, k % GROUPS)
            p_exp(k // GROUPS, k % GROUPS)

        g_at = [0]
        g_split = [0]
        p_at = [0]

        def g_work(n, limit):
            while g_at[0] < len(g_items):
                eng, piece, k = g_items[g_at[0]]
                if k >= limit or (eng == "v" and n == 0):
                    return
                piece(*units[k])
                if piece == g_lo:
                    g_split[0] = k + 1
                g_at[0] = g_at[0] + 1
                if eng == "v":
                    n = n - 1

        def p_work(n, limit):
            for q in range(n):
                if p_at[0] < min(limit, NG):
                    p_step(p_at[0])
                    p_at[0] = p_at[0] + 1

        with ExitStack() as early:
            xin = early.enter_context(tc.tile_pool(name="xin", bufs=NX))
            stage = early.enter_context(tc.tile_pool(name="stage", bufs=2))
            hbp = early.enter_context(tc.tile_pool(name="hbp", bufs=2 * GROUP))

            x_views = x.rearrange("(p m v) d -> v p m d", m=CHUNKS, v=VIEWS)

            def ok(g):
                return 0 <= g < NG

            def load(g):
                if not ok(g):
                    return
                x_sb = xin.tile([P, GROUP * D], BF16, name="x_sb", tag="x_sb")
                j = g % GROUPS
                nc.sync.dma_start(out=x_sb[:].rearrange("p (m d) -> p m d", m=GROUP),
                                  in_=x_views[g // GROUPS][:, GROUP * j:GROUP * j + GROUP, :])
                live[("x", g)] = x_sb

            def words_tp(src, half):
                src32 = src[:].bitcast(F32)
                xt = ring.tile([P, 2, 2, P], F32, name="wt", tag="b")
                for cc in range(2):
                    for u in range(2):
                        lo = 256 * (2 * half + cc) + 128 * u
                        nc.tensor.transpose(xt[:, cc, u, :], src32[:, lo:lo + 128], ident_f[:])
                return xt

            def words_cp(xt, grouped, half, on_scalar):
                g32 = grouped[:].bitcast(F32).rearrange("p (c s u) -> p c s u", c=GROUP, u=2)
                dst = g32[:, 2 * half:2 * half + 2, :, :]
                srcv = xt[:].rearrange("p c u s -> p c s u")
                if on_scalar:
                    nc.scalar.copy(out=dst, in_=srcv)
                else:
                    nc.vector.tensor_copy(out=dst, in_=srcv)

            def k_to_partitions(src, grouped, half, on_scalar):
                words_cp(words_tp(src, half), grouped, half, on_scalar)

            def x_tp(g, half, on_scalar):
                if not ok(g):
                    return
                if half == 0:
                    live[("xg", g)] = stage.tile([P, GROUP * D], BF16, name="xg", tag="xg", align_bytes=64)
                k_to_partitions(live[("x", g)], live[("xg", g)], half, on_scalar)

            def x_q(g):
                if not ok(g):
                    return
                xq = stage.tile([P, W], U32, name="xq", tag="xq", align_bytes=64)
                xs = stage.tile([P, W], U8, name="xs", tag="xs", align_bytes=64)
                nc.vector.quantize_mx(out=xq[:].bitcast(FP8X4), scales=xs[:], in_=live[("xg", g)][:])
                drip()
                live[("xq", g)] = (xq, xs)

            def head_pe(g, c):
                if not ok(g):
                    return
                xq, xs = live[("xq", g)]
                h_ps = ring.tile([P, C], F32, name="h_ps", tag="b")
                nc.tensor.matmul_mx(out=h_ps[:], lhsT=xq[:, P * c:P * c + P].bitcast(FP8X4),
                                    lhsT_scale=xs[:, P * c:P * c + P], rhs=wq[:].bitcast(FP8X4),
                                    rhs_scale=ws[:], start=True, stop=True)
                live[("h_ps", g, c)] = h_ps

            def head_out(g, c):
                if not ok(g):
                    return
                if c == 0:
                    live[("ss", g)] = small.tile([P, GROUP], F32, name="ss", tag="ss")
                ss = live[("ss", g)]
                hb = hbp.tile([P, C], F32, name="hb", tag="hb")
                nc.vector.tensor_tensor(out=hb[:], in0=live[("h_ps", g, c)][:], in1=b_bc[:], op=ALU.add)
                drip()
                junk = stage.tile([P, C], BF16, name="junk", tag="junk")
                nc.scalar.activation(out=junk[:], in_=hb[:], func=ACT.Square, accum_out=ss[:, c:c + 1])
                live[("hb", g, c)] = hb

            def rnorm(g):
                if not ok(g):
                    return
                ssm = small.tile([P, GROUP], F32, name="ssm", tag="ssm")
                nc.vector.tensor_scalar_max(out=ssm[:], in0=live[("ss", g)][:], scalar1=1e-24)
                rn = small.tile([P, GROUP], F32, name="rn", tag="rn")
                nc.gpsimd.tensor_tensor(out=rn[:], in0=ssm[:], in1=neg_half[:], op=ALU.pow)
                live[("rn", g)] = rn
                live[("hn", g)] = stage.tile([P, GROUP * C], BF16, name="hn", tag="hn")

            def scale(g, c, eng):
                if not ok(g):
                    return
                dst = live[("hn", g)][:, C * c:C * c + C]
                hb = live[("hb", g, c)]
                rn = live[("rn", g)]
                if eng == "g":
                    nc.gpsimd.tensor_scalar(out=dst, in0=hb[:], scalar1=rn[:, c:c + 1], scalar2=0.0,
                                            op0=ALU.mult, op1=ALU.add)
                else:
                    nc.vector.tensor_scalar(out=dst, in0=hb[:], scalar1=rn[:, c:c + 1], scalar2=None, op0=ALU.mult)
                    drip()

            def h_tp(g, half):
                if not ok(g):
                    return
                live[("ht", g, half)] = words_tp(live[("hn", g)], half)

            def h_cp(g, half, on_scalar):
                if not ok(g):
                    return
                if half == 0:
                    live[("hg", g)] = stage.tile([P, GROUP * C], BF16, name="hg", tag="hg", align_bytes=64)
                words_cp(live[("ht", g, half)], live[("hg", g)], half, on_scalar)

            def h_q(g):
                if not ok(g):
                    return
                hq = stage.tile([P, W], U32, name="hq", tag="hq", align_bytes=64)
                hs = stage.tile([P, W], U8, name="hs", tag="hs", align_bytes=64)
                nc.vector.quantize_mx(out=hq[:].bitcast(FP8X4), scales=hs[:], in_=live[("hg", g)][:])
                drip()
                live[("hq", g)] = (hq, hs)

            def logits_pe(g):
                if not ok(g):
                    return
                hq, hs = live[("hq", g)]
                z_ps = ring.tile([P, W], F32, name="z_ps", tag="b")
                nc.tensor.matmul_mx(out=z_ps[:], lhsT=cq[:].bitcast(FP8X4), lhsT_scale=cs8[:],
                                    rhs=hq[:].bitcast(FP8X4), rhs_scale=hs[:], start=True, stop=True)
                live[("z_ps", g)] = z_ps

            def logits_out(g):
                if not ok(g):
                    return
                v = g // GROUPS
                j = g % GROUPS
                nc.vector.tensor_scalar(out=zc[v][:, bank(j)], in0=live[("z_ps", g)][:], scalar1=-INV_EPS, scalar2=None,
                                        op0=ALU.mult, op1=ALU.min, accum_out=nb_e[v][:, j:j + 1])
                drip()
                if j == GROUPS - 1:
                    factors_a(v)

            w_sb = stage.tile([P, GROUP * D], BF16, name="w_sb", tag="hn")
            w_rows = head_w.rearrange("(c p) k -> p c k", p=P)
            x0_sb = xin.tile([P, GROUP * D], BF16, name="x_sb", tag="x_sb")
            live[("x", 0)] = x0_sb
            for half in range(2):
                cols = slice(2 * D * half, 2 * D * half + 2 * D)
                nc.sync.dma_start(out=w_sb[:, cols].rearrange("p (c k) -> p c k", c=2),
                                  in_=w_rows[:, 2 * half:2 * half + 2, :])
                nc.sync.dma_start(out=x0_sb[:, cols].rearrange("p (m d) -> p m d", m=2),
                                  in_=x_views[0][:, 2 * half:2 * half + 2, :])
            for g in range(1, NX):
                load(g)
            b_bc = const.tile([P, C], BF16, name="b_bc")
            nc.scalar.dma_start(out=b_bc[:], in_=head_b.partition_broadcast(P))
            v_sb = const.tile([P, C], BF16, name="v_sb")
            nc.scalar.dma_start(out=v_sb[:], in_=cb_v)
            g_sb = const.tile([P, 1], BF16, name="g_sb")
            with nc.allow_non_contiguous_dma(reason="one gain for each code's partition"):
                nc.scalar.dma_start(out=g_sb[:], in_=cb_g.rearrange("(p o) -> p o", o=1))
            ident_f = const.tile([P, P], F32, name="ident_f")
            make_identity(nc, ident_f[:])
            ident_b = const.tile([P, P], BF16, name="ident_b")
            make_identity(nc, ident_b[:])
            neg_half = const.tile([P, GROUP], F32, name="neg_half")
            nc.vector.memset(neg_half[:], -0.5)

            wgr = stage.tile([P, GROUP * D], BF16, name="wgr", tag="hg", align_bytes=64)
            k_to_partitions(w_sb, wgr, 0, False)
            x_tp(0, 0, True)
            k_to_partitions(w_sb, wgr, 1, False)
            x_tp(0, 1, True)
            wq = const.tile([P, C], U32, name="wq", align_bytes=64)
            ws = const.tile([P, C], U8, name="ws", align_bytes=64)
            nc.vector.quantize_mx(out=wq[:].bitcast(FP8X4), scales=ws[:], in_=wgr[:])
            x_q(0)
            x_tp(1, 0, False)
            x_tp(1, 1, True)

            junk0 = stage.tile([P, C], BF16, name="junk0", tag="junk")
            vss = const.tile([P, 1], F32, name="vss")
            nc.scalar.activation(out=junk0[:], in_=v_sb[:], func=ACT.Square, accum_out=vss[:, 0:1])
            vrn = const.tile([P, 1], F32, name="vrn")
            nc.gpsimd.tensor_tensor(out=vrn[:], in0=vss[:], in1=neg_half[:, 0:1], op=ALU.pow)
            w_bf = const.tile([P, C], BF16, name="w_bf")
            wg = const.tile([P, C], BF16, name="wg", align_bytes=64)

            def codebook_a():
                wsc = const.tile([P, 1], F32, name="wsc")
                nc.vector.tensor_tensor(out=wsc[:], in0=vrn[:], in1=g_sb[:], op=ALU.mult)
                nc.vector.tensor_scalar(out=w_bf[:], in0=v_sb[:], scalar1=wsc[:, 0:1], scalar2=None, op0=ALU.mult)
                wt = aux.tile([P, 2, P], F32, name="cbt", tag="aux")
                for u in range(2):
                    nc.tensor.transpose(wt[:, u, :], w_bf[:].bitcast(F32)[:, 128 * u:128 * u + 128], ident_f[:])
                live["wt"] = wt

            def codebook_b():
                nc.vector.tensor_copy(out=wg[:].bitcast(F32).rearrange("p (s u) -> p s u", u=2),
                                      in_=live["wt"][:].rearrange("p u s -> p s u"))

            def codebook_c():
                nc.vector.quantize_mx(out=cq[:].bitcast(FP8X4), scales=cs8[:], in_=wg[:])

            cq = const.tile([P, K], U32, name="cq", align_bytes=64)
            cs8 = const.tile([P, K], U8, name="cs8", align_bytes=64)

            def unit_at(i, rounds_later):
                n, odd = divmod(i - 4 - rounds_later, 2)
                return n if (odd == 0 and 0 <= n < NU - 1) else None

            def stop(i, where):
                if where == "a" and 0 <= i - 3 < NG - 1:
                    e_exp((i - 3) // GROUPS, (i - 3) % GROUPS)
                    if (i - 3) % GROUPS == GROUPS - 1:
                        factors_b((i - 3) // GROUPS)
                for what, rounds_later, place in WHEN:
                    n = unit_at(i, rounds_later)
                    if n is None or place != where:
                        continue
                    v, j = units[n]
                    if what == "hi":
                        e_hi(v, j)
                        if j == UNITS - 1:
                            small_ops(v, c_from(v, csum[v][:], 1))
                            g_max_a(v)
                    if what == "lo":
                        e_lo(v, j)
                    if what == "tp":
                        e_tp(v, 2 * j)
                        e_tp(v, 2 * j + 1)
                    if what == "cp":
                        e_cp(v, 2 * j)
                        e_cp(v, 2 * j + 1)
                if i == 2 * UNITS + 3 and where == "a":
                    g_max_b(0)
                if i > 2 * UNITS + 2:
                    advance(0, BUDGET[where])
                if i >= P_FROM:
                    g_work(G_SIDE[where], (i - G_FROM) // 2 + 1)
                    if i < NG + 1 or where != "d":
                        p_work(P_SIDE[where], GROUPS)

            for c in range(GROUP):
                head_pe(0, c)
            for i in range(NG + 2):
                if i == 2:
                    codebook_c()
                logits_out(i - 3)
                h_cp(i - 2, 0, True)
                h_cp(i - 2, 1, True)
                stop(i, "a")
                for c in range(ON_VECTOR, GROUP):
                    scale(i - 1, c, "g")
                for c in range(GROUP):
                    head_out(i, c)
                load(i + NX)
                stop(i, "b")
                x_tp(i + 2, 0, True)
                x_tp(i + 2, 1, True)
                stop(i, "c")
                for c in range(ON_VECTOR):
                    scale(i - 1, c, "v")
                h_tp(i - 1, 0)
                h_tp(i - 1, 1)
                h_q(i - 2)
                logits_pe(i - 2)
                x_q(i + 1)
                for c in range(GROUP):
                    head_pe(i + 1, c)
                stop(i, "d")
                rnorm(i)
                if i == 0:
                    codebook_a()
                if i == 1:
                    codebook_b()
            logits_out(NG - 1)
            in_rounds[0] = False

        late = ctx.enter_context(tc.tile_pool(name="late", bufs=1))
        gh.append(late.tile([P, CHUNKS * P], BF16, name="gh1"))
        gl.append(late.tile([P, CHUNKS * P], BF16, name="gl1"))
        f_at = [0]

        def fill(n):
            if at[0] < len(todo[0]):
                advance(0, n)
                return
            for q in range(n):
                if f_at[0] < min(GROUPS, 2 * g_split[0]):
                    f_block(0, f_at[0])
                    f_at[0] = f_at[0] + 1

        def loss_logs():
            for v in range(VIEWS):
                nc.scalar.activation(out=lnp[v][:], in_=sump[v][:], func=ACT.Ln)
            lsum = const.tile([P, CHUNKS], F32, name="lsum")
            nc.vector.tensor_tensor(out=lsum[:], in0=lnp[0][:], in1=lnp[1][:], op=ALU.add)
            msum = const.tile([P, 1], F32, name="msum")
            nc.vector.tensor_tensor(out=msum[:], in0=nb_t[0][:], in1=nb_t[1][:], op=ALU.add)
            msc = const.tile([P, 1], F32, name="msc")
            nc.vector.tensor_scalar(out=msc[:], in0=msum[:], scalar1=-0.5, scalar2=None, op0=ALU.mult)
            part = const.tile([P, CHUNKS], F32, name="part")
            nc.vector.tensor_scalar(out=part[:], in0=lsum[:], scalar1=0.5, scalar2=msc[:, 0:1],
                                    op0=ALU.mult, op1=ALU.add)
            live["res"] = part

        def loss_view(v):
            fsum = small.tile([P, CHUNKS], F32, name="fsum", tag="r")
            nc.vector.tensor_reduce(out=fsum[:], in_=live[("f_ps", v)][:, :, 0, :], axis=AX.X, op=ALU.add)
            nc.vector.tensor_tensor(out=tq[v][:], in0=fsum[:], in1=live[("u", v)][:], op=ALU.mult)
            res = const.tile([P, CHUNKS], F32, name="res%d" % v)
            nc.vector.scalar_tensor_tensor(out=res[:], in0=tq[v][:], scalar=0.5 * INV_T / INV_EPS, in1=live["res"][:],
                                           op0=ALU.mult, op1=ALU.add)
            live["res"] = res

        def loss_tail():
            loss_view(1)

        last = UNITS - 1
        e_exp(1, GROUPS - 1)
        factors_b(1)
        small_ops(1, c_from(1, csum[1][:], 1))
        e_hi(1, last)
        e_lo(1, last)
        e_tp(1, 2 * last - 2)
        e_tp(1, 2 * last - 1)
        e_cp(1, 2 * last - 2)
        e_cp(1, 2 * last - 1)
        while dripped[0] < len(pending):
            drip()
        fill(FILL0)
        p_work(GROUPS, GROUPS)
        for sweep in range(5):
            advance(1, GROUPS)
            if sweep == 0:
                e_tp(1, 2 * last)
                e_tp(1, 2 * last + 1)
                e_cp(1, 2 * last)
                e_cp(1, 2 * last + 1)
                g_max_a(1)
            else:
                fill(FILL)
                p_work(P_GAP, NG)
            advance(1, 1)
            if sweep == 0:
                g_max_b(1)
            g_work(G_TAIL[sweep], NU)
        p_work(NG, NG)
        loss_logs()
        g_work(len(g_items), NU)
        for q in range(6):
            fill(GROUPS)
        for b in range(GROUPS):
            f_block(1, b)
        loss_view(0)
        assert at[0] == len(todo[0]) and at[1] == len(todo[1]) and f_at[0] == GROUPS
        assert g_at[0] == len(g_items) and p_at[0] == NG

        loss_tail()
        nc.sync.dma_start(out=out.rearrange("(p m) -> p m", m=CHUNKS), in_=live["res"][:])
